import numpy as np
import ml_dtypes


def mxq(x, axis, fmt="e4m3"):
    dtype, down = {"e4m3": (ml_dtypes.float8_e4m3fn, 7), "e5m2": (ml_dtypes.float8_e5m2, 14)}[fmt]
    v = np.moveaxis(np.asarray(x, np.float32).astype(ml_dtypes.bfloat16).astype(np.float64), axis, -1)
    blocks = v.reshape(v.shape[:-1] + (-1, 32))
    amax = np.abs(blocks).max(-1, keepdims=True)
    byte = np.maximum(np.where(amax > 0, np.frexp(amax)[1] - 1 + 127, 0) - down, 1)
    scale = np.exp2(byte - 127.0)
    codes = (blocks / scale).astype(np.float32).astype(dtype).astype(np.float64)
    return np.moveaxis((codes * scale).reshape(v.shape), -1, axis)


WIDE = False


def mx_kscale(k):
    if not WIDE:
        return np.ones(k)
    levels = np.array([10, -10, 5, -5, 0])
    if k % 512:
        return np.exp2(np.random.permutation(np.resize(levels, k // 32))).repeat(32)
    a = np.empty((k // 512, 16))
    for p in range(k // 512):
        a[p, :8] = np.random.permutation(np.resize(levels, 8))
        for g in range(8):
            far = levels[np.abs(levels - a[p, g]) >= 10]
            a[p, g + 8] = far[np.random.randint(len(far))]
    return np.exp2(a.ravel()).repeat(32)


BF16 = ml_dtypes.bfloat16


def bf(x):
    return np.asarray(x, np.float32).astype(BF16)


def f64(x):
    return np.asarray(x).astype(np.float64)


B, S, DI, DO = 4, 1024, 512, 1024
OUTLIER_SCALE = 1.0
STD_K = 1.6


def binarize_except_outliers(weight):
    w = weight
    mean = np.mean(w)
    std = np.std(w, ddof=1)
    lower = mean - STD_K * std
    upper = mean + STD_K * std
    outlier_mask = (w < lower) | (w > upper)
    keep = ~outlier_mask
    binary_scale = np.sum(np.abs(w) * keep) / np.sum(keep)
    sign_ste = w + (np.sign(w) - w)
    binary_weight = sign_ste * binary_scale
    scaled_weight = w * OUTLIER_SCALE
    return np.where(outlier_mask, scaled_weight, binary_weight)


def setup_inputs():
    s = mx_kscale(DI)
    big = (s == s.min()) & (s < 1.0)
    big = big & (np.cumsum(big) <= DI // 4)
    u = np.where(big, s * s, 1.0)
    n = np.random.standard_normal((DO, DI))
    n = np.where(big, np.sign(n) * (1.0 + 0.1 * np.abs(n)), n)
    return {"x": bf(np.random.standard_normal((B, S, DI)) * u),
            "weight": bf(n / np.sqrt(DI) / u),
            "bias": bf(np.random.standard_normal(DO) * 0.3)}


def reference(x, weight, bias):
    w_sim = binarize_except_outliers(f64(weight))
    return (mxq(f64(x), 2, "e4m3") @ mxq(w_sim, 1, "e4m3").T) + f64(bias)

@@ -1,0 +1,521 @@
+from contextlib import ExitStack
+import math
+
+import concourse.bass as bass
+import concourse.masks as masks
+import concourse.mybir as mybir
+import concourse.tile as tile
+
+F32 = mybir.dt.float32
+BF16 = mybir.dt.bfloat16
+U32 = mybir.dt.uint32
+U8 = mybir.dt.uint8
+FP8X4 = mybir.dt.float8_e4m3fn_x4
+ALU = mybir.AluOpType
+ACT = mybir.ActivationFunctionType
+AX = mybir.AxisListType
+
+P = 128
+TOK = 4096
+K = 512
+NOUT = 1024
+NW = NOUT * K
+FLOPS = 2 * TOK * NOUT * K
+GROUPS = 8
+SC = math.sqrt((NW - 1) / (1.6 * 1.6))
+TINY = 2.0 ** -126
+HUGE = 2.0 ** 126
+
+
+def tile_binaryxnorexceptoutlierslinear_t_kernel(tc, x, weight, bias, out):
+    nc = tc.nc
+    xf = x.flatten_outer_dims()
+    of = out.flatten_outer_dims()
+    with ExitStack() as ctx:
+        ctx.enter_context(tc.manual_schedule())
+        keep = ctx.enter_context(tc.tile_pool(name="keep", bufs=1))
+        xgpool = ctx.enter_context(tc.tile_pool(name="xgp", bufs=2))
+        opool = ctx.enter_context(tc.tile_pool(name="op", bufs=3))
+        psum = ctx.enter_context(tc.psum_pool(name="psum", bufs=1))
+
+        ones_bf = keep.tile([P, P], BF16, name="ones_bf")
+        tinycol = keep.tile([P, 2], BF16, name="tinycol")
+        ident = keep.tile([P, P], F32, name="ident")
+        w_sb = keep.tile([P, 8, K], BF16, name="w_sb")
+        x_sb = keep.tile([P, GROUPS, 4, K], BF16, name="x_sb")
+        bias_bc = keep.tile([P, NOUT], BF16, name="bias_bc")
+        bias_f = keep.tile([P, NOUT], F32, name="bias_f")
+        x_codes = keep.tile([P, GROUPS, 512], U32, name="x_codes", align_bytes=64)
+        x_scales = keep.tile([P, GROUPS, 512], U8, name="x_scales", align_bytes=64)
+        w_codes = keep.tile([P, NOUT], U32, name="w_codes", align_bytes=64)
+        w_scales = keep.tile([P, NOUT], U8, name="w_scales", align_bytes=64)
+        wT = keep.tile([P, NOUT, 4], BF16, name="wT")
+        wT32 = wT[:].bitcast(F32)
+        wTf = wT[:].rearrange("p n v -> p (n v)")
+        ws = keep.tile([P, 4 * NOUT], BF16, name="ws")
+        q = keep.tile([P, 4 * NOUT], F32, name="q")
+        kk = keep.tile([P, 4 * NOUT], BF16, name="kk")
+        bm = keep.tile([P, 4 * NOUT], BF16, name="bm")
+        oo = keep.tile([P, 4 * NOUT], BF16, name="oo")
+        aa = keep.tile([P, 4 * NOUT], BF16, name="aa")
+        cb = keep.tile([P, 4 * NOUT], BF16, name="cb")
+        wsim = keep.tile([P, 4 * NOUT], BF16, name="wsim", align_bytes=64)
+        junk_s = keep.tile([P, 1024], BF16, name="junk_s")
+        junk_v = keep.tile([P, 1024], F32, name="junk_v")
+        st_s = keep.tile([P, 4], F32, name="st_s")
+        st2 = keep.tile([P, 2], F32, name="st2")
+        hl = keep.tile([P, 16], BF16, name="hl")
+        hl2 = keep.tile([P, 4], BF16, name="hl2")
+        nbt = keep.tile([P, 1], F32, name="nbt")
+        sm = keep.tile([P, 8], F32, name="sm")
+        w_flat = w_sb[:].rearrange("p j k -> p (j k)")
+        tl = {}
+        nc.vector.memset(ones_bf[:], 1.0)
+        nc.vector.memset(tinycol[:], TINY)
+        masks.make_identity(nc, ident[:])
+        ident_bf = keep.tile([P, P], BF16, name="ident_bf")
+        c_ident = keep.tile([P, P], BF16, name="c_ident")
+        masks.make_identity(nc, ident_bf[:])
+        nc.sync.dma_start(out=w_sb[:, 0 : 2, :], in_=weight[0 : 256, :].rearrange("(j p) k -> p j k", p=P))
+        nc.sync.dma_start(out=w_sb[:, 2 : 4, :], in_=weight[256 : 512, :].rearrange("(j p) k -> p j k", p=P))
+        nc.sync.dma_start(out=w_sb[:, 4 : 6, :], in_=weight[512 : 768, :].rearrange("(j p) k -> p j k", p=P))
+        nc.sync.dma_start(out=w_sb[:, 6 : 8, :], in_=weight[768 : 1024, :].rearrange("(j p) k -> p j k", p=P))
+        nc.sync.dma_start(out=x_sb[:, 0, :, :], in_=xf[0 : 512, :].rearrange("(p t) k -> p t k", t=4))
+        nc.sync.dma_start(out=x_sb[:, 1, :, :], in_=xf[512 : 1024, :].rearrange("(p t) k -> p t k", t=4))
+        nc.sync.dma_start(out=bias_bc[:], in_=bias.partition_broadcast(P))
+        nc.sync.dma_start(out=x_sb[:, 2, :, :], in_=xf[1024 : 1536, :].rearrange("(p t) k -> p t k", t=4))
+        nc.sync.dma_start(out=x_sb[:, 3, :, :], in_=xf[1536 : 2048, :].rearrange("(p t) k -> p t k", t=4))
+        nc.sync.dma_start(out=x_sb[:, 4, :, :], in_=xf[2048 : 2560, :].rearrange("(p t) k -> p t k", t=4))
+        nc.sync.dma_start(out=x_sb[:, 5, :, :], in_=xf[2560 : 3072, :].rearrange("(p t) k -> p t k", t=4))
+        nc.sync.dma_start(out=x_sb[:, 6, :, :], in_=xf[3072 : 3584, :].rearrange("(p t) k -> p t k", t=4))
+        nc.sync.dma_start(out=x_sb[:, 7, :, :], in_=xf[3584 : 4096, :].rearrange("(p t) k -> p t k", t=4))
+        nc.gpsimd.tensor_scalar(out=bias_f[:], in0=bias_bc[:], scalar1=1.0, scalar2=0.0, op0=ALU.mult, op1=ALU.add)
+        tl["pw0"] = psum.tile([P, 2, 2, P], F32, name="pw0", tag="b0")
+        for jj in range(2):
+            for u in range(2):
+                nc.tensor.transpose(out=tl["pw0"][:, jj, u, :], in_=w_sb[:, 0 + jj, :].bitcast(F32)[:, u : 2 * P : 2], identity=ident[:])
+        tl["sw"] = psum.tile([P, 256], F32, name="ps_sw", tag="b4")
+        for j in (0, 1):
+            for b in range(2):
+                nc.tensor.matmul(out=tl["sw"][:], lhsT=ones_bf[:], rhs=w_sb[:, j, 256 * b : 256 * b + 256], start=(j == 0 and b == 0), stop=(j == 7 and b == 1))
+        nc.scalar.activation(out=junk_s[:, 0:1024], in_=w_flat[:, 0:1024], func=ACT.Square, accum_out=st_s[:, 0:1])
+        nc.vector.tensor_copy(out=wT32[:, 0 : 256, :].rearrange("p (j r) u -> p j r u", j=2), in_=tl["pw0"][:].rearrange("p j u r -> p j r u"))
+        tl["pw1"] = psum.tile([P, 2, 2, P], F32, name="pw1", tag="b1")
+        for jj in range(2):
+            for u in range(2):
+                nc.tensor.transpose(out=tl["pw1"][:, jj, u, :], in_=w_sb[:, 2 + jj, :].bitcast(F32)[:, u : 2 * P : 2], identity=ident[:])
+        for j in (2, 3):
+            for b in range(2):
+                nc.tensor.matmul(out=tl["sw"][:], lhsT=ones_bf[:], rhs=w_sb[:, j, 256 * b : 256 * b + 256], start=(j == 0 and b == 0), stop=(j == 7 and b == 1))
+        nc.scalar.activation(out=junk_s[:, 0:1024], in_=w_flat[:, 1024:2048], func=ACT.Square, accum_out=st_s[:, 1:2])
+        nc.vector.tensor_copy(out=wT32[:, 256 : 512, :].rearrange("p (j r) u -> p j r u", j=2), in_=tl["pw1"][:].rearrange("p j u r -> p j r u"))
+        tl["pw2"] = psum.tile([P, 2, 2, P], F32, name="pw2", tag="b2")
+        for jj in range(2):
+            for u in range(2):
+                nc.tensor.transpose(out=tl["pw2"][:, jj, u, :], in_=w_sb[:, 4 + jj, :].bitcast(F32)[:, u : 2 * P : 2], identity=ident[:])
+        for j in (4, 5):
+            for b in range(2):
+                nc.tensor.matmul(out=tl["sw"][:], lhsT=ones_bf[:], rhs=w_sb[:, j, 256 * b : 256 * b + 256], start=(j == 0 and b == 0), stop=(j == 7 and b == 1))
+        nc.scalar.activation(out=junk_s[:, 0:1024], in_=w_flat[:, 2048:3072], func=ACT.Square, accum_out=st_s[:, 2:3])
+        nc.vector.tensor_scalar(out=ws[:, 0:2048], in0=wTf[:, 0:2048], scalar1=-TINY, scalar2=TINY, op0=ALU.max, op1=ALU.min)
+        nc.vector.tensor_copy(out=wT32[:, 512 : 768, :].rearrange("p (j r) u -> p j r u", j=2), in_=tl["pw2"][:].rearrange("p j u r -> p j r u"))
+        tl["pw3"] = psum.tile([P, 2, 2, P], F32, name="pw3", tag="b3")
+        for jj in range(2):
+            for u in range(2):
+                nc.tensor.transpose(out=tl["pw3"][:, jj, u, :], in_=w_sb[:, 6 + jj, :].bitcast(F32)[:, u : 2 * P : 2], identity=ident[:])
+        for j in (6, 7):
+            for b in range(2):
+                nc.tensor.matmul(out=tl["sw"][:], lhsT=ones_bf[:], rhs=w_sb[:, j, 256 * b : 256 * b + 256], start=(j == 0 and b == 0), stop=(j == 7 and b == 1))
+        nc.scalar.activation(out=junk_s[:, 0:1024], in_=w_flat[:, 3072:4096], func=ACT.Square, accum_out=st_s[:, 3:4])
+        nc.vector.tensor_copy(out=hl[:, 0:4], in_=st_s[:, 0:4])
+        nc.vector.tensor_tensor(out=hl[:, 4:8], in0=st_s[:, 0:4], in1=hl[:, 0:4], op=ALU.subtract)
+        nc.vector.tensor_copy(out=wT32[:, 768 : 1024, :].rearrange("p (j r) u -> p j r u", j=2), in_=tl["pw3"][:].rearrange("p j u r -> p j r u"))
+        nc.scalar.activation(out=junk_s[:, 0:256], in_=tl["sw"][:], func=ACT.Identity, scale=-SC / NW, accum_out=nbt[:, 0:1])
+        tl["l2a"] = psum.tile([P, 8], F32, name="ps_l2a", tag="b5")
+        nc.tensor.matmul(out=tl["l2a"][:, 0:4], lhsT=ones_bf[:], rhs=hl[:, 0:4], start=True, stop=False)
+        nc.tensor.matmul(out=tl["l2a"][:, 0:4], lhsT=ones_bf[:], rhs=hl[:, 4:8], start=False, stop=True)
+        for b in range(2):
+            tl["pt0_%d" % b] = psum.tile([P, 2, 2, P], F32, name="pt0_%d" % b, tag="b%d" % (0 + b))
+            for tt in range(2):
+                for u in range(2):
+                    nc.tensor.transpose(out=tl["pt0_%d" % b][:, tt, u, :], in_=x_sb[:, 0, 2 * b + tt, :].bitcast(F32)[:, u : 2 * P : 2], identity=ident[:])
+        nc.vector.tensor_scalar(out=ws[:, 2048:4096], in0=wTf[:, 2048:4096], scalar1=-TINY, scalar2=TINY, op0=ALU.max, op1=ALU.min)
+        nc.vector.tensor_scalar(out=sm[:, 2:3], in0=nbt[:, 0:1], scalar1=nbt[:, 0:1], scalar2=-NW / (SC * SC), op0=ALU.mult, op1=ALU.mult)
+        nc.vector.reduce_sum(out=sm[:, 3:4], in_=tl["l2a"][:, 0:4], axis=AX.X)
+        nc.vector.tensor_scalar(out=sm[:, 4:5], in0=sm[:, 3:4], scalar1=sm[:, 2:3], scalar2=None, op0=ALU.add)
+        nc.scalar.activation(out=q[:, 0:1024], in_=wTf[:, 0:1024], func=ACT.Square, bias=nbt[:, 0:1], scale=SC)
+        nc.vector.tensor_scalar(out=kk[:, 0:1024], in0=q[:, 0:1024], scalar1=sm[:, 4:5], scalar2=HUGE, op0=ALU.is_le, op1=ALU.mult)
+        nc.scalar.activation(out=q[:, 1024:2048], in_=wTf[:, 1024:2048], func=ACT.Square, bias=nbt[:, 0:1], scale=SC)
+        for b in range(2):
+            tl["pt1_%d" % b] = psum.tile([P, 2, 2, P], F32, name="pt1_%d" % b, tag="b%d" % (4 + b))
+            for tt in range(2):
+                for u in range(2):
+                    nc.tensor.transpose(out=tl["pt1_%d" % b][:, tt, u, :], in_=x_sb[:, 1, 2 * b + tt, :].bitcast(F32)[:, u : 2 * P : 2], identity=ident[:])
+        nc.vector.tensor_scalar(out=kk[:, 1024:2048], in0=q[:, 1024:2048], scalar1=sm[:, 4:5], scalar2=HUGE, op0=ALU.is_le, op1=ALU.mult)
+        nc.vector.tensor_tensor(out=bm[:, 0:1024], in0=ws[:, 0:1024], in1=kk[:, 0:1024], op=ALU.mult)
+        tl["g"] = psum.tile([P, P], F32, name="ps_g", tag="b6")
+        tl["ck"] = psum.tile([P, 8], F32, name="ps_ck", tag="b7")
+        for b in range(0, 8):
+            nc.tensor.matmul(out=tl["g"][:], lhsT=wTf[:, P * b : P * b + P], rhs=bm[:, P * b : P * b + P], start=(b == 0), stop=(b == 31))
+            nc.tensor.matmul(out=tl["ck"][:, 0:1], lhsT=kk[:, P * b : P * b + P], rhs=tinycol[:, 0:1], start=(b == 0), stop=(b == 31))
+        nc.scalar.activation(out=q[:, 2048:3072], in_=wTf[:, 2048:3072], func=ACT.Square, bias=nbt[:, 0:1], scale=SC)
+        nc.vector.tensor_scalar(out=kk[:, 2048:3072], in0=q[:, 2048:3072], scalar1=sm[:, 4:5], scalar2=HUGE, op0=ALU.is_le, op1=ALU.mult)
+        nc.vector.tensor_tensor(out=bm[:, 1024:2048], in0=ws[:, 1024:2048], in1=kk[:, 1024:2048], op=ALU.mult)
+        for b in range(8, 16):
+            nc.tensor.matmul(out=tl["g"][:], lhsT=wTf[:, P * b : P * b + P], rhs=bm[:, P * b : P * b + P], start=(b == 0), stop=(b == 31))
+            nc.tensor.matmul(out=tl["ck"][:, 0:1], lhsT=kk[:, P * b : P * b + P], rhs=tinycol[:, 0:1], start=(b == 0), stop=(b == 31))
+        nc.scalar.activation(out=q[:, 3072:3584], in_=wTf[:, 3072:3584], func=ACT.Square, bias=nbt[:, 0:1], scale=SC)
+        nc.vector.tensor_scalar(out=kk[:, 3072:3584], in0=q[:, 3072:3584], scalar1=sm[:, 4:5], scalar2=HUGE, op0=ALU.is_le, op1=ALU.mult)
+        nc.vector.tensor_tensor(out=bm[:, 2048:3072], in0=ws[:, 2048:3072], in1=kk[:, 2048:3072], op=ALU.mult)
+        for b in range(16, 24):
+            nc.tensor.matmul(out=tl["g"][:], lhsT=wTf[:, P * b : P * b + P], rhs=bm[:, P * b : P * b + P], start=(b == 0), stop=(b == 31))
+            nc.tensor.matmul(out=tl["ck"][:, 0:1], lhsT=kk[:, P * b : P * b + P], rhs=tinycol[:, 0:1], start=(b == 0), stop=(b == 31))
+        nc.scalar.activation(out=q[:, 3584:4096], in_=wTf[:, 3584:4096], func=ACT.Square, bias=nbt[:, 0:1], scale=SC)
+        nc.vector.tensor_scalar(out=kk[:, 3584:4096], in0=q[:, 3584:4096], scalar1=sm[:, 4:5], scalar2=HUGE, op0=ALU.is_le, op1=ALU.mult)
+        nc.vector.tensor_tensor(out=bm[:, 3072:3584], in0=ws[:, 3072:3584], in1=kk[:, 3072:3584], op=ALU.mult)
+        for b in range(24, 28):
+            nc.tensor.matmul(out=tl["g"][:], lhsT=wTf[:, P * b : P * b + P], rhs=bm[:, P * b : P * b + P], start=(b == 0), stop=(b == 31))
+            nc.tensor.matmul(out=tl["ck"][:, 0:1], lhsT=kk[:, P * b : P * b + P], rhs=tinycol[:, 0:1], start=(b == 0), stop=(b == 31))
+        nc.vector.tensor_tensor(out=bm[:, 3584:4096], in0=ws[:, 3584:4096], in1=kk[:, 3584:4096], op=ALU.mult)
+        for b in range(28, 32):
+            nc.tensor.matmul(out=tl["g"][:], lhsT=wTf[:, P * b : P * b + P], rhs=bm[:, P * b : P * b + P], start=(b == 0), stop=(b == 31))
+            nc.tensor.matmul(out=tl["ck"][:, 0:1], lhsT=kk[:, P * b : P * b + P], rhs=tinycol[:, 0:1], start=(b == 0), stop=(b == 31))
+        tl["xg0"] = xgpool.tile([P, 4, P, 4], BF16, name="xg", align_bytes=64)
+        for b in range(2):
+            nc.scalar.copy(out=tl["xg0"][:].bitcast(F32)[:, 2 * b : 2 * b + 2, :, :], in_=tl["pt0_%d" % b][:].rearrange("p t u r -> p t r u"))
+        nc.scalar.activation(out=oo[:, 2048:3072], in_=kk[:, 2048:3072], func=ACT.Identity, scale=-TINY, bias=1.0)
+        nc.scalar.activation(out=oo[:, 3072:4096], in_=kk[:, 3072:4096], func=ACT.Identity, scale=-TINY, bias=1.0)
+        nc.scalar.activation(out=oo[:, 0:1024], in_=kk[:, 0:1024], func=ACT.Identity, scale=-TINY, bias=1.0)
+        nc.scalar.activation(out=oo[:, 1024:2048], in_=kk[:, 1024:2048], func=ACT.Identity, scale=-TINY, bias=1.0)
+        tl["xg1"] = xgpool.tile([P, 4, P, 4], BF16, name="xg", align_bytes=64)
+        for b in range(2):
+            nc.scalar.copy(out=tl["xg1"][:].bitcast(F32)[:, 2 * b : 2 * b + 2, :, :], in_=tl["pt1_%d" % b][:].rearrange("p t u r -> p t r u"))
+        nc.vector.tensor_tensor(out=aa[:, 2048:3072], in0=wTf[:, 2048:3072], in1=oo[:, 2048:3072], op=ALU.mult)
+        tl["wacc0"] = psum.tile([P, 512], F32, name="wacc0", tag="b2")
+        nc.tensor.matmul(out=tl["wacc0"][:], lhsT=ident_bf[:], rhs=aa[:, 2048:2560], start=True, stop=False)
+        tl["wacc1"] = psum.tile([P, 512], F32, name="wacc1", tag="b3")
+        nc.tensor.matmul(out=tl["wacc1"][:], lhsT=ident_bf[:], rhs=aa[:, 2560:3072], start=True, stop=False)
+        nc.vector.quantize_mx(out=x_codes[:, 0, :].bitcast(FP8X4), scales=x_scales[:, 0, :], in_=tl["xg0"][:].rearrange("p t r v -> p (t r v)"))
+        nc.vector.tensor_tensor(out=aa[:, 3072:4096], in0=wTf[:, 3072:4096], in1=oo[:, 3072:4096], op=ALU.mult)
+        tl["wacc2"] = psum.tile([P, 512], F32, name="wacc2", tag="b0")
+        nc.tensor.matmul(out=tl["wacc2"][:], lhsT=ident_bf[:], rhs=aa[:, 3072:3584], start=True, stop=False)
+        tl["wacc3"] = psum.tile([P, 512], F32, name="wacc3", tag="b1")
+        nc.tensor.matmul(out=tl["wacc3"][:], lhsT=ident_bf[:], rhs=aa[:, 3584:4096], start=True, stop=False)
+        nc.vector.tensor_copy(out=st2[:, 1:2], in_=tl["ck"][:, 0:1])
+        nc.vector.scalar_tensor_tensor(out=junk_v[:, 0:P], in0=tl["g"][:], scalar=1.0, in1=ident[:], op0=ALU.mult, op1=ALU.mult, accum_out=st2[:, 0:1])
+        nc.vector.tensor_copy(out=hl2[:, 0:2], in_=st2[:])
+        nc.vector.tensor_tensor(out=hl2[:, 2:4], in0=st2[:], in1=hl2[:, 0:2], op=ALU.subtract)
+        tl["l2b"] = psum.tile([P, 8], F32, name="ps_l2b", tag="b7")
+        nc.tensor.matmul(out=tl["l2b"][:, 0:2], lhsT=ones_bf[:], rhs=hl2[:, 0:2], start=True, stop=False)
+        nc.tensor.matmul(out=tl["l2b"][:, 0:2], lhsT=ones_bf[:], rhs=hl2[:, 2:4], start=False, stop=True)
+        nc.vector.tensor_tensor(out=aa[:, 0:1024], in0=wTf[:, 0:1024], in1=oo[:, 0:1024], op=ALU.mult)
+        nc.vector.reciprocal(out=sm[:, 5:6], in_=tl["l2b"][:, 1:2])
+        nc.vector.tensor_scalar(out=sm[:, 6:7], in0=tl["l2b"][:, 0:1], scalar1=sm[:, 5:6], scalar2=None, op0=ALU.mult)
+        nc.vector.tensor_scalar(out=c_ident[:], in0=ident_bf[:], scalar1=sm[:, 6:7], scalar2=None, op0=ALU.mult)
+        nc.tensor.matmul(out=tl["wacc0"][:], lhsT=c_ident[:], rhs=bm[:, 2048:2560], start=False, stop=True)
+        nc.tensor.matmul(out=tl["wacc1"][:], lhsT=c_ident[:], rhs=bm[:, 2560:3072], start=False, stop=True)
+        nc.tensor.matmul(out=tl["wacc2"][:], lhsT=c_ident[:], rhs=bm[:, 3072:3584], start=False, stop=True)
+        nc.tensor.matmul(out=tl["wacc3"][:], lhsT=c_ident[:], rhs=bm[:, 3584:4096], start=False, stop=True)
+        nc.scalar.copy(out=wsim[:, 2048:2560], in_=tl["wacc0"][:])
+        nc.scalar.copy(out=wsim[:, 2560:3072], in_=tl["wacc1"][:])
+        nc.scalar.copy(out=wsim[:, 3072:3584], in_=tl["wacc2"][:])
+        nc.vector.tensor_tensor(out=aa[:, 1024:2048], in0=wTf[:, 1024:2048], in1=oo[:, 1024:2048], op=ALU.mult)
+        nc.vector.tensor_scalar(out=cb[:, 0:2048], in0=bm[:, 0:2048], scalar1=sm[:, 6:7], scalar2=None, op0=ALU.mult)
+        nc.vector.tensor_tensor(out=wsim[:, 0:2048], in0=cb[:, 0:2048], in1=aa[:, 0:2048], op=ALU.add)
+        nc.vector.quantize_mx(out=w_codes[:, 0:512].bitcast(FP8X4), scales=w_scales[:, 0:512], in_=wsim[:, 0:2048])
+        nc.scalar.copy(out=wsim[:, 3584:4096], in_=tl["wacc3"][:])
+        nc.vector.quantize_mx(out=w_codes[:, 512:1024].bitcast(FP8X4), scales=w_scales[:, 512:1024], in_=wsim[:, 2048:4096])
+        tl["o0"] = opool.tile([P, 4, NOUT], F32, name="o_sb")
+        tl["acc"] = psum.tile([P, 512], F32, name="acc4", tag="b4")
+        nc.tensor.matmul_mx(out=tl["acc"][:], lhsT=x_codes[:, 0, 0:128].bitcast(FP8X4), lhsT_scale=x_scales[:, 0, 0:128], rhs=w_codes[:, 0:512].bitcast(FP8X4), rhs_scale=w_scales[:, 0:512], start=True, stop=True)
+        nc.vector.tensor_tensor(out=tl["o0"][:, 0, 0:512], in0=tl["acc"][:], in1=bias_f[:, 0:512], op=ALU.add)
+        tl["acc"] = psum.tile([P, 512], F32, name="acc5", tag="b5")
+        nc.tensor.matmul_mx(out=tl["acc"][:], lhsT=x_codes[:, 0, 0:128].bitcast(FP8X4), lhsT_scale=x_scales[:, 0, 0:128], rhs=w_codes[:, 512:1024].bitcast(FP8X4), rhs_scale=w_scales[:, 512:1024], start=True, stop=True)
+        nc.vector.tensor_tensor(out=tl["o0"][:, 0, 512:1024], in0=tl["acc"][:], in1=bias_f[:, 512:1024], op=ALU.add)
+        nc.sync.dma_start(out=of[0 : 512, :].rearrange("(p t) n -> p t n", t=4)[:, 0, 0:1024], in_=tl["o0"][:, 0, 0:1024])
+        tl["acc"] = psum.tile([P, 512], F32, name="acc6", tag="b6")
+        nc.tensor.matmul_mx(out=tl["acc"][:], lhsT=x_codes[:, 0, 128:256].bitcast(FP8X4), lhsT_scale=x_scales[:, 0, 128:256], rhs=w_codes[:, 0:512].bitcast(FP8X4), rhs_scale=w_scales[:, 0:512], start=True, stop=True)
+        nc.scalar.copy(out=tl["o0"][:, 1, 0:512], in_=tl["acc"][:])
+        nc.gpsimd.tensor_tensor(out=tl["o0"][:, 1, 0:512], in0=tl["o0"][:, 1, 0:512], in1=bias_f[:, 0:512], op=ALU.add)
+        tl["acc"] = psum.tile([P, 512], F32, name="acc7", tag="b7")
+        nc.tensor.matmul_mx(out=tl["acc"][:], lhsT=x_codes[:, 0, 128:256].bitcast(FP8X4), lhsT_scale=x_scales[:, 0, 128:256], rhs=w_codes[:, 512:1024].bitcast(FP8X4), rhs_scale=w_scales[:, 512:1024], start=True, stop=True)
+        nc.vector.tensor_tensor(out=tl["o0"][:, 1, 512:1024], in0=tl["acc"][:], in1=bias_f[:, 512:1024], op=ALU.add)
+        nc.vector.quantize_mx(out=x_codes[:, 1, :].bitcast(FP8X4), scales=x_scales[:, 1, :], in_=tl["xg1"][:].rearrange("p t r v -> p (t r v)"))
+        nc.sync.dma_start(out=of[0 : 512, :].rearrange("(p t) n -> p t n", t=4)[:, 1, 0:1024], in_=tl["o0"][:, 1, 0:1024])
+        tl["acc"] = psum.tile([P, 512], F32, name="acc4", tag="b4")
+        nc.tensor.matmul_mx(out=tl["acc"][:], lhsT=x_codes[:, 0, 256:384].bitcast(FP8X4), lhsT_scale=x_scales[:, 0, 256:384], rhs=w_codes[:, 0:512].bitcast(FP8X4), rhs_scale=w_scales[:, 0:512], start=True, stop=True)
+        nc.scalar.copy(out=tl["o0"][:, 2, 0:512], in_=tl["acc"][:])
+        nc.gpsimd.tensor_tensor(out=tl["o0"][:, 2, 0:512], in0=tl["o0"][:, 2, 0:512], in1=bias_f[:, 0:512], op=ALU.add)
+        tl["acc"] = psum.tile([P, 512], F32, name="acc5", tag="b5")
+        nc.tensor.matmul_mx(out=tl["acc"][:], lhsT=x_codes[:, 0, 256:384].bitcast(FP8X4), lhsT_scale=x_scales[:, 0, 256:384], rhs=w_codes[:, 512:1024].bitcast(FP8X4), rhs_scale=w_scales[:, 512:1024], start=True, stop=True)
+        nc.vector.tensor_tensor(out=tl["o0"][:, 2, 512:1024], in0=tl["acc"][:], in1=bias_f[:, 512:1024], op=ALU.add)
+        nc.sync.dma_start(out=of[0 : 512, :].rearrange("(p t) n -> p t n", t=4)[:, 2, 0:1024], in_=tl["o0"][:, 2, 0:1024])
+        tl["acc"] = psum.tile([P, 512], F32, name="acc6", tag="b6")
+        nc.tensor.matmul_mx(out=tl["acc"][:], lhsT=x_codes[:, 0, 384:512].bitcast(FP8X4), lhsT_scale=x_scales[:, 0, 384:512], rhs=w_codes[:, 0:512].bitcast(FP8X4), rhs_scale=w_scales[:, 0:512], start=True, stop=True)
+        nc.vector.tensor_tensor(out=tl["o0"][:, 3, 0:512], in0=tl["acc"][:], in1=bias_f[:, 0:512], op=ALU.add)
+        tl["acc"] = psum.tile([P, 512], F32, name="acc7", tag="b7")
+        nc.tensor.matmul_mx(out=tl["acc"][:], lhsT=x_codes[:, 0, 384:512].bitcast(FP8X4), lhsT_scale=x_scales[:, 0, 384:512], rhs=w_codes[:, 512:1024].bitcast(FP8X4), rhs_scale=w_scales[:, 512:1024], start=True, stop=True)
+        nc.vector.tensor_tensor(out=tl["o0"][:, 3, 512:1024], in0=tl["acc"][:], in1=bias_f[:, 512:1024], op=ALU.add)
+        nc.sync.dma_start(out=of[0 : 512, :].rearrange("(p t) n -> p t n", t=4)[:, 3, 0:1024], in_=tl["o0"][:, 3, 0:1024])
+        for b in range(2):
+            tl["pt2_%d" % b] = psum.tile([P, 2, 2, P], F32, name="pt2_%d" % b, tag="b%d" % (2 + b))
+            for tt in range(2):
+                for u in range(2):
+                    nc.tensor.transpose(out=tl["pt2_%d" % b][:, tt, u, :], in_=x_sb[:, 2, 2 * b + tt, :].bitcast(F32)[:, u : 2 * P : 2], identity=ident[:])
+        tl["o1"] = opool.tile([P, 4, NOUT], F32, name="o_sb")
+        tl["acc"] = psum.tile([P, 512], F32, name="acc4", tag="b4")
+        nc.tensor.matmul_mx(out=tl["acc"][:], lhsT=x_codes[:, 1, 0:128].bitcast(FP8X4), lhsT_scale=x_scales[:, 1, 0:128], rhs=w_codes[:, 0:512].bitcast(FP8X4), rhs_scale=w_scales[:, 0:512], start=True, stop=True)
+        nc.scalar.copy(out=tl["o1"][:, 0, 0:512], in_=tl["acc"][:])
+        nc.gpsimd.tensor_tensor(out=tl["o1"][:, 0, 0:512], in0=tl["o1"][:, 0, 0:512], in1=bias_f[:, 0:512], op=ALU.add)
+        tl["acc"] = psum.tile([P, 512], F32, name="acc5", tag="b5")
+        nc.tensor.matmul_mx(out=tl["acc"][:], lhsT=x_codes[:, 1, 0:128].bitcast(FP8X4), lhsT_scale=x_scales[:, 1, 0:128], rhs=w_codes[:, 512:1024].bitcast(FP8X4), rhs_scale=w_scales[:, 512:1024], start=True, stop=True)
+        nc.vector.tensor_tensor(out=tl["o1"][:, 0, 512:1024], in0=tl["acc"][:], in1=bias_f[:, 512:1024], op=ALU.add)
+        tl["acc"] = psum.tile([P, 512], F32, name="acc6", tag="b6")
+        nc.tensor.matmul_mx(out=tl["acc"][:], lhsT=x_codes[:, 1, 128:256].bitcast(FP8X4), lhsT_scale=x_scales[:, 1, 128:256], rhs=w_codes[:, 0:512].bitcast(FP8X4), rhs_scale=w_scales[:, 0:512], start=True, stop=True)
+        nc.scalar.copy(out=tl["o1"][:, 1, 0:512], in_=tl["acc"][:])
+        nc.gpsimd.tensor_tensor(out=tl["o1"][:, 1, 0:512], in0=tl["o1"][:, 1, 0:512], in1=bias_f[:, 0:512], op=ALU.add)
+        tl["xg2"] = xgpool.tile([P, 4, P, 4], BF16, name="xg", align_bytes=64)
+        for b in range(2):
+            nc.scalar.copy(out=tl["xg2"][:].bitcast(F32)[:, 2 * b : 2 * b + 2, :, :], in_=tl["pt2_%d" % b][:].rearrange("p t u r -> p t r u"))
+        tl["acc"] = psum.tile([P, 512], F32, name="acc7", tag="b7")
+        nc.tensor.matmul_mx(out=tl["acc"][:], lhsT=x_codes[:, 1, 128:256].bitcast(FP8X4), lhsT_scale=x_scales[:, 1, 128:256], rhs=w_codes[:, 512:1024].bitcast(FP8X4), rhs_scale=w_scales[:, 512:1024], start=True, stop=True)
+        nc.vector.tensor_tensor(out=tl["o1"][:, 1, 512:1024], in0=tl["acc"][:], in1=bias_f[:, 512:1024], op=ALU.add)
+        nc.sync.dma_start(out=of[512 : 1024, :].rearrange("(p t) n -> p t n", t=4)[:, 0:2, 0:1024], in_=tl["o1"][:, 0:2, 0:1024])
+        tl["acc"] = psum.tile([P, 512], F32, name="acc4", tag="b4")
+        nc.tensor.matmul_mx(out=tl["acc"][:], lhsT=x_codes[:, 1, 256:384].bitcast(FP8X4), lhsT_scale=x_scales[:, 1, 256:384], rhs=w_codes[:, 0:512].bitcast(FP8X4), rhs_scale=w_scales[:, 0:512], start=True, stop=True)
+        nc.scalar.copy(out=tl["o1"][:, 2, 0:512], in_=tl["acc"][:])
+        nc.gpsimd.tensor_tensor(out=tl["o1"][:, 2, 0:512], in0=tl["o1"][:, 2, 0:512], in1=bias_f[:, 0:512], op=ALU.add)
+        tl["acc"] = psum.tile([P, 512], F32, name="acc5", tag="b5")
+        nc.tensor.matmul_mx(out=tl["acc"][:], lhsT=x_codes[:, 1, 256:384].bitcast(FP8X4), lhsT_scale=x_scales[:, 1, 256:384], rhs=w_codes[:, 512:1024].bitcast(FP8X4), rhs_scale=w_scales[:, 512:1024], start=True, stop=True)
+        nc.vector.tensor_tensor(out=tl["o1"][:, 2, 512:1024], in0=tl["acc"][:], in1=bias_f[:, 512:1024], op=ALU.add)
+        nc.vector.quantize_mx(out=x_codes[:, 2, :].bitcast(FP8X4), scales=x_scales[:, 2, :], in_=tl["xg2"][:].rearrange("p t r v -> p (t r v)"))
+        tl["acc"] = psum.tile([P, 512], F32, name="acc6", tag="b6")
+        nc.tensor.matmul_mx(out=tl["acc"][:], lhsT=x_codes[:, 1, 384:512].bitcast(FP8X4), lhsT_scale=x_scales[:, 1, 384:512], rhs=w_codes[:, 0:512].bitcast(FP8X4), rhs_scale=w_scales[:, 0:512], start=True, stop=True)
+        nc.vector.tensor_tensor(out=tl["o1"][:, 3, 0:512], in0=tl["acc"][:], in1=bias_f[:, 0:512], op=ALU.add)
+        tl["acc"] = psum.tile([P, 512], F32, name="acc7", tag="b7")
+        nc.tensor.matmul_mx(out=tl["acc"][:], lhsT=x_codes[:, 1, 384:512].bitcast(FP8X4), lhsT_scale=x_scales[:, 1, 384:512], rhs=w_codes[:, 512:1024].bitcast(FP8X4), rhs_scale=w_scales[:, 512:1024], start=True, stop=True)
+        nc.vector.tensor_tensor(out=tl["o1"][:, 3, 512:1024], in0=tl["acc"][:], in1=bias_f[:, 512:1024], op=ALU.add)
+        nc.sync.dma_start(out=of[512 : 1024, :].rearrange("(p t) n -> p t n", t=4)[:, 2:4, 0:1024], in_=tl["o1"][:, 2:4, 0:1024])
+        for b in range(2):
+            tl["pt3_%d" % b] = psum.tile([P, 2, 2, P], F32, name="pt3_%d" % b, tag="b%d" % (0 + b))
+            for tt in range(2):
+                for u in range(2):
+                    nc.tensor.transpose(out=tl["pt3_%d" % b][:, tt, u, :], in_=x_sb[:, 3, 2 * b + tt, :].bitcast(F32)[:, u : 2 * P : 2], identity=ident[:])
+        tl["o2"] = opool.tile([P, 4, NOUT], F32, name="o_sb")
+        tl["acc"] = psum.tile([P, 512], F32, name="acc4", tag="b4")
+        nc.tensor.matmul_mx(out=tl["acc"][:], lhsT=x_codes[:, 2, 0:128].bitcast(FP8X4), lhsT_scale=x_scales[:, 2, 0:128], rhs=w_codes[:, 0:512].bitcast(FP8X4), rhs_scale=w_scales[:, 0:512], start=True, stop=True)
+        nc.scalar.copy(out=tl["o2"][:, 0, 0:512], in_=tl["acc"][:])
+        nc.gpsimd.tensor_tensor(out=tl["o2"][:, 0, 0:512], in0=tl["o2"][:, 0, 0:512], in1=bias_f[:, 0:512], op=ALU.add)
+        tl["acc"] = psum.tile([P, 512], F32, name="acc5", tag="b5")
+        nc.tensor.matmul_mx(out=tl["acc"][:], lhsT=x_codes[:, 2, 0:128].bitcast(FP8X4), lhsT_scale=x_scales[:, 2, 0:128], rhs=w_codes[:, 512:1024].bitcast(FP8X4), rhs_scale=w_scales[:, 512:1024], start=True, stop=True)
+        nc.vector.tensor_tensor(out=tl["o2"][:, 0, 512:1024], in0=tl["acc"][:], in1=bias_f[:, 512:1024], op=ALU.add)
+        tl["acc"] = psum.tile([P, 512], F32, name="acc6", tag="b6")
+        nc.tensor.matmul_mx(out=tl["acc"][:], lhsT=x_codes[:, 2, 128:256].bitcast(FP8X4), lhsT_scale=x_scales[:, 2, 128:256], rhs=w_codes[:, 0:512].bitcast(FP8X4), rhs_scale=w_scales[:, 0:512], start=True, stop=True)
+        nc.scalar.copy(out=tl["o2"][:, 1, 0:512], in_=tl["acc"][:])
+        nc.gpsimd.tensor_tensor(out=tl["o2"][:, 1, 0:512], in0=tl["o2"][:, 1, 0:512], in1=bias_f[:, 0:512], op=ALU.add)
+        tl["xg3"] = xgpool.tile([P, 4, P, 4], BF16, name="xg", align_bytes=64)
+        for b in range(2):
+            nc.scalar.copy(out=tl["xg3"][:].bitcast(F32)[:, 2 * b : 2 * b + 2, :, :], in_=tl["pt3_%d" % b][:].rearrange("p t u r -> p t r u"))
+        tl["acc"] = psum.tile([P, 512], F32, name="acc7", tag="b7")
+        nc.tensor.matmul_mx(out=tl["acc"][:], lhsT=x_codes[:, 2, 128:256].bitcast(FP8X4), lhsT_scale=x_scales[:, 2, 128:256], rhs=w_codes[:, 512:1024].bitcast(FP8X4), rhs_scale=w_scales[:, 512:1024], start=True, stop=True)
+        nc.vector.tensor_tensor(out=tl["o2"][:, 1, 512:1024], in0=tl["acc"][:], in1=bias_f[:, 512:1024], op=ALU.add)
+        nc.sync.dma_start(out=of[1024 : 1536, :].rearrange("(p t) n -> p t n", t=4)[:, 0:2, 0:1024], in_=tl["o2"][:, 0:2, 0:1024])
+        tl["acc"] = psum.tile([P, 512], F32, name="acc4", tag="b4")
+        nc.tensor.matmul_mx(out=tl["acc"][:], lhsT=x_codes[:, 2, 256:384].bitcast(FP8X4), lhsT_scale=x_scales[:, 2, 256:384], rhs=w_codes[:, 0:512].bitcast(FP8X4), rhs_scale=w_scales[:, 0:512], start=True, stop=True)
+        nc.scalar.copy(out=tl["o2"][:, 2, 0:512], in_=tl["acc"][:])
+        nc.gpsimd.tensor_tensor(out=tl["o2"][:, 2, 0:512], in0=tl["o2"][:, 2, 0:512], in1=bias_f[:, 0:512], op=ALU.add)
+        tl["acc"] = psum.tile([P, 512], F32, name="acc5", tag="b5")
+        nc.tensor.matmul_mx(out=tl["acc"][:], lhsT=x_codes[:, 2, 256:384].bitcast(FP8X4), lhsT_scale=x_scales[:, 2, 256:384], rhs=w_codes[:, 512:1024].bitcast(FP8X4), rhs_scale=w_scales[:, 512:1024], start=True, stop=True)
+        nc.vector.tensor_tensor(out=tl["o2"][:, 2, 512:1024], in0=tl["acc"][:], in1=bias_f[:, 512:1024], op=ALU.add)
+        nc.vector.quantize_mx(out=x_codes[:, 3, :].bitcast(FP8X4), scales=x_scales[:, 3, :], in_=tl["xg3"][:].rearrange("p t r v -> p (t r v)"))
+        tl["acc"] = psum.tile([P, 512], F32, name="acc6", tag="b6")
+        nc.tensor.matmul_mx(out=tl["acc"][:], lhsT=x_codes[:, 2, 384:512].bitcast(FP8X4), lhsT_scale=x_scales[:, 2, 384:512], rhs=w_codes[:, 0:512].bitcast(FP8X4), rhs_scale=w_scales[:, 0:512], start=True, stop=True)
+        nc.vector.tensor_tensor(out=tl["o2"][:, 3, 0:512], in0=tl["acc"][:], in1=bias_f[:, 0:512], op=ALU.add)
+        tl["acc"] = psum.tile([P, 512], F32, name="acc7", tag="b7")
+        nc.tensor.matmul_mx(out=tl["acc"][:], lhsT=x_codes[:, 2, 384:512].bitcast(FP8X4), lhsT_scale=x_scales[:, 2, 384:512], rhs=w_codes[:, 512:1024].bitcast(FP8X4), rhs_scale=w_scales[:, 512:1024], start=True, stop=True)
+        nc.vector.tensor_tensor(out=tl["o2"][:, 3, 512:1024], in0=tl["acc"][:], in1=bias_f[:, 512:1024], op=ALU.add)
+        nc.sync.dma_start(out=of[1024 : 1536, :].rearrange("(p t) n -> p t n", t=4)[:, 2:4, 0:1024], in_=tl["o2"][:, 2:4, 0:1024])
+        for b in range(2):
+            tl["pt4_%d" % b] = psum.tile([P, 2, 2, P], F32, name="pt4_%d" % b, tag="b%d" % (2 + b))
+            for tt in range(2):
+                for u in range(2):
+                    nc.tensor.transpose(out=tl["pt4_%d" % b][:, tt, u, :], in_=x_sb[:, 4, 2 * b + tt, :].bitcast(F32)[:, u : 2 * P : 2], identity=ident[:])
+        tl["o3"] = opool.tile([P, 4, NOUT], F32, name="o_sb")
+        tl["acc"] = psum.tile([P, 512], F32, name="acc4", tag="b4")
+        nc.tensor.matmul_mx(out=tl["acc"][:], lhsT=x_codes[:, 3, 0:128].bitcast(FP8X4), lhsT_scale=x_scales[:, 3, 0:128], rhs=w_codes[:, 0:512].bitcast(FP8X4), rhs_scale=w_scales[:, 0:512], start=True, stop=True)
+        nc.scalar.copy(out=tl["o3"][:, 0, 0:512], in_=tl["acc"][:])
+        nc.gpsimd.tensor_tensor(out=tl["o3"][:, 0, 0:512], in0=tl["o3"][:, 0, 0:512], in1=bias_f[:, 0:512], op=ALU.add)
+        tl["acc"] = psum.tile([P, 512], F32, name="acc5", tag="b5")
+        nc.tensor.matmul_mx(out=tl["acc"][:], lhsT=x_codes[:, 3, 0:128].bitcast(FP8X4), lhsT_scale=x_scales[:, 3, 0:128], rhs=w_codes[:, 512:1024].bitcast(FP8X4), rhs_scale=w_scales[:, 512:1024], start=True, stop=True)
+        nc.vector.tensor_tensor(out=tl["o3"][:, 0, 512:1024], in0=tl["acc"][:], in1=bias_f[:, 512:1024], op=ALU.add)
+        tl["acc"] = psum.tile([P, 512], F32, name="acc6", tag="b6")
+        nc.tensor.matmul_mx(out=tl["acc"][:], lhsT=x_codes[:, 3, 128:256].bitcast(FP8X4), lhsT_scale=x_scales[:, 3, 128:256], rhs=w_codes[:, 0:512].bitcast(FP8X4), rhs_scale=w_scales[:, 0:512], start=True, stop=True)
+        nc.scalar.copy(out=tl["o3"][:, 1, 0:512], in_=tl["acc"][:])
+        nc.gpsimd.tensor_tensor(out=tl["o3"][:, 1, 0:512], in0=tl["o3"][:, 1, 0:512], in1=bias_f[:, 0:512], op=ALU.add)
+        tl["xg4"] = xgpool.tile([P, 4, P, 4], BF16, name="xg", align_bytes=64)
+        for b in range(2):
+            nc.scalar.copy(out=tl["xg4"][:].bitcast(F32)[:, 2 * b : 2 * b + 2, :, :], in_=tl["pt4_%d" % b][:].rearrange("p t u r -> p t r u"))
+        tl["acc"] = psum.tile([P, 512], F32, name="acc7", tag="b7")
+        nc.tensor.matmul_mx(out=tl["acc"][:], lhsT=x_codes[:, 3, 128:256].bitcast(FP8X4), lhsT_scale=x_scales[:, 3, 128:256], rhs=w_codes[:, 512:1024].bitcast(FP8X4), rhs_scale=w_scales[:, 512:1024], start=True, stop=True)
+        nc.vector.tensor_tensor(out=tl["o3"][:, 1, 512:1024], in0=tl["acc"][:], in1=bias_f[:, 512:1024], op=ALU.add)
+        tl["acc"] = psum.tile([P, 512], F32, name="acc4", tag="b4")
+        nc.tensor.matmul_mx(out=tl["acc"][:], lhsT=x_codes[:, 3, 256:384].bitcast(FP8X4), lhsT_scale=x_scales[:, 3, 256:384], rhs=w_codes[:, 0:512].bitcast(FP8X4), rhs_scale=w_scales[:, 0:512], start=True, stop=True)
+        nc.scalar.copy(out=tl["o3"][:, 2, 0:512], in_=tl["acc"][:])
+        nc.gpsimd.tensor_tensor(out=tl["o3"][:, 2, 0:512], in0=tl["o3"][:, 2, 0:512], in1=bias_f[:, 0:512], op=ALU.add)
+        tl["acc"] = psum.tile([P, 512], F32, name="acc5", tag="b5")
+        nc.tensor.matmul_mx(out=tl["acc"][:], lhsT=x_codes[:, 3, 256:384].bitcast(FP8X4), lhsT_scale=x_scales[:, 3, 256:384], rhs=w_codes[:, 512:1024].bitcast(FP8X4), rhs_scale=w_scales[:, 512:1024], start=True, stop=True)
+        nc.vector.tensor_tensor(out=tl["o3"][:, 2, 512:1024], in0=tl["acc"][:], in1=bias_f[:, 512:1024], op=ALU.add)
+        nc.vector.quantize_mx(out=x_codes[:, 4, :].bitcast(FP8X4), scales=x_scales[:, 4, :], in_=tl["xg4"][:].rearrange("p t r v -> p (t r v)"))
+        tl["acc"] = psum.tile([P, 512], F32, name="acc6", tag="b6")
+        nc.tensor.matmul_mx(out=tl["acc"][:], lhsT=x_codes[:, 3, 384:512].bitcast(FP8X4), lhsT_scale=x_scales[:, 3, 384:512], rhs=w_codes[:, 0:512].bitcast(FP8X4), rhs_scale=w_scales[:, 0:512], start=True, stop=True)
+        nc.vector.tensor_tensor(out=tl["o3"][:, 3, 0:512], in0=tl["acc"][:], in1=bias_f[:, 0:512], op=ALU.add)
+        tl["acc"] = psum.tile([P, 512], F32, name="acc7", tag="b7")
+        nc.tensor.matmul_mx(out=tl["acc"][:], lhsT=x_codes[:, 3, 384:512].bitcast(FP8X4), lhsT_scale=x_scales[:, 3, 384:512], rhs=w_codes[:, 512:1024].bitcast(FP8X4), rhs_scale=w_scales[:, 512:1024], start=True, stop=True)
+        nc.vector.tensor_tensor(out=tl["o3"][:, 3, 512:1024], in0=tl["acc"][:], in1=bias_f[:, 512:1024], op=ALU.add)
+        nc.sync.dma_start(out=of[1536 : 2048, :].rearrange("(p t) n -> p t n", t=4)[:, 0:4, 0:1024], in_=tl["o3"][:, 0:4, 0:1024])
+        for b in range(2):
+            tl["pt5_%d" % b] = psum.tile([P, 2, 2, P], F32, name="pt5_%d" % b, tag="b%d" % (0 + b))
+            for tt in range(2):
+                for u in range(2):
+                    nc.tensor.transpose(out=tl["pt5_%d" % b][:, tt, u, :], in_=x_sb[:, 5, 2 * b + tt, :].bitcast(F32)[:, u : 2 * P : 2], identity=ident[:])
+        tl["o4"] = opool.tile([P, 4, NOUT], F32, name="o_sb")
+        tl["acc"] = psum.tile([P, 512], F32, name="acc4", tag="b4")
+        nc.tensor.matmul_mx(out=tl["acc"][:], lhsT=x_codes[:, 4, 0:128].bitcast(FP8X4), lhsT_scale=x_scales[:, 4, 0:128], rhs=w_codes[:, 0:512].bitcast(FP8X4), rhs_scale=w_scales[:, 0:512], start=True, stop=True)
+        nc.scalar.copy(out=tl["o4"][:, 0, 0:512], in_=tl["acc"][:])
+        nc.gpsimd.tensor_tensor(out=tl["o4"][:, 0, 0:512], in0=tl["o4"][:, 0, 0:512], in1=bias_f[:, 0:512], op=ALU.add)
+        tl["acc"] = psum.tile([P, 512], F32, name="acc5", tag="b5")
+        nc.tensor.matmul_mx(out=tl["acc"][:], lhsT=x_codes[:, 4, 0:128].bitcast(FP8X4), lhsT_scale=x_scales[:, 4, 0:128], rhs=w_codes[:, 512:1024].bitcast(FP8X4), rhs_scale=w_scales[:, 512:1024], start=True, stop=True)
+        nc.vector.tensor_tensor(out=tl["o4"][:, 0, 512:1024], in0=tl["acc"][:], in1=bias_f[:, 512:1024], op=ALU.add)
+        tl["acc"] = psum.tile([P, 512], F32, name="acc6", tag="b6")
+        nc.tensor.matmul_mx(out=tl["acc"][:], lhsT=x_codes[:, 4, 128:256].bitcast(FP8X4), lhsT_scale=x_scales[:, 4, 128:256], rhs=w_codes[:, 0:512].bitcast(FP8X4), rhs_scale=w_scales[:, 0:512], start=True, stop=True)
+        nc.scalar.copy(out=tl["o4"][:, 1, 0:512], in_=tl["acc"][:])
+        nc.gpsimd.tensor_tensor(out=tl["o4"][:, 1, 0:512], in0=tl["o4"][:, 1, 0:512], in1=bias_f[:, 0:512], op=ALU.add)
+        tl["xg5"] = xgpool.tile([P, 4, P, 4], BF16, name="xg", align_bytes=64)
+        for b in range(2):
+            nc.scalar.copy(out=tl["xg5"][:].bitcast(F32)[:, 2 * b : 2 * b + 2, :, :], in_=tl["pt5_%d" % b][:].rearrange("p t u r -> p t r u"))
+        tl["acc"] = psum.tile([P, 512], F32, name="acc7", tag="b7")
+        nc.tensor.matmul_mx(out=tl["acc"][:], lhsT=x_codes[:, 4, 128:256].bitcast(FP8X4), lhsT_scale=x_scales[:, 4, 128:256], rhs=w_codes[:, 512:1024].bitcast(FP8X4), rhs_scale=w_scales[:, 512:1024], start=True, stop=True)
+        nc.vector.tensor_tensor(out=tl["o4"][:, 1, 512:1024], in0=tl["acc"][:], in1=bias_f[:, 512:1024], op=ALU.add)
+        tl["acc"] = psum.tile([P, 512], F32, name="acc4", tag="b4")
+        nc.tensor.matmul_mx(out=tl["acc"][:], lhsT=x_codes[:, 4, 256:384].bitcast(FP8X4), lhsT_scale=x_scales[:, 4, 256:384], rhs=w_codes[:, 0:512].bitcast(FP8X4), rhs_scale=w_scales[:, 0:512], start=True, stop=True)
+        nc.scalar.copy(out=tl["o4"][:, 2, 0:512], in_=tl["acc"][:])
+        nc.gpsimd.tensor_tensor(out=tl["o4"][:, 2, 0:512], in0=tl["o4"][:, 2, 0:512], in1=bias_f[:, 0:512], op=ALU.add)
+        tl["acc"] = psum.tile([P, 512], F32, name="acc5", tag="b5")
+        nc.tensor.matmul_mx(out=tl["acc"][:], lhsT=x_codes[:, 4, 256:384].bitcast(FP8X4), lhsT_scale=x_scales[:, 4, 256:384], rhs=w_codes[:, 512:1024].bitcast(FP8X4), rhs_scale=w_scales[:, 512:1024], start=True, stop=True)
+        nc.vector.tensor_tensor(out=tl["o4"][:, 2, 512:1024], in0=tl["acc"][:], in1=bias_f[:, 512:1024], op=ALU.add)
+        nc.vector.quantize_mx(out=x_codes[:, 5, :].bitcast(FP8X4), scales=x_scales[:, 5, :], in_=tl["xg5"][:].rearrange("p t r v -> p (t r v)"))
+        tl["acc"] = psum.tile([P, 512], F32, name="acc6", tag="b6")
+        nc.tensor.matmul_mx(out=tl["acc"][:], lhsT=x_codes[:, 4, 384:512].bitcast(FP8X4), lhsT_scale=x_scales[:, 4, 384:512], rhs=w_codes[:, 0:512].bitcast(FP8X4), rhs_scale=w_scales[:, 0:512], start=True, stop=True)
+        nc.vector.tensor_tensor(out=tl["o4"][:, 3, 0:512], in0=tl["acc"][:], in1=bias_f[:, 0:512], op=ALU.add)
+        tl["acc"] = psum.tile([P, 512], F32, name="acc7", tag="b7")
+        nc.tensor.matmul_mx(out=tl["acc"][:], lhsT=x_codes[:, 4, 384:512].bitcast(FP8X4), lhsT_scale=x_scales[:, 4, 384:512], rhs=w_codes[:, 512:1024].bitcast(FP8X4), rhs_scale=w_scales[:, 512:1024], start=True, stop=True)
+        nc.vector.tensor_tensor(out=tl["o4"][:, 3, 512:1024], in0=tl["acc"][:], in1=bias_f[:, 512:1024], op=ALU.add)
+        nc.sync.dma_start(out=of[2048 : 2560, :].rearrange("(p t) n -> p t n", t=4)[:, 0:4, 0:1024], in_=tl["o4"][:, 0:4, 0:1024])
+        for b in range(2):
+            tl["pt6_%d" % b] = psum.tile([P, 2, 2, P], F32, name="pt6_%d" % b, tag="b%d" % (2 + b))
+            for tt in range(2):
+                for u in range(2):
+                    nc.tensor.transpose(out=tl["pt6_%d" % b][:, tt, u, :], in_=x_sb[:, 6, 2 * b + tt, :].bitcast(F32)[:, u : 2 * P : 2], identity=ident[:])
+        tl["o5"] = opool.tile([P, 4, NOUT], F32, name="o_sb")
+        tl["acc"] = psum.tile([P, 512], F32, name="acc4", tag="b4")
+        nc.tensor.matmul_mx(out=tl["acc"][:], lhsT=x_codes[:, 5, 0:128].bitcast(FP8X4), lhsT_scale=x_scales[:, 5, 0:128], rhs=w_codes[:, 0:512].bitcast(FP8X4), rhs_scale=w_scales[:, 0:512], start=True, stop=True)
+        nc.scalar.copy(out=tl["o5"][:, 0, 0:512], in_=tl["acc"][:])
+        nc.gpsimd.tensor_tensor(out=tl["o5"][:, 0, 0:512], in0=tl["o5"][:, 0, 0:512], in1=bias_f[:, 0:512], op=ALU.add)
+        tl["acc"] = psum.tile([P, 512], F32, name="acc5", tag="b5")
+        nc.tensor.matmul_mx(out=tl["acc"][:], lhsT=x_codes[:, 5, 0:128].bitcast(FP8X4), lhsT_scale=x_scales[:, 5, 0:128], rhs=w_codes[:, 512:1024].bitcast(FP8X4), rhs_scale=w_scales[:, 512:1024], start=True, stop=True)
+        nc.vector.tensor_tensor(out=tl["o5"][:, 0, 512:1024], in0=tl["acc"][:], in1=bias_f[:, 512:1024], op=ALU.add)
+        tl["acc"] = psum.tile([P, 512], F32, name="acc6", tag="b6")
+        nc.tensor.matmul_mx(out=tl["acc"][:], lhsT=x_codes[:, 5, 128:256].bitcast(FP8X4), lhsT_scale=x_scales[:, 5, 128:256], rhs=w_codes[:, 0:512].bitcast(FP8X4), rhs_scale=w_scales[:, 0:512], start=True, stop=True)
+        nc.scalar.copy(out=tl["o5"][:, 1, 0:512], in_=tl["acc"][:])
+        nc.gpsimd.tensor_tensor(out=tl["o5"][:, 1, 0:512], in0=tl["o5"][:, 1, 0:512], in1=bias_f[:, 0:512], op=ALU.add)
+        tl["xg6"] = xgpool.tile([P, 4, P, 4], BF16, name="xg", align_bytes=64)
+        for b in range(2):
+            nc.scalar.copy(out=tl["xg6"][:].bitcast(F32)[:, 2 * b : 2 * b + 2, :, :], in_=tl["pt6_%d" % b][:].rearrange("p t u r -> p t r u"))
+        tl["acc"] = psum.tile([P, 512], F32, name="acc7", tag="b7")
+        nc.tensor.matmul_mx(out=tl["acc"][:], lhsT=x_codes[:, 5, 128:256].bitcast(FP8X4), lhsT_scale=x_scales[:, 5, 128:256], rhs=w_codes[:, 512:1024].bitcast(FP8X4), rhs_scale=w_scales[:, 512:1024], start=True, stop=True)
+        nc.vector.tensor_tensor(out=tl["o5"][:, 1, 512:1024], in0=tl["acc"][:], in1=bias_f[:, 512:1024], op=ALU.add)
+        tl["acc"] = psum.tile([P, 512], F32, name="acc4", tag="b4")
+        nc.tensor.matmul_mx(out=tl["acc"][:], lhsT=x_codes[:, 5, 256:384].bitcast(FP8X4), lhsT_scale=x_scales[:, 5, 256:384], rhs=w_codes[:, 0:512].bitcast(FP8X4), rhs_scale=w_scales[:, 0:512], start=True, stop=True)
+        nc.scalar.copy(out=tl["o5"][:, 2, 0:512], in_=tl["acc"][:])
+        nc.gpsimd.tensor_tensor(out=tl["o5"][:, 2, 0:512], in0=tl["o5"][:, 2, 0:512], in1=bias_f[:, 0:512], op=ALU.add)
+        tl["acc"] = psum.tile([P, 512], F32, name="acc5", tag="b5")
+        nc.tensor.matmul_mx(out=tl["acc"][:], lhsT=x_codes[:, 5, 256:384].bitcast(FP8X4), lhsT_scale=x_scales[:, 5, 256:384], rhs=w_codes[:, 512:1024].bitcast(FP8X4), rhs_scale=w_scales[:, 512:1024], start=True, stop=True)
+        nc.vector.tensor_tensor(out=tl["o5"][:, 2, 512:1024], in0=tl["acc"][:], in1=bias_f[:, 512:1024], op=ALU.add)
+        nc.vector.quantize_mx(out=x_codes[:, 6, :].bitcast(FP8X4), scales=x_scales[:, 6, :], in_=tl["xg6"][:].rearrange("p t r v -> p (t r v)"))
+        tl["acc"] = psum.tile([P, 512], F32, name="acc6", tag="b6")
+        nc.tensor.matmul_mx(out=tl["acc"][:], lhsT=x_codes[:, 5, 384:512].bitcast(FP8X4), lhsT_scale=x_scales[:, 5, 384:512], rhs=w_codes[:, 0:512].bitcast(FP8X4), rhs_scale=w_scales[:, 0:512], start=True, stop=True)
+        nc.vector.tensor_tensor(out=tl["o5"][:, 3, 0:512], in0=tl["acc"][:], in1=bias_f[:, 0:512], op=ALU.add)
+        tl["acc"] = psum.tile([P, 512], F32, name="acc7", tag="b7")
+        nc.tensor.matmul_mx(out=tl["acc"][:], lhsT=x_codes[:, 5, 384:512].bitcast(FP8X4), lhsT_scale=x_scales[:, 5, 384:512], rhs=w_codes[:, 512:1024].bitcast(FP8X4), rhs_scale=w_scales[:, 512:1024], start=True, stop=True)
+        nc.vector.tensor_tensor(out=tl["o5"][:, 3, 512:1024], in0=tl["acc"][:], in1=bias_f[:, 512:1024], op=ALU.add)
+        nc.sync.dma_start(out=of[2560 : 3072, :].rearrange("(p t) n -> p t n", t=4)[:, 0:4, 0:1024], in_=tl["o5"][:, 0:4, 0:1024])
+        for b in range(2):
+            tl["pt7_%d" % b] = psum.tile([P, 2, 2, P], F32, name="pt7_%d" % b, tag="b%d" % (0 + b))
+            for tt in range(2):
+                for u in range(2):
+                    nc.tensor.transpose(out=tl["pt7_%d" % b][:, tt, u, :], in_=x_sb[:, 7, 2 * b + tt, :].bitcast(F32)[:, u : 2 * P : 2], identity=ident[:])
+        tl["o6"] = opool.tile([P, 4, NOUT], F32, name="o_sb")
+        tl["acc"] = psum.tile([P, 512], F32, name="acc4", tag="b4")
+        nc.tensor.matmul_mx(out=tl["acc"][:], lhsT=x_codes[:, 6, 0:128].bitcast(FP8X4), lhsT_scale=x_scales[:, 6, 0:128], rhs=w_codes[:, 0:512].bitcast(FP8X4), rhs_scale=w_scales[:, 0:512], start=True, stop=True)
+        nc.scalar.copy(out=tl["o6"][:, 0, 0:512], in_=tl["acc"][:])
+        nc.gpsimd.tensor_tensor(out=tl["o6"][:, 0, 0:512], in0=tl["o6"][:, 0, 0:512], in1=bias_f[:, 0:512], op=ALU.add)
+        tl["acc"] = psum.tile([P, 512], F32, name="acc5", tag="b5")
+        nc.tensor.matmul_mx(out=tl["acc"][:], lhsT=x_codes[:, 6, 0:128].bitcast(FP8X4), lhsT_scale=x_scales[:, 6, 0:128], rhs=w_codes[:, 512:1024].bitcast(FP8X4), rhs_scale=w_scales[:, 512:1024], start=True, stop=True)
+        nc.vector.tensor_tensor(out=tl["o6"][:, 0, 512:1024], in0=tl["acc"][:], in1=bias_f[:, 512:1024], op=ALU.add)
+        tl["acc"] = psum.tile([P, 512], F32, name="acc6", tag="b6")
+        nc.tensor.matmul_mx(out=tl["acc"][:], lhsT=x_codes[:, 6, 128:256].bitcast(FP8X4), lhsT_scale=x_scales[:, 6, 128:256], rhs=w_codes[:, 0:512].bitcast(FP8X4), rhs_scale=w_scales[:, 0:512], start=True, stop=True)
+        nc.scalar.copy(out=tl["o6"][:, 1, 0:512], in_=tl["acc"][:])
+        nc.gpsimd.tensor_tensor(out=tl["o6"][:, 1, 0:512], in0=tl["o6"][:, 1, 0:512], in1=bias_f[:, 0:512], op=ALU.add)
+        tl["xg7"] = xgpool.tile([P, 4, P, 4], BF16, name="xg", align_bytes=64)
+        for b in range(2):
+            nc.scalar.copy(out=tl["xg7"][:].bitcast(F32)[:, 2 * b : 2 * b + 2, :, :], in_=tl["pt7_%d" % b][:].rearrange("p t u r -> p t r u"))
+        tl["acc"] = psum.tile([P, 512], F32, name="acc7", tag="b7")
+        nc.tensor.matmul_mx(out=tl["acc"][:], lhsT=x_codes[:, 6, 128:256].bitcast(FP8X4), lhsT_scale=x_scales[:, 6, 128:256], rhs=w_codes[:, 512:1024].bitcast(FP8X4), rhs_scale=w_scales[:, 512:1024], start=True, stop=True)
+        nc.vector.tensor_tensor(out=tl["o6"][:, 1, 512:1024], in0=tl["acc"][:], in1=bias_f[:, 512:1024], op=ALU.add)
+        tl["acc"] = psum.tile([P, 512], F32, name="acc4", tag="b4")
+        nc.tensor.matmul_mx(out=tl["acc"][:], lhsT=x_codes[:, 6, 256:384].bitcast(FP8X4), lhsT_scale=x_scales[:, 6, 256:384], rhs=w_codes[:, 0:512].bitcast(FP8X4), rhs_scale=w_scales[:, 0:512], start=True, stop=True)
+        nc.scalar.copy(out=tl["o6"][:, 2, 0:512], in_=tl["acc"][:])
+        nc.gpsimd.tensor_tensor(out=tl["o6"][:, 2, 0:512], in0=tl["o6"][:, 2, 0:512], in1=bias_f[:, 0:512], op=ALU.add)
+        tl["acc"] = psum.tile([P, 512], F32, name="acc5", tag="b5")
+        nc.tensor.matmul_mx(out=tl["acc"][:], lhsT=x_codes[:, 6, 256:384].bitcast(FP8X4), lhsT_scale=x_scales[:, 6, 256:384], rhs=w_codes[:, 512:1024].bitcast(FP8X4), rhs_scale=w_scales[:, 512:1024], start=True, stop=True)
+        nc.vector.tensor_tensor(out=tl["o6"][:, 2, 512:1024], in0=tl["acc"][:], in1=bias_f[:, 512:1024], op=ALU.add)
+        nc.vector.quantize_mx(out=x_codes[:, 7, :].bitcast(FP8X4), scales=x_scales[:, 7, :], in_=tl["xg7"][:].rearrange("p t r v -> p (t r v)"))
+        tl["acc"] = psum.tile([P, 512], F32, name="acc6", tag="b6")
+        nc.tensor.matmul_mx(out=tl["acc"][:], lhsT=x_codes[:, 6, 384:512].bitcast(FP8X4), lhsT_scale=x_scales[:, 6, 384:512], rhs=w_codes[:, 0:512].bitcast(FP8X4), rhs_scale=w_scales[:, 0:512], start=True, stop=True)
+        nc.vector.tensor_tensor(out=tl["o6"][:, 3, 0:512], in0=tl["acc"][:], in1=bias_f[:, 0:512], op=ALU.add)
+        tl["acc"] = psum.tile([P, 512], F32, name="acc7", tag="b7")
+        nc.tensor.matmul_mx(out=tl["acc"][:], lhsT=x_codes[:, 6, 384:512].bitcast(FP8X4), lhsT_scale=x_scales[:, 6, 384:512], rhs=w_codes[:, 512:1024].bitcast(FP8X4), rhs_scale=w_scales[:, 512:1024], start=True, stop=True)
+        nc.vector.tensor_tensor(out=tl["o6"][:, 3, 512:1024], in0=tl["acc"][:], in1=bias_f[:, 512:1024], op=ALU.add)
+        nc.sync.dma_start(out=of[3072 : 3584, :].rearrange("(p t) n -> p t n", t=4)[:, 0:4, 0:1024], in_=tl["o6"][:, 0:4, 0:1024])
+        tl["o7"] = opool.tile([P, 4, NOUT], F32, name="o_sb")
+        tl["acc"] = psum.tile([P, 512], F32, name="acc4", tag="b4")
+        nc.tensor.matmul_mx(out=tl["acc"][:], lhsT=x_codes[:, 7, 0:128].bitcast(FP8X4), lhsT_scale=x_scales[:, 7, 0:128], rhs=w_codes[:, 0:512].bitcast(FP8X4), rhs_scale=w_scales[:, 0:512], start=True, stop=True)
+        nc.scalar.copy(out=tl["o7"][:, 0, 0:512], in_=tl["acc"][:])
+        nc.gpsimd.tensor_tensor(out=tl["o7"][:, 0, 0:512], in0=tl["o7"][:, 0, 0:512], in1=bias_f[:, 0:512], op=ALU.add)
+        tl["acc"] = psum.tile([P, 512], F32, name="acc5", tag="b5")
+        nc.tensor.matmul_mx(out=tl["acc"][:], lhsT=x_codes[:, 7, 0:128].bitcast(FP8X4), lhsT_scale=x_scales[:, 7, 0:128], rhs=w_codes[:, 512:1024].bitcast(FP8X4), rhs_scale=w_scales[:, 512:1024], start=True, stop=True)
+        nc.vector.tensor_tensor(out=tl["o7"][:, 0, 512:1024], in0=tl["acc"][:], in1=bias_f[:, 512:1024], op=ALU.add)
+        nc.sync.dma_start(out=of[3584 : 4096, :].rearrange("(p t) n -> p t n", t=4)[:, 0, 0:1024], in_=tl["o7"][:, 0, 0:1024])
+        tl["acc"] = psum.tile([P, 512], F32, name="acc6", tag="b6")
+        nc.tensor.matmul_mx(out=tl["acc"][:], lhsT=x_codes[:, 7, 128:256].bitcast(FP8X4), lhsT_scale=x_scales[:, 7, 128:256], rhs=w_codes[:, 0:512].bitcast(FP8X4), rhs_scale=w_scales[:, 0:512], start=True, stop=True)
+        nc.scalar.copy(out=tl["o7"][:, 1, 0:512], in_=tl["acc"][:])
+        nc.gpsimd.tensor_tensor(out=tl["o7"][:, 1, 0:512], in0=tl["o7"][:, 1, 0:512], in1=bias_f[:, 0:512], op=ALU.add)
+        tl["acc"] = psum.tile([P, 512], F32, name="acc7", tag="b7")
+        nc.tensor.matmul_mx(out=tl["acc"][:], lhsT=x_codes[:, 7, 128:256].bitcast(FP8X4), lhsT_scale=x_scales[:, 7, 128:256], rhs=w_codes[:, 512:1024].bitcast(FP8X4), rhs_scale=w_scales[:, 512:1024], start=True, stop=True)
+        nc.vector.tensor_tensor(out=tl["o7"][:, 1, 512:1024], in0=tl["acc"][:], in1=bias_f[:, 512:1024], op=ALU.add)
+        nc.sync.dma_start(out=of[3584 : 4096, :].rearrange("(p t) n -> p t n", t=4)[:, 1, 0:1024], in_=tl["o7"][:, 1, 0:1024])
+        tl["acc"] = psum.tile([P, 512], F32, name="acc4", tag="b4")
+        nc.tensor.matmul_mx(out=tl["acc"][:], lhsT=x_codes[:, 7, 256:384].bitcast(FP8X4), lhsT_scale=x_scales[:, 7, 256:384], rhs=w_codes[:, 0:512].bitcast(FP8X4), rhs_scale=w_scales[:, 0:512], start=True, stop=True)
+        nc.scalar.copy(out=tl["o7"][:, 2, 0:512], in_=tl["acc"][:])
+        nc.gpsimd.tensor_tensor(out=tl["o7"][:, 2, 0:512], in0=tl["o7"][:, 2, 0:512], in1=bias_f[:, 0:512], op=ALU.add)
+        tl["acc"] = psum.tile([P, 512], F32, name="acc5", tag="b5")
+        nc.tensor.matmul_mx(out=tl["acc"][:], lhsT=x_codes[:, 7, 256:384].bitcast(FP8X4), lhsT_scale=x_scales[:, 7, 256:384], rhs=w_codes[:, 512:1024].bitcast(FP8X4), rhs_scale=w_scales[:, 512:1024], start=True, stop=True)
+        nc.vector.tensor_tensor(out=tl["o7"][:, 2, 512:1024], in0=tl["acc"][:], in1=bias_f[:, 512:1024], op=ALU.add)
+        nc.sync.dma_start(out=of[3584 : 4096, :].rearrange("(p t) n -> p t n", t=4)[:, 2, 0:1024], in_=tl["o7"][:, 2, 0:1024])
+        tl["acc"] = psum.tile([P, 512], F32, name="acc6", tag="b6")
+        nc.tensor.matmul_mx(out=tl["acc"][:], lhsT=x_codes[:, 7, 384:512].bitcast(FP8X4), lhsT_scale=x_scales[:, 7, 384:512], rhs=w_codes[:, 0:512].bitcast(FP8X4), rhs_scale=w_scales[:, 0:512], start=True, stop=True)
+        nc.vector.tensor_tensor(out=tl["o7"][:, 3, 0:512], in0=tl["acc"][:], in1=bias_f[:, 0:512], op=ALU.add)
+        tl["acc"] = psum.tile([P, 512], F32, name="acc7", tag="b7")
+        nc.tensor.matmul_mx(out=tl["acc"][:], lhsT=x_codes[:, 7, 384:512].bitcast(FP8X4), lhsT_scale=x_scales[:, 7, 384:512], rhs=w_codes[:, 512:1024].bitcast(FP8X4), rhs_scale=w_scales[:, 512:1024], start=True, stop=True)
+        nc.vector.tensor_tensor(out=tl["o7"][:, 3, 512:1024], in0=tl["acc"][:], in1=bias_f[:, 512:1024], op=ALU.add)
+        nc.sync.dma_start(out=of[3584 : 4096, :].rearrange("(p t) n -> p t n", t=4)[:, 3, 0:1024], in_=tl["o7"][:, 3, 0:1024])

@@ -1,10 +1,8 @@
 from contextlib import ExitStack
 import math
 
-import concourse.bass as bass
 import concourse.masks as masks
 import concourse.mybir as mybir
-import concourse.tile as tile
 
 F32 = mybir.dt.float32
 BF16 = mybir.dt.bfloat16
@@ -13,7 +11,6 @@ U8 = mybir.dt.uint8
 FP8X4 = mybir.dt.float8_e4m3fn_x4
 ALU = mybir.AluOpType
 ACT = mybir.ActivationFunctionType
-AX = mybir.AxisListType
 
 P = 128
 TOK = 4096
@@ -39,12 +36,14 @@ def tile_binaryxnorexceptoutlierslinear_t_kernel(tc, x, weight, bias, out):
         psum = ctx.enter_context(tc.psum_pool(name="psum", bufs=1))
 
         ones_bf = keep.tile([P, P], BF16, name="ones_bf")
+        ones_f = keep.tile([P, P], F32, name="ones_f")
         tinycol = keep.tile([P, 2], BF16, name="tinycol")
         ident = keep.tile([P, P], F32, name="ident")
+        ident_bf = keep.tile([P, P], BF16, name="ident_bf")
+        c_ident = keep.tile([P, P], BF16, name="c_ident")
         w_sb = keep.tile([P, 8, K], BF16, name="w_sb")
         x_sb = keep.tile([P, GROUPS, 4, K], BF16, name="x_sb")
         bias_bc = keep.tile([P, NOUT], BF16, name="bias_bc")
-        bias_f = keep.tile([P, NOUT], F32, name="bias_f")
         x_codes = keep.tile([P, GROUPS, 512], U32, name="x_codes", align_bytes=64)
         x_scales = keep.tile([P, GROUPS, 512], U8, name="x_scales", align_bytes=64)
         w_codes = keep.tile([P, NOUT], U32, name="w_codes", align_bytes=64)
@@ -58,464 +57,203 @@ def tile_binaryxnorexceptoutlierslinear_t_kernel(tc, x, weight, bias, out):
         bm = keep.tile([P, 4 * NOUT], BF16, name="bm")
         oo = keep.tile([P, 4 * NOUT], BF16, name="oo")
         aa = keep.tile([P, 4 * NOUT], BF16, name="aa")
-        cb = keep.tile([P, 4 * NOUT], BF16, name="cb")
+        cb = keep.tile([P, 2 * NOUT], BF16, name="cb")
         wsim = keep.tile([P, 4 * NOUT], BF16, name="wsim", align_bytes=64)
-        junk_s = keep.tile([P, 1024], BF16, name="junk_s")
-        junk_v = keep.tile([P, 1024], F32, name="junk_v")
-        st_s = keep.tile([P, 4], F32, name="st_s")
+        junk_s = keep.tile([P, 512], BF16, name="junk_s")
+        junk_d = keep.tile([P, P], F32, name="junk_d")
+        bn = keep.tile([P, 4, 6], F32, name="bn")
+        st = keep.tile([P, 8], F32, name="st")
+        nbs = keep.tile([P, 1], F32, name="nbs")
+        s4 = keep.tile([P, 1], F32, name="s4")
+        ssq = keep.tile([P, 1], F32, name="ssq")
         st2 = keep.tile([P, 2], F32, name="st2")
-        hl = keep.tile([P, 16], BF16, name="hl")
-        hl2 = keep.tile([P, 4], BF16, name="hl2")
         nbt = keep.tile([P, 1], F32, name="nbt")
-        sm = keep.tile([P, 8], F32, name="sm")
-        w_flat = w_sb[:].rearrange("p j k -> p (j k)")
-        tl = {}
+        sm2 = keep.tile([P, 1], F32, name="sm2")
+        thr = keep.tile([P, 1], F32, name="thr")
+        rc = keep.tile([P, 1], F32, name="rc")
+
+        def cols(c, n=1024):
+            return slice(n * c, n * c + n)
+
         nc.vector.memset(ones_bf[:], 1.0)
+        nc.vector.memset(ones_f[:], 1.0)
         nc.vector.memset(tinycol[:], TINY)
         masks.make_identity(nc, ident[:])
-        ident_bf = keep.tile([P, P], BF16, name="ident_bf")
-        c_ident = keep.tile([P, P], BF16, name="c_ident")
         masks.make_identity(nc, ident_bf[:])
-        nc.sync.dma_start(out=w_sb[:, 0 : 2, :], in_=weight[0 : 256, :].rearrange("(j p) k -> p j k", p=P))
-        nc.sync.dma_start(out=w_sb[:, 2 : 4, :], in_=weight[256 : 512, :].rearrange("(j p) k -> p j k", p=P))
-        nc.sync.dma_start(out=w_sb[:, 4 : 6, :], in_=weight[512 : 768, :].rearrange("(j p) k -> p j k", p=P))
-        nc.sync.dma_start(out=w_sb[:, 6 : 8, :], in_=weight[768 : 1024, :].rearrange("(j p) k -> p j k", p=P))
-        nc.sync.dma_start(out=x_sb[:, 0, :, :], in_=xf[0 : 512, :].rearrange("(p t) k -> p t k", t=4))
-        nc.sync.dma_start(out=x_sb[:, 1, :, :], in_=xf[512 : 1024, :].rearrange("(p t) k -> p t k", t=4))
-        nc.sync.dma_start(out=bias_bc[:], in_=bias.partition_broadcast(P))
-        nc.sync.dma_start(out=x_sb[:, 2, :, :], in_=xf[1024 : 1536, :].rearrange("(p t) k -> p t k", t=4))
-        nc.sync.dma_start(out=x_sb[:, 3, :, :], in_=xf[1536 : 2048, :].rearrange("(p t) k -> p t k", t=4))
-        nc.sync.dma_start(out=x_sb[:, 4, :, :], in_=xf[2048 : 2560, :].rearrange("(p t) k -> p t k", t=4))
-        nc.sync.dma_start(out=x_sb[:, 5, :, :], in_=xf[2560 : 3072, :].rearrange("(p t) k -> p t k", t=4))
-        nc.sync.dma_start(out=x_sb[:, 6, :, :], in_=xf[3072 : 3584, :].rearrange("(p t) k -> p t k", t=4))
-        nc.sync.dma_start(out=x_sb[:, 7, :, :], in_=xf[3584 : 4096, :].rearrange("(p t) k -> p t k", t=4))
-        nc.gpsimd.tensor_scalar(out=bias_f[:], in0=bias_bc[:], scalar1=1.0, scalar2=0.0, op0=ALU.mult, op1=ALU.add)
-        tl["pw0"] = psum.tile([P, 2, 2, P], F32, name="pw0", tag="b0")
-        for jj in range(2):
-            for u in range(2):
-                nc.tensor.transpose(out=tl["pw0"][:, jj, u, :], in_=w_sb[:, 0 + jj, :].bitcast(F32)[:, u : 2 * P : 2], identity=ident[:])
-        tl["sw"] = psum.tile([P, 256], F32, name="ps_sw", tag="b4")
-        for j in (0, 1):
+
+        for c in range(4):
+            nc.sync.dma_start(out=w_sb[:, 2 * c : 2 * c + 2, :], in_=weight[256 * c : 256 * c + 256, :].rearrange("(j p) k -> p j k", p=P))
+        for g in range(GROUPS):
+            nc.sync.dma_start(out=x_sb[:, g, :, :], in_=xf[512 * g : 512 * g + 512, :].rearrange("(p t) k -> p t k", t=4))
+            if g == 1:
+                nc.sync.dma_start(out=bias_bc[:], in_=bias.partition_broadcast(P))
+
+        half = NW // (2 * P)
+        sw = psum.tile([P, 256], F32, name="sw", tag="b4")
+        for c in range(4):
             for b in range(2):
-                nc.tensor.matmul(out=tl["sw"][:], lhsT=ones_bf[:], rhs=w_sb[:, j, 256 * b : 256 * b + 256], start=(j == 0 and b == 0), stop=(j == 7 and b == 1))
-        nc.scalar.activation(out=junk_s[:, 0:1024], in_=w_flat[:, 0:1024], func=ACT.Square, accum_out=st_s[:, 0:1])
-        nc.vector.tensor_copy(out=wT32[:, 0 : 256, :].rearrange("p (j r) u -> p j r u", j=2), in_=tl["pw0"][:].rearrange("p j u r -> p j r u"))
-        tl["pw1"] = psum.tile([P, 2, 2, P], F32, name="pw1", tag="b1")
-        for jj in range(2):
-            for u in range(2):
-                nc.tensor.transpose(out=tl["pw1"][:, jj, u, :], in_=w_sb[:, 2 + jj, :].bitcast(F32)[:, u : 2 * P : 2], identity=ident[:])
-        for j in (2, 3):
+                nc.tensor.matmul(out=sw[:], lhsT=ones_bf[:], rhs=w_sb[:, 2 * c, cols(b, 256)], start=(c == 0 and b == 0), stop=(c == 3 and b == 1))
+            nc.scalar.activation(out=junk_s[:], in_=w_sb[:, 2 * c, :], func=ACT.Square, accum_out=st[:, 2 + c : 3 + c])
+            nc.vector.bn_stats(out=bn[:, c, :], in_=w_sb[:, 2 * c + 1, :])
+        nc.scalar.activation(out=junk_s[:, 0:256], in_=sw[:], func=ACT.Identity, scale=-SC / NW, accum_out=nbs[:])
+        nc.vector.bn_aggr(out=st[:, 0:2], in_=bn[:].rearrange("p c s -> p (c s)"))
+        nc.vector.scalar_tensor_tensor(out=st[:, 6:7], in0=st[:, 0:1], scalar=st[:, 0:1], in1=st[:, 1:2], op0=ALU.mult, op1=ALU.add)
+        pw = []
+        for c in range(4):
+            pw.append(psum.tile([P, 2, 2, P], F32, name="pw", tag="b%d" % c))
+
+        def w_transposes(c):
+            for jj in range(2):
+                for u in range(2):
+                    nc.tensor.transpose(out=pw[c][:, jj, u, :], in_=w_sb[:, 2 * c + jj, :].bitcast(F32)[:, u : 2 * P : 2], identity=ident[:])
+
+        w_transposes(0)
+        cs = psum.tile([P, 8], F32, name="cs", tag="b5")
+        nc.tensor.matmul(out=cs[:, 0:7], lhsT=ones_f[:], rhs=st[:, 0:7], start=True, stop=True)
+        for c in range(1, 4):
+            w_transposes(c)
+
+        def evac(c, copy):
+            copy(out=wT32[:, 256 * c : 256 * c + 256, :].rearrange("p (j r) u -> p j r u", j=2), in_=pw[c][:].rearrange("p j u r -> p j r u"))
+
+        def sign(c):
+            nc.vector.tensor_scalar(out=ws[:, cols(c)], in0=wTf[:, cols(c)], scalar1=-TINY, scalar2=TINY, op0=ALU.max, op1=ALU.min)
+
+        def square(c):
+            nc.scalar.activation(out=q[:, cols(c)], in_=wTf[:, cols(c)], func=ACT.Square, bias=nbt[:], scale=SC)
+
+        def mask(c):
+            nc.vector.tensor_scalar(out=kk[:, cols(c)], in0=q[:, cols(c)], scalar1=thr[:], scalar2=HUGE, op0=ALU.is_le, op1=ALU.mult)
+
+        def masked_sign(c):
+            nc.vector.tensor_tensor(out=bm[:, cols(c)], in0=ws[:, cols(c)], in1=kk[:, cols(c)], op=ALU.mult)
+
+        def outlier_mask(c, by_scalar):
+            if by_scalar:
+                nc.scalar.activation(out=oo[:, cols(c)], in_=kk[:, cols(c)], func=ACT.Identity, scale=-TINY, bias=1.0)
+            else:
+                nc.vector.tensor_scalar(out=oo[:, cols(c)], in0=kk[:, cols(c)], scalar1=-TINY, scalar2=1.0, op0=ALU.mult, op1=ALU.add)
+
+        def outliers(c):
+            nc.vector.tensor_tensor(out=aa[:, cols(c)], in0=wTf[:, cols(c)], in1=oo[:, cols(c)], op=ALU.mult)
+
+        gram = psum.tile([P, P], F32, name="gram", tag="b6")
+        ck = psum.tile([P, 1], F32, name="ck", tag="b7")
+
+        def keep_sums(c):
+            for b in range(8 * c, 8 * c + 8):
+                nc.tensor.matmul(out=gram[:], lhsT=wTf[:, cols(b, P)], rhs=bm[:, cols(b, P)], start=(b == 0), stop=(b == 31))
+                nc.tensor.matmul(out=ck[:], lhsT=kk[:, cols(b, P)], rhs=tinycol[:, 0:1], start=(b == 0), stop=(b == 31))
+
+        def transposes(g, bank):
+            pts = []
             for b in range(2):
-                nc.tensor.matmul(out=tl["sw"][:], lhsT=ones_bf[:], rhs=w_sb[:, j, 256 * b : 256 * b + 256], start=(j == 0 and b == 0), stop=(j == 7 and b == 1))
-        nc.scalar.activation(out=junk_s[:, 0:1024], in_=w_flat[:, 1024:2048], func=ACT.Square, accum_out=st_s[:, 1:2])
-        nc.vector.tensor_copy(out=wT32[:, 256 : 512, :].rearrange("p (j r) u -> p j r u", j=2), in_=tl["pw1"][:].rearrange("p j u r -> p j r u"))
-        tl["pw2"] = psum.tile([P, 2, 2, P], F32, name="pw2", tag="b2")
-        for jj in range(2):
-            for u in range(2):
-                nc.tensor.transpose(out=tl["pw2"][:, jj, u, :], in_=w_sb[:, 4 + jj, :].bitcast(F32)[:, u : 2 * P : 2], identity=ident[:])
-        for j in (4, 5):
+                pt = psum.tile([P, 2, 2, P], F32, name="pt", tag="b%d" % (bank + b))
+                for tt in range(2):
+                    for u in range(2):
+                        nc.tensor.transpose(out=pt[:, tt, u, :], in_=x_sb[:, g, 2 * b + tt, :].bitcast(F32)[:, u : 2 * P : 2], identity=ident[:])
+                pts.append(pt)
+            return pts
+
+        def x_copies(pts):
+            xg = xgpool.tile([P, 4, P, 4], BF16, name="xg", align_bytes=64)
             for b in range(2):
-                nc.tensor.matmul(out=tl["sw"][:], lhsT=ones_bf[:], rhs=w_sb[:, j, 256 * b : 256 * b + 256], start=(j == 0 and b == 0), stop=(j == 7 and b == 1))
-        nc.scalar.activation(out=junk_s[:, 0:1024], in_=w_flat[:, 2048:3072], func=ACT.Square, accum_out=st_s[:, 2:3])
-        nc.vector.tensor_scalar(out=ws[:, 0:2048], in0=wTf[:, 0:2048], scalar1=-TINY, scalar2=TINY, op0=ALU.max, op1=ALU.min)
-        nc.vector.tensor_copy(out=wT32[:, 512 : 768, :].rearrange("p (j r) u -> p j r u", j=2), in_=tl["pw2"][:].rearrange("p j u r -> p j r u"))
-        tl["pw3"] = psum.tile([P, 2, 2, P], F32, name="pw3", tag="b3")
-        for jj in range(2):
-            for u in range(2):
-                nc.tensor.transpose(out=tl["pw3"][:, jj, u, :], in_=w_sb[:, 6 + jj, :].bitcast(F32)[:, u : 2 * P : 2], identity=ident[:])
-        for j in (6, 7):
-            for b in range(2):
-                nc.tensor.matmul(out=tl["sw"][:], lhsT=ones_bf[:], rhs=w_sb[:, j, 256 * b : 256 * b + 256], start=(j == 0 and b == 0), stop=(j == 7 and b == 1))
-        nc.scalar.activation(out=junk_s[:, 0:1024], in_=w_flat[:, 3072:4096], func=ACT.Square, accum_out=st_s[:, 3:4])
-        nc.vector.tensor_copy(out=hl[:, 0:4], in_=st_s[:, 0:4])
-        nc.vector.tensor_tensor(out=hl[:, 4:8], in0=st_s[:, 0:4], in1=hl[:, 0:4], op=ALU.subtract)
-        nc.vector.tensor_copy(out=wT32[:, 768 : 1024, :].rearrange("p (j r) u -> p j r u", j=2), in_=tl["pw3"][:].rearrange("p j u r -> p j r u"))
-        nc.scalar.activation(out=junk_s[:, 0:256], in_=tl["sw"][:], func=ACT.Identity, scale=-SC / NW, accum_out=nbt[:, 0:1])
-        tl["l2a"] = psum.tile([P, 8], F32, name="ps_l2a", tag="b5")
-        nc.tensor.matmul(out=tl["l2a"][:, 0:4], lhsT=ones_bf[:], rhs=hl[:, 0:4], start=True, stop=False)
-        nc.tensor.matmul(out=tl["l2a"][:, 0:4], lhsT=ones_bf[:], rhs=hl[:, 4:8], start=False, stop=True)
+                nc.scalar.copy(out=xg[:].bitcast(F32)[:, 2 * b : 2 * b + 2, :, :], in_=pts[b][:].rearrange("p t u r -> p t r u"))
+            return xg
+
+        def x_quant(g, xg):
+            nc.vector.quantize_mx(out=x_codes[:, g, :].bitcast(FP8X4), scales=x_scales[:, g, :], in_=xg[:].rearrange("p t r v -> p (t r v)"))
+
+        vcopy, scopy = nc.vector.tensor_copy, nc.scalar.copy
+        evac(0, vcopy)
+        nc.vector.tensor_scalar(out=nbt[:], in0=cs[:, 0:1], scalar1=-SC * half / NW, scalar2=nbs[:], op0=ALU.mult, op1=ALU.add)
+        nc.vector.reduce_sum(out=s4[:], in_=cs[:, 2:6], axis=mybir.AxisListType.X)
+        nc.vector.tensor_scalar(out=sm2[:], in0=nbt[:], scalar1=nbt[:], scalar2=-NW / (SC * SC), op0=ALU.mult, op1=ALU.mult)
+        nc.vector.tensor_scalar(out=ssq[:], in0=cs[:, 6:7], scalar1=float(half), scalar2=s4[:], op0=ALU.mult, op1=ALU.add)
+        sign(0)
+        nc.vector.tensor_scalar(out=thr[:], in0=ssq[:], scalar1=sm2[:], scalar2=None, op0=ALU.add)
+        evac(1, vcopy)
+        square(0)
+        mask(0)
+        sign(1)
+        masked_sign(0)
+        keep_sums(0)
+        pt0 = transposes(0, 0)
+        square(1)
+        evac(2, scopy)
+        mask(1)
+        sign(2)
+        masked_sign(1)
+        keep_sums(1)
+        pt1 = transposes(1, 4)
+        square(2)
+        evac(3, scopy)
+        mask(2)
+        sign(3)
+        masked_sign(2)
+        keep_sums(2)
+        square(3)
+        xg0 = x_copies(pt0)
+        outlier_mask(2, False)
+        mask(3)
+        outliers(2)
+        masked_sign(3)
+        keep_sums(3)
+        outlier_mask(3, False)
+        outlier_mask(0, True)
+        wacc = []
+        for b in range(4):
+            wacc.append(psum.tile([P, 512], F32, name="wacc", tag="b%d" % ((2, 3, 0, 1)[b])))
         for b in range(2):
-            tl["pt0_%d" % b] = psum.tile([P, 2, 2, P], F32, name="pt0_%d" % b, tag="b%d" % (0 + b))
-            for tt in range(2):
-                for u in range(2):
-                    nc.tensor.transpose(out=tl["pt0_%d" % b][:, tt, u, :], in_=x_sb[:, 0, 2 * b + tt, :].bitcast(F32)[:, u : 2 * P : 2], identity=ident[:])
-        nc.vector.tensor_scalar(out=ws[:, 2048:4096], in0=wTf[:, 2048:4096], scalar1=-TINY, scalar2=TINY, op0=ALU.max, op1=ALU.min)
-        nc.vector.tensor_scalar(out=sm[:, 2:3], in0=nbt[:, 0:1], scalar1=nbt[:, 0:1], scalar2=-NW / (SC * SC), op0=ALU.mult, op1=ALU.mult)
-        nc.vector.reduce_sum(out=sm[:, 3:4], in_=tl["l2a"][:, 0:4], axis=AX.X)
-        nc.vector.tensor_scalar(out=sm[:, 4:5], in0=sm[:, 3:4], scalar1=sm[:, 2:3], scalar2=None, op0=ALU.add)
-        nc.scalar.activation(out=q[:, 0:1024], in_=wTf[:, 0:1024], func=ACT.Square, bias=nbt[:, 0:1], scale=SC)
-        nc.vector.tensor_scalar(out=kk[:, 0:1024], in0=q[:, 0:1024], scalar1=sm[:, 4:5], scalar2=HUGE, op0=ALU.is_le, op1=ALU.mult)
-        nc.scalar.activation(out=q[:, 1024:2048], in_=wTf[:, 1024:2048], func=ACT.Square, bias=nbt[:, 0:1], scale=SC)
-        for b in range(2):
-            tl["pt1_%d" % b] = psum.tile([P, 2, 2, P], F32, name="pt1_%d" % b, tag="b%d" % (4 + b))
-            for tt in range(2):
-                for u in range(2):
-                    nc.tensor.transpose(out=tl["pt1_%d" % b][:, tt, u, :], in_=x_sb[:, 1, 2 * b + tt, :].bitcast(F32)[:, u : 2 * P : 2], identity=ident[:])
-        nc.vector.tensor_scalar(out=kk[:, 1024:2048], in0=q[:, 1024:2048], scalar1=sm[:, 4:5], scalar2=HUGE, op0=ALU.is_le, op1=ALU.mult)
-        nc.vector.tensor_tensor(out=bm[:, 0:1024], in0=ws[:, 0:1024], in1=kk[:, 0:1024], op=ALU.mult)
-        tl["g"] = psum.tile([P, P], F32, name="ps_g", tag="b6")
-        tl["ck"] = psum.tile([P, 8], F32, name="ps_ck", tag="b7")
-        for b in range(0, 8):
-            nc.tensor.matmul(out=tl["g"][:], lhsT=wTf[:, P * b : P * b + P], rhs=bm[:, P * b : P * b + P], start=(b == 0), stop=(b == 31))
-            nc.tensor.matmul(out=tl["ck"][:, 0:1], lhsT=kk[:, P * b : P * b + P], rhs=tinycol[:, 0:1], start=(b == 0), stop=(b == 31))
-        nc.scalar.activation(out=q[:, 2048:3072], in_=wTf[:, 2048:3072], func=ACT.Square, bias=nbt[:, 0:1], scale=SC)
-        nc.vector.tensor_scalar(out=kk[:, 2048:3072], in0=q[:, 2048:3072], scalar1=sm[:, 4:5], scalar2=HUGE, op0=ALU.is_le, op1=ALU.mult)
-        nc.vector.tensor_tensor(out=bm[:, 1024:2048], in0=ws[:, 1024:2048], in1=kk[:, 1024:2048], op=ALU.mult)
-        for b in range(8, 16):
-            nc.tensor.matmul(out=tl["g"][:], lhsT=wTf[:, P * b : P * b + P], rhs=bm[:, P * b : P * b + P], start=(b == 0), stop=(b == 31))
-            nc.tensor.matmul(out=tl["ck"][:, 0:1], lhsT=kk[:, P * b : P * b + P], rhs=tinycol[:, 0:1], start=(b == 0), stop=(b == 31))
-        nc.scalar.activation(out=q[:, 3072:3584], in_=wTf[:, 3072:3584], func=ACT.Square, bias=nbt[:, 0:1], scale=SC)
-        nc.vector.tensor_scalar(out=kk[:, 3072:3584], in0=q[:, 3072:3584], scalar1=sm[:, 4:5], scalar2=HUGE, op0=ALU.is_le, op1=ALU.mult)
-        nc.vector.tensor_tensor(out=bm[:, 2048:3072], in0=ws[:, 2048:3072], in1=kk[:, 2048:3072], op=ALU.mult)
-        for b in range(16, 24):
-            nc.tensor.matmul(out=tl["g"][:], lhsT=wTf[:, P * b : P * b + P], rhs=bm[:, P * b : P * b + P], start=(b == 0), stop=(b == 31))
-            nc.tensor.matmul(out=tl["ck"][:, 0:1], lhsT=kk[:, P * b : P * b + P], rhs=tinycol[:, 0:1], start=(b == 0), stop=(b == 31))
-        nc.scalar.activation(out=q[:, 3584:4096], in_=wTf[:, 3584:4096], func=ACT.Square, bias=nbt[:, 0:1], scale=SC)
-        nc.vector.tensor_scalar(out=kk[:, 3584:4096], in0=q[:, 3584:4096], scalar1=sm[:, 4:5], scalar2=HUGE, op0=ALU.is_le, op1=ALU.mult)
-        nc.vector.tensor_tensor(out=bm[:, 3072:3584], in0=ws[:, 3072:3584], in1=kk[:, 3072:3584], op=ALU.mult)
-        for b in range(24, 28):
-            nc.tensor.matmul(out=tl["g"][:], lhsT=wTf[:, P * b : P * b + P], rhs=bm[:, P * b : P * b + P], start=(b == 0), stop=(b == 31))
-            nc.tensor.matmul(out=tl["ck"][:, 0:1], lhsT=kk[:, P * b : P * b + P], rhs=tinycol[:, 0:1], start=(b == 0), stop=(b == 31))
-        nc.vector.tensor_tensor(out=bm[:, 3584:4096], in0=ws[:, 3584:4096], in1=kk[:, 3584:4096], op=ALU.mult)
-        for b in range(28, 32):
-            nc.tensor.matmul(out=tl["g"][:], lhsT=wTf[:, P * b : P * b + P], rhs=bm[:, P * b : P * b + P], start=(b == 0), stop=(b == 31))
-            nc.tensor.matmul(out=tl["ck"][:, 0:1], lhsT=kk[:, P * b : P * b + P], rhs=tinycol[:, 0:1], start=(b == 0), stop=(b == 31))
-        tl["xg0"] = xgpool.tile([P, 4, P, 4], BF16, name="xg", align_bytes=64)
-        for b in range(2):
-            nc.scalar.copy(out=tl["xg0"][:].bitcast(F32)[:, 2 * b : 2 * b + 2, :, :], in_=tl["pt0_%d" % b][:].rearrange("p t u r -> p t r u"))
-        nc.scalar.activation(out=oo[:, 2048:3072], in_=kk[:, 2048:3072], func=ACT.Identity, scale=-TINY, bias=1.0)
-        nc.scalar.activation(out=oo[:, 3072:4096], in_=kk[:, 3072:4096], func=ACT.Identity, scale=-TINY, bias=1.0)
-        nc.scalar.activation(out=oo[:, 0:1024], in_=kk[:, 0:1024], func=ACT.Identity, scale=-TINY, bias=1.0)
-        nc.scalar.activation(out=oo[:, 1024:2048], in_=kk[:, 1024:2048], func=ACT.Identity, scale=-TINY, bias=1.0)
-        tl["xg1"] = xgpool.tile([P, 4, P, 4], BF16, name="xg", align_bytes=64)
-        for b in range(2):
-            nc.scalar.copy(out=tl["xg1"][:].bitcast(F32)[:, 2 * b : 2 * b + 2, :, :], in_=tl["pt1_%d" % b][:].rearrange("p t u r -> p t r u"))
-        nc.vector.tensor_tensor(out=aa[:, 2048:3072], in0=wTf[:, 2048:3072], in1=oo[:, 2048:3072], op=ALU.mult)
-        tl["wacc0"] = psum.tile([P, 512], F32, name="wacc0", tag="b2")
-        nc.tensor.matmul(out=tl["wacc0"][:], lhsT=ident_bf[:], rhs=aa[:, 2048:2560], start=True, stop=False)
-        tl["wacc1"] = psum.tile([P, 512], F32, name="wacc1", tag="b3")
-        nc.tensor.matmul(out=tl["wacc1"][:], lhsT=ident_bf[:], rhs=aa[:, 2560:3072], start=True, stop=False)
-        nc.vector.quantize_mx(out=x_codes[:, 0, :].bitcast(FP8X4), scales=x_scales[:, 0, :], in_=tl["xg0"][:].rearrange("p t r v -> p (t r v)"))
-        nc.vector.tensor_tensor(out=aa[:, 3072:4096], in0=wTf[:, 3072:4096], in1=oo[:, 3072:4096], op=ALU.mult)
-        tl["wacc2"] = psum.tile([P, 512], F32, name="wacc2", tag="b0")
-        nc.tensor.matmul(out=tl["wacc2"][:], lhsT=ident_bf[:], rhs=aa[:, 3072:3584], start=True, stop=False)
-        tl["wacc3"] = psum.tile([P, 512], F32, name="wacc3", tag="b1")
-        nc.tensor.matmul(out=tl["wacc3"][:], lhsT=ident_bf[:], rhs=aa[:, 3584:4096], start=True, stop=False)
-        nc.vector.tensor_copy(out=st2[:, 1:2], in_=tl["ck"][:, 0:1])
-        nc.vector.scalar_tensor_tensor(out=junk_v[:, 0:P], in0=tl["g"][:], scalar=1.0, in1=ident[:], op0=ALU.mult, op1=ALU.mult, accum_out=st2[:, 0:1])
-        nc.vector.tensor_copy(out=hl2[:, 0:2], in_=st2[:])
-        nc.vector.tensor_tensor(out=hl2[:, 2:4], in0=st2[:], in1=hl2[:, 0:2], op=ALU.subtract)
-        tl["l2b"] = psum.tile([P, 8], F32, name="ps_l2b", tag="b7")
-        nc.tensor.matmul(out=tl["l2b"][:, 0:2], lhsT=ones_bf[:], rhs=hl2[:, 0:2], start=True, stop=False)
-        nc.tensor.matmul(out=tl["l2b"][:, 0:2], lhsT=ones_bf[:], rhs=hl2[:, 2:4], start=False, stop=True)
-        nc.vector.tensor_tensor(out=aa[:, 0:1024], in0=wTf[:, 0:1024], in1=oo[:, 0:1024], op=ALU.mult)
-        nc.vector.reciprocal(out=sm[:, 5:6], in_=tl["l2b"][:, 1:2])
-        nc.vector.tensor_scalar(out=sm[:, 6:7], in0=tl["l2b"][:, 0:1], scalar1=sm[:, 5:6], scalar2=None, op0=ALU.mult)
-        nc.vector.tensor_scalar(out=c_ident[:], in0=ident_bf[:], scalar1=sm[:, 6:7], scalar2=None, op0=ALU.mult)
-        nc.tensor.matmul(out=tl["wacc0"][:], lhsT=c_ident[:], rhs=bm[:, 2048:2560], start=False, stop=True)
-        nc.tensor.matmul(out=tl["wacc1"][:], lhsT=c_ident[:], rhs=bm[:, 2560:3072], start=False, stop=True)
-        nc.tensor.matmul(out=tl["wacc2"][:], lhsT=c_ident[:], rhs=bm[:, 3072:3584], start=False, stop=True)
-        nc.tensor.matmul(out=tl["wacc3"][:], lhsT=c_ident[:], rhs=bm[:, 3584:4096], start=False, stop=True)
-        nc.scalar.copy(out=wsim[:, 2048:2560], in_=tl["wacc0"][:])
-        nc.scalar.copy(out=wsim[:, 2560:3072], in_=tl["wacc1"][:])
-        nc.scalar.copy(out=wsim[:, 3072:3584], in_=tl["wacc2"][:])
-        nc.vector.tensor_tensor(out=aa[:, 1024:2048], in0=wTf[:, 1024:2048], in1=oo[:, 1024:2048], op=ALU.mult)
-        nc.vector.tensor_scalar(out=cb[:, 0:2048], in0=bm[:, 0:2048], scalar1=sm[:, 6:7], scalar2=None, op0=ALU.mult)
-        nc.vector.tensor_tensor(out=wsim[:, 0:2048], in0=cb[:, 0:2048], in1=aa[:, 0:2048], op=ALU.add)
-        nc.vector.quantize_mx(out=w_codes[:, 0:512].bitcast(FP8X4), scales=w_scales[:, 0:512], in_=wsim[:, 0:2048])
-        nc.scalar.copy(out=wsim[:, 3584:4096], in_=tl["wacc3"][:])
-        nc.vector.quantize_mx(out=w_codes[:, 512:1024].bitcast(FP8X4), scales=w_scales[:, 512:1024], in_=wsim[:, 2048:4096])
-        tl["o0"] = opool.tile([P, 4, NOUT], F32, name="o_sb")
-        tl["acc"] = psum.tile([P, 512], F32, name="acc4", tag="b4")
-        nc.tensor.matmul_mx(out=tl["acc"][:], lhsT=x_codes[:, 0, 0:128].bitcast(FP8X4), lhsT_scale=x_scales[:, 0, 0:128], rhs=w_codes[:, 0:512].bitcast(FP8X4), rhs_scale=w_scales[:, 0:512], start=True, stop=True)
-        nc.vector.tensor_tensor(out=tl["o0"][:, 0, 0:512], in0=tl["acc"][:], in1=bias_f[:, 0:512], op=ALU.add)
-        tl["acc"] = psum.tile([P, 512], F32, name="acc5", tag="b5")
-        nc.tensor.matmul_mx(out=tl["acc"][:], lhsT=x_codes[:, 0, 0:128].bitcast(FP8X4), lhsT_scale=x_scales[:, 0, 0:128], rhs=w_codes[:, 512:1024].bitcast(FP8X4), rhs_scale=w_scales[:, 512:1024], start=True, stop=True)
-        nc.vector.tensor_tensor(out=tl["o0"][:, 0, 512:1024], in0=tl["acc"][:], in1=bias_f[:, 512:1024], op=ALU.add)
-        nc.sync.dma_start(out=of[0 : 512, :].rearrange("(p t) n -> p t n", t=4)[:, 0, 0:1024], in_=tl["o0"][:, 0, 0:1024])
-        tl["acc"] = psum.tile([P, 512], F32, name="acc6", tag="b6")
-        nc.tensor.matmul_mx(out=tl["acc"][:], lhsT=x_codes[:, 0, 128:256].bitcast(FP8X4), lhsT_scale=x_scales[:, 0, 128:256], rhs=w_codes[:, 0:512].bitcast(FP8X4), rhs_scale=w_scales[:, 0:512], start=True, stop=True)
-        nc.scalar.copy(out=tl["o0"][:, 1, 0:512], in_=tl["acc"][:])
-        nc.gpsimd.tensor_tensor(out=tl["o0"][:, 1, 0:512], in0=tl["o0"][:, 1, 0:512], in1=bias_f[:, 0:512], op=ALU.add)
-        tl["acc"] = psum.tile([P, 512], F32, name="acc7", tag="b7")
-        nc.tensor.matmul_mx(out=tl["acc"][:], lhsT=x_codes[:, 0, 128:256].bitcast(FP8X4), lhsT_scale=x_scales[:, 0, 128:256], rhs=w_codes[:, 512:1024].bitcast(FP8X4), rhs_scale=w_scales[:, 512:1024], start=True, stop=True)
-        nc.vector.tensor_tensor(out=tl["o0"][:, 1, 512:1024], in0=tl["acc"][:], in1=bias_f[:, 512:1024], op=ALU.add)
-        nc.vector.quantize_mx(out=x_codes[:, 1, :].bitcast(FP8X4), scales=x_scales[:, 1, :], in_=tl["xg1"][:].rearrange("p t r v -> p (t r v)"))
-        nc.sync.dma_start(out=of[0 : 512, :].rearrange("(p t) n -> p t n", t=4)[:, 1, 0:1024], in_=tl["o0"][:, 1, 0:1024])
-        tl["acc"] = psum.tile([P, 512], F32, name="acc4", tag="b4")
-        nc.tensor.matmul_mx(out=tl["acc"][:], lhsT=x_codes[:, 0, 256:384].bitcast(FP8X4), lhsT_scale=x_scales[:, 0, 256:384], rhs=w_codes[:, 0:512].bitcast(FP8X4), rhs_scale=w_scales[:, 0:512], start=True, stop=True)
-        nc.scalar.copy(out=tl["o0"][:, 2, 0:512], in_=tl["acc"][:])
-        nc.gpsimd.tensor_tensor(out=tl["o0"][:, 2, 0:512], in0=tl["o0"][:, 2, 0:512], in1=bias_f[:, 0:512], op=ALU.add)
-        tl["acc"] = psum.tile([P, 512], F32, name="acc5", tag="b5")
-        nc.tensor.matmul_mx(out=tl["acc"][:], lhsT=x_codes[:, 0, 256:384].bitcast(FP8X4), lhsT_scale=x_scales[:, 0, 256:384], rhs=w_codes[:, 512:1024].bitcast(FP8X4), rhs_scale=w_scales[:, 512:1024], start=True, stop=True)
-        nc.vector.tensor_tensor(out=tl["o0"][:, 2, 512:1024], in0=tl["acc"][:], in1=bias_f[:, 512:1024], op=ALU.add)
-        nc.sync.dma_start(out=of[0 : 512, :].rearrange("(p t) n -> p t n", t=4)[:, 2, 0:1024], in_=tl["o0"][:, 2, 0:1024])
-        tl["acc"] = psum.tile([P, 512], F32, name="acc6", tag="b6")
-        nc.tensor.matmul_mx(out=tl["acc"][:], lhsT=x_codes[:, 0, 384:512].bitcast(FP8X4), lhsT_scale=x_scales[:, 0, 384:512], rhs=w_codes[:, 0:512].bitcast(FP8X4), rhs_scale=w_scales[:, 0:512], start=True, stop=True)
-        nc.vector.tensor_tensor(out=tl["o0"][:, 3, 0:512], in0=tl["acc"][:], in1=bias_f[:, 0:512], op=ALU.add)
-        tl["acc"] = psum.tile([P, 512], F32, name="acc7", tag="b7")
-        nc.tensor.matmul_mx(out=tl["acc"][:], lhsT=x_codes[:, 0, 384:512].bitcast(FP8X4), lhsT_scale=x_scales[:, 0, 384:512], rhs=w_codes[:, 512:1024].bitcast(FP8X4), rhs_scale=w_scales[:, 512:1024], start=True, stop=True)
-        nc.vector.tensor_tensor(out=tl["o0"][:, 3, 512:1024], in0=tl["acc"][:], in1=bias_f[:, 512:1024], op=ALU.add)
-        nc.sync.dma_start(out=of[0 : 512, :].rearrange("(p t) n -> p t n", t=4)[:, 3, 0:1024], in_=tl["o0"][:, 3, 0:1024])
-        for b in range(2):
-            tl["pt2_%d" % b] = psum.tile([P, 2, 2, P], F32, name="pt2_%d" % b, tag="b%d" % (2 + b))
-            for tt in range(2):
-                for u in range(2):
-                    nc.tensor.transpose(out=tl["pt2_%d" % b][:, tt, u, :], in_=x_sb[:, 2, 2 * b + tt, :].bitcast(F32)[:, u : 2 * P : 2], identity=ident[:])
-        tl["o1"] = opool.tile([P, 4, NOUT], F32, name="o_sb")
-        tl["acc"] = psum.tile([P, 512], F32, name="acc4", tag="b4")
-        nc.tensor.matmul_mx(out=tl["acc"][:], lhsT=x_codes[:, 1, 0:128].bitcast(FP8X4), lhsT_scale=x_scales[:, 1, 0:128], rhs=w_codes[:, 0:512].bitcast(FP8X4), rhs_scale=w_scales[:, 0:512], start=True, stop=True)
-        nc.scalar.copy(out=tl["o1"][:, 0, 0:512], in_=tl["acc"][:])
-        nc.gpsimd.tensor_tensor(out=tl["o1"][:, 0, 0:512], in0=tl["o1"][:, 0, 0:512], in1=bias_f[:, 0:512], op=ALU.add)
-        tl["acc"] = psum.tile([P, 512], F32, name="acc5", tag="b5")
-        nc.tensor.matmul_mx(out=tl["acc"][:], lhsT=x_codes[:, 1, 0:128].bitcast(FP8X4), lhsT_scale=x_scales[:, 1, 0:128], rhs=w_codes[:, 512:1024].bitcast(FP8X4), rhs_scale=w_scales[:, 512:1024], start=True, stop=True)
-        nc.vector.tensor_tensor(out=tl["o1"][:, 0, 512:1024], in0=tl["acc"][:], in1=bias_f[:, 512:1024], op=ALU.add)
-        tl["acc"] = psum.tile([P, 512], F32, name="acc6", tag="b6")
-        nc.tensor.matmul_mx(out=tl["acc"][:], lhsT=x_codes[:, 1, 128:256].bitcast(FP8X4), lhsT_scale=x_scales[:, 1, 128:256], rhs=w_codes[:, 0:512].bitcast(FP8X4), rhs_scale=w_scales[:, 0:512], start=True, stop=True)
-        nc.scalar.copy(out=tl["o1"][:, 1, 0:512], in_=tl["acc"][:])
-        nc.gpsimd.tensor_tensor(out=tl["o1"][:, 1, 0:512], in0=tl["o1"][:, 1, 0:512], in1=bias_f[:, 0:512], op=ALU.add)
-        tl["xg2"] = xgpool.tile([P, 4, P, 4], BF16, name="xg", align_bytes=64)
-        for b in range(2):
-            nc.scalar.copy(out=tl["xg2"][:].bitcast(F32)[:, 2 * b : 2 * b + 2, :, :], in_=tl["pt2_%d" % b][:].rearrange("p t u r -> p t r u"))
-        tl["acc"] = psum.tile([P, 512], F32, name="acc7", tag="b7")
-        nc.tensor.matmul_mx(out=tl["acc"][:], lhsT=x_codes[:, 1, 128:256].bitcast(FP8X4), lhsT_scale=x_scales[:, 1, 128:256], rhs=w_codes[:, 512:1024].bitcast(FP8X4), rhs_scale=w_scales[:, 512:1024], start=True, stop=True)
-        nc.vector.tensor_tensor(out=tl["o1"][:, 1, 512:1024], in0=tl["acc"][:], in1=bias_f[:, 512:1024], op=ALU.add)
-        nc.sync.dma_start(out=of[512 : 1024, :].rearrange("(p t) n -> p t n", t=4)[:, 0:2, 0:1024], in_=tl["o1"][:, 0:2, 0:1024])
-        tl["acc"] = psum.tile([P, 512], F32, name="acc4", tag="b4")
-        nc.tensor.matmul_mx(out=tl["acc"][:], lhsT=x_codes[:, 1, 256:384].bitcast(FP8X4), lhsT_scale=x_scales[:, 1, 256:384], rhs=w_codes[:, 0:512].bitcast(FP8X4), rhs_scale=w_scales[:, 0:512], start=True, stop=True)
-        nc.scalar.copy(out=tl["o1"][:, 2, 0:512], in_=tl["acc"][:])
-        nc.gpsimd.tensor_tensor(out=tl["o1"][:, 2, 0:512], in0=tl["o1"][:, 2, 0:512], in1=bias_f[:, 0:512], op=ALU.add)
-        tl["acc"] = psum.tile([P, 512], F32, name="acc5", tag="b5")
-        nc.tensor.matmul_mx(out=tl["acc"][:], lhsT=x_codes[:, 1, 256:384].bitcast(FP8X4), lhsT_scale=x_scales[:, 1, 256:384], rhs=w_codes[:, 512:1024].bitcast(FP8X4), rhs_scale=w_scales[:, 512:1024], start=True, stop=True)
-        nc.vector.tensor_tensor(out=tl["o1"][:, 2, 512:1024], in0=tl["acc"][:], in1=bias_f[:, 512:1024], op=ALU.add)
-        nc.vector.quantize_mx(out=x_codes[:, 2, :].bitcast(FP8X4), scales=x_scales[:, 2, :], in_=tl["xg2"][:].rearrange("p t r v -> p (t r v)"))
-        tl["acc"] = psum.tile([P, 512], F32, name="acc6", tag="b6")
-        nc.tensor.matmul_mx(out=tl["acc"][:], lhsT=x_codes[:, 1, 384:512].bitcast(FP8X4), lhsT_scale=x_scales[:, 1, 384:512], rhs=w_codes[:, 0:512].bitcast(FP8X4), rhs_scale=w_scales[:, 0:512], start=True, stop=True)
-        nc.vector.tensor_tensor(out=tl["o1"][:, 3, 0:512], in0=tl["acc"][:], in1=bias_f[:, 0:512], op=ALU.add)
-        tl["acc"] = psum.tile([P, 512], F32, name="acc7", tag="b7")
-        nc.tensor.matmul_mx(out=tl["acc"][:], lhsT=x_codes[:, 1, 384:512].bitcast(FP8X4), lhsT_scale=x_scales[:, 1, 384:512], rhs=w_codes[:, 512:1024].bitcast(FP8X4), rhs_scale=w_scales[:, 512:1024], start=True, stop=True)
-        nc.vector.tensor_tensor(out=tl["o1"][:, 3, 512:1024], in0=tl["acc"][:], in1=bias_f[:, 512:1024], op=ALU.add)
-        nc.sync.dma_start(out=of[512 : 1024, :].rearrange("(p t) n -> p t n", t=4)[:, 2:4, 0:1024], in_=tl["o1"][:, 2:4, 0:1024])
-        for b in range(2):
-            tl["pt3_%d" % b] = psum.tile([P, 2, 2, P], F32, name="pt3_%d" % b, tag="b%d" % (0 + b))
-            for tt in range(2):
-                for u in range(2):
-                    nc.tensor.transpose(out=tl["pt3_%d" % b][:, tt, u, :], in_=x_sb[:, 3, 2 * b + tt, :].bitcast(F32)[:, u : 2 * P : 2], identity=ident[:])
-        tl["o2"] = opool.tile([P, 4, NOUT], F32, name="o_sb")
-        tl["acc"] = psum.tile([P, 512], F32, name="acc4", tag="b4")
-        nc.tensor.matmul_mx(out=tl["acc"][:], lhsT=x_codes[:, 2, 0:128].bitcast(FP8X4), lhsT_scale=x_scales[:, 2, 0:128], rhs=w_codes[:, 0:512].bitcast(FP8X4), rhs_scale=w_scales[:, 0:512], start=True, stop=True)
-        nc.scalar.copy(out=tl["o2"][:, 0, 0:512], in_=tl["acc"][:])
-        nc.gpsimd.tensor_tensor(out=tl["o2"][:, 0, 0:512], in0=tl["o2"][:, 0, 0:512], in1=bias_f[:, 0:512], op=ALU.add)
-        tl["acc"] = psum.tile([P, 512], F32, name="acc5", tag="b5")
-        nc.tensor.matmul_mx(out=tl["acc"][:], lhsT=x_codes[:, 2, 0:128].bitcast(FP8X4), lhsT_scale=x_scales[:, 2, 0:128], rhs=w_codes[:, 512:1024].bitcast(FP8X4), rhs_scale=w_scales[:, 512:1024], start=True, stop=True)
-        nc.vector.tensor_tensor(out=tl["o2"][:, 0, 512:1024], in0=tl["acc"][:], in1=bias_f[:, 512:1024], op=ALU.add)
-        tl["acc"] = psum.tile([P, 512], F32, name="acc6", tag="b6")
-        nc.tensor.matmul_mx(out=tl["acc"][:], lhsT=x_codes[:, 2, 128:256].bitcast(FP8X4), lhsT_scale=x_scales[:, 2, 128:256], rhs=w_codes[:, 0:512].bitcast(FP8X4), rhs_scale=w_scales[:, 0:512], start=True, stop=True)
-        nc.scalar.copy(out=tl["o2"][:, 1, 0:512], in_=tl["acc"][:])
-        nc.gpsimd.tensor_tensor(out=tl["o2"][:, 1, 0:512], in0=tl["o2"][:, 1, 0:512], in1=bias_f[:, 0:512], op=ALU.add)
-        tl["xg3"] = xgpool.tile([P, 4, P, 4], BF16, name="xg", align_bytes=64)
-        for b in range(2):
-            nc.scalar.copy(out=tl["xg3"][:].bitcast(F32)[:, 2 * b : 2 * b + 2, :, :], in_=tl["pt3_%d" % b][:].rearrange("p t u r -> p t r u"))
-        tl["acc"] = psum.tile([P, 512], F32, name="acc7", tag="b7")
-        nc.tensor.matmul_mx(out=tl["acc"][:], lhsT=x_codes[:, 2, 128:256].bitcast(FP8X4), lhsT_scale=x_scales[:, 2, 128:256], rhs=w_codes[:, 512:1024].bitcast(FP8X4), rhs_scale=w_scales[:, 512:1024], start=True, stop=True)
-        nc.vector.tensor_tensor(out=tl["o2"][:, 1, 512:1024], in0=tl["acc"][:], in1=bias_f[:, 512:1024], op=ALU.add)
-        nc.sync.dma_start(out=of[1024 : 1536, :].rearrange("(p t) n -> p t n", t=4)[:, 0:2, 0:1024], in_=tl["o2"][:, 0:2, 0:1024])
-        tl["acc"] = psum.tile([P, 512], F32, name="acc4", tag="b4")
-        nc.tensor.matmul_mx(out=tl["acc"][:], lhsT=x_codes[:, 2, 256:384].bitcast(FP8X4), lhsT_scale=x_scales[:, 2, 256:384], rhs=w_codes[:, 0:512].bitcast(FP8X4), rhs_scale=w_scales[:, 0:512], start=True, stop=True)
-        nc.scalar.copy(out=tl["o2"][:, 2, 0:512], in_=tl["acc"][:])
-        nc.gpsimd.tensor_tensor(out=tl["o2"][:, 2, 0:512], in0=tl["o2"][:, 2, 0:512], in1=bias_f[:, 0:512], op=ALU.add)
-        tl["acc"] = psum.tile([P, 512], F32, name="acc5", tag="b5")
-        nc.tensor.matmul_mx(out=tl["acc"][:], lhsT=x_codes[:, 2, 256:384].bitcast(FP8X4), lhsT_scale=x_scales[:, 2, 256:384], rhs=w_codes[:, 512:1024].bitcast(FP8X4), rhs_scale=w_scales[:, 512:1024], start=True, stop=True)
-        nc.vector.tensor_tensor(out=tl["o2"][:, 2, 512:1024], in0=tl["acc"][:], in1=bias_f[:, 512:1024], op=ALU.add)
-        nc.vector.quantize_mx(out=x_codes[:, 3, :].bitcast(FP8X4), scales=x_scales[:, 3, :], in_=tl["xg3"][:].rearrange("p t r v -> p (t r v)"))
-        tl["acc"] = psum.tile([P, 512], F32, name="acc6", tag="b6")
-        nc.tensor.matmul_mx(out=tl["acc"][:], lhsT=x_codes[:, 2, 384:512].bitcast(FP8X4), lhsT_scale=x_scales[:, 2, 384:512], rhs=w_codes[:, 0:512].bitcast(FP8X4), rhs_scale=w_scales[:, 0:512], start=True, stop=True)
-        nc.vector.tensor_tensor(out=tl["o2"][:, 3, 0:512], in0=tl["acc"][:], in1=bias_f[:, 0:512], op=ALU.add)
-        tl["acc"] = psum.tile([P, 512], F32, name="acc7", tag="b7")
-        nc.tensor.matmul_mx(out=tl["acc"][:], lhsT=x_codes[:, 2, 384:512].bitcast(FP8X4), lhsT_scale=x_scales[:, 2, 384:512], rhs=w_codes[:, 512:1024].bitcast(FP8X4), rhs_scale=w_scales[:, 512:1024], start=True, stop=True)
-        nc.vector.tensor_tensor(out=tl["o2"][:, 3, 512:1024], in0=tl["acc"][:], in1=bias_f[:, 512:1024], op=ALU.add)
-        nc.sync.dma_start(out=of[1024 : 1536, :].rearrange("(p t) n -> p t n", t=4)[:, 2:4, 0:1024], in_=tl["o2"][:, 2:4, 0:1024])
-        for b in range(2):
-            tl["pt4_%d" % b] = psum.tile([P, 2, 2, P], F32, name="pt4_%d" % b, tag="b%d" % (2 + b))
-            for tt in range(2):
-                for u in range(2):
-                    nc.tensor.transpose(out=tl["pt4_%d" % b][:, tt, u, :], in_=x_sb[:, 4, 2 * b + tt, :].bitcast(F32)[:, u : 2 * P : 2], identity=ident[:])
-        tl["o3"] = opool.tile([P, 4, NOUT], F32, name="o_sb")
-        tl["acc"] = psum.tile([P, 512], F32, name="acc4", tag="b4")
-        nc.tensor.matmul_mx(out=tl["acc"][:], lhsT=x_codes[:, 3, 0:128].bitcast(FP8X4), lhsT_scale=x_scales[:, 3, 0:128], rhs=w_codes[:, 0:512].bitcast(FP8X4), rhs_scale=w_scales[:, 0:512], start=True, stop=True)
-        nc.scalar.copy(out=tl["o3"][:, 0, 0:512], in_=tl["acc"][:])
-        nc.gpsimd.tensor_tensor(out=tl["o3"][:, 0, 0:512], in0=tl["o3"][:, 0, 0:512], in1=bias_f[:, 0:512], op=ALU.add)
-        tl["acc"] = psum.tile([P, 512], F32, name="acc5", tag="b5")
-        nc.tensor.matmul_mx(out=tl["acc"][:], lhsT=x_codes[:, 3, 0:128].bitcast(FP8X4), lhsT_scale=x_scales[:, 3, 0:128], rhs=w_codes[:, 512:1024].bitcast(FP8X4), rhs_scale=w_scales[:, 512:1024], start=True, stop=True)
-        nc.vector.tensor_tensor(out=tl["o3"][:, 0, 512:1024], in0=tl["acc"][:], in1=bias_f[:, 512:1024], op=ALU.add)
-        tl["acc"] = psum.tile([P, 512], F32, name="acc6", tag="b6")
-        nc.tensor.matmul_mx(out=tl["acc"][:], lhsT=x_codes[:, 3, 128:256].bitcast(FP8X4), lhsT_scale=x_scales[:, 3, 128:256], rhs=w_codes[:, 0:512].bitcast(FP8X4), rhs_scale=w_scales[:, 0:512], start=True, stop=True)
-        nc.scalar.copy(out=tl["o3"][:, 1, 0:512], in_=tl["acc"][:])
-        nc.gpsimd.tensor_tensor(out=tl["o3"][:, 1, 0:512], in0=tl["o3"][:, 1, 0:512], in1=bias_f[:, 0:512], op=ALU.add)
-        tl["xg4"] = xgpool.tile([P, 4, P, 4], BF16, name="xg", align_bytes=64)
-        for b in range(2):
-            nc.scalar.copy(out=tl["xg4"][:].bitcast(F32)[:, 2 * b : 2 * b + 2, :, :], in_=tl["pt4_%d" % b][:].rearrange("p t u r -> p t r u"))
-        tl["acc"] = psum.tile([P, 512], F32, name="acc7", tag="b7")
-        nc.tensor.matmul_mx(out=tl["acc"][:], lhsT=x_codes[:, 3, 128:256].bitcast(FP8X4), lhsT_scale=x_scales[:, 3, 128:256], rhs=w_codes[:, 512:1024].bitcast(FP8X4), rhs_scale=w_scales[:, 512:1024], start=True, stop=True)
-        nc.vector.tensor_tensor(out=tl["o3"][:, 1, 512:1024], in0=tl["acc"][:], in1=bias_f[:, 512:1024], op=ALU.add)
-        tl["acc"] = psum.tile([P, 512], F32, name="acc4", tag="b4")
-        nc.tensor.matmul_mx(out=tl["acc"][:], lhsT=x_codes[:, 3, 256:384].bitcast(FP8X4), lhsT_scale=x_scales[:, 3, 256:384], rhs=w_codes[:, 0:512].bitcast(FP8X4), rhs_scale=w_scales[:, 0:512], start=True, stop=True)
-        nc.scalar.copy(out=tl["o3"][:, 2, 0:512], in_=tl["acc"][:])
-        nc.gpsimd.tensor_tensor(out=tl["o3"][:, 2, 0:512], in0=tl["o3"][:, 2, 0:512], in1=bias_f[:, 0:512], op=ALU.add)
-        tl["acc"] = psum.tile([P, 512], F32, name="acc5", tag="b5")
-        nc.tensor.matmul_mx(out=tl["acc"][:], lhsT=x_codes[:, 3, 256:384].bitcast(FP8X4), lhsT_scale=x_scales[:, 3, 256:384], rhs=w_codes[:, 512:1024].bitcast(FP8X4), rhs_scale=w_scales[:, 512:1024], start=True, stop=True)
-        nc.vector.tensor_tensor(out=tl["o3"][:, 2, 512:1024], in0=tl["acc"][:], in1=bias_f[:, 512:1024], op=ALU.add)
-        nc.vector.quantize_mx(out=x_codes[:, 4, :].bitcast(FP8X4), scales=x_scales[:, 4, :], in_=tl["xg4"][:].rearrange("p t r v -> p (t r v)"))
-        tl["acc"] = psum.tile([P, 512], F32, name="acc6", tag="b6")
-        nc.tensor.matmul_mx(out=tl["acc"][:], lhsT=x_codes[:, 3, 384:512].bitcast(FP8X4), lhsT_scale=x_scales[:, 3, 384:512], rhs=w_codes[:, 0:512].bitcast(FP8X4), rhs_scale=w_scales[:, 0:512], start=True, stop=True)
-        nc.vector.tensor_tensor(out=tl["o3"][:, 3, 0:512], in0=tl["acc"][:], in1=bias_f[:, 0:512], op=ALU.add)
-        tl["acc"] = psum.tile([P, 512], F32, name="acc7", tag="b7")
-        nc.tensor.matmul_mx(out=tl["acc"][:], lhsT=x_codes[:, 3, 384:512].bitcast(FP8X4), lhsT_scale=x_scales[:, 3, 384:512], rhs=w_codes[:, 512:1024].bitcast(FP8X4), rhs_scale=w_scales[:, 512:1024], start=True, stop=True)
-        nc.vector.tensor_tensor(out=tl["o3"][:, 3, 512:1024], in0=tl["acc"][:], in1=bias_f[:, 512:1024], op=ALU.add)
-        nc.sync.dma_start(out=of[1536 : 2048, :].rearrange("(p t) n -> p t n", t=4)[:, 0:4, 0:1024], in_=tl["o3"][:, 0:4, 0:1024])
-        for b in range(2):
-            tl["pt5_%d" % b] = psum.tile([P, 2, 2, P], F32, name="pt5_%d" % b, tag="b%d" % (0 + b))
-            for tt in range(2):
-                for u in range(2):
-                    nc.tensor.transpose(out=tl["pt5_%d" % b][:, tt, u, :], in_=x_sb[:, 5, 2 * b + tt, :].bitcast(F32)[:, u : 2 * P : 2], identity=ident[:])
-        tl["o4"] = opool.tile([P, 4, NOUT], F32, name="o_sb")
-        tl["acc"] = psum.tile([P, 512], F32, name="acc4", tag="b4")
-        nc.tensor.matmul_mx(out=tl["acc"][:], lhsT=x_codes[:, 4, 0:128].bitcast(FP8X4), lhsT_scale=x_scales[:, 4, 0:128], rhs=w_codes[:, 0:512].bitcast(FP8X4), rhs_scale=w_scales[:, 0:512], start=True, stop=True)
-        nc.scalar.copy(out=tl["o4"][:, 0, 0:512], in_=tl["acc"][:])
-        nc.gpsimd.tensor_tensor(out=tl["o4"][:, 0, 0:512], in0=tl["o4"][:, 0, 0:512], in1=bias_f[:, 0:512], op=ALU.add)
-        tl["acc"] = psum.tile([P, 512], F32, name="acc5", tag="b5")
-        nc.tensor.matmul_mx(out=tl["acc"][:], lhsT=x_codes[:, 4, 0:128].bitcast(FP8X4), lhsT_scale=x_scales[:, 4, 0:128], rhs=w_codes[:, 512:1024].bitcast(FP8X4), rhs_scale=w_scales[:, 512:1024], start=True, stop=True)
-        nc.vector.tensor_tensor(out=tl["o4"][:, 0, 512:1024], in0=tl["acc"][:], in1=bias_f[:, 512:1024], op=ALU.add)
-        tl["acc"] = psum.tile([P, 512], F32, name="acc6", tag="b6")
-        nc.tensor.matmul_mx(out=tl["acc"][:], lhsT=x_codes[:, 4, 128:256].bitcast(FP8X4), lhsT_scale=x_scales[:, 4, 128:256], rhs=w_codes[:, 0:512].bitcast(FP8X4), rhs_scale=w_scales[:, 0:512], start=True, stop=True)
-        nc.scalar.copy(out=tl["o4"][:, 1, 0:512], in_=tl["acc"][:])
-        nc.gpsimd.tensor_tensor(out=tl["o4"][:, 1, 0:512], in0=tl["o4"][:, 1, 0:512], in1=bias_f[:, 0:512], op=ALU.add)
-        tl["xg5"] = xgpool.tile([P, 4, P, 4], BF16, name="xg", align_bytes=64)
-        for b in range(2):
-            nc.scalar.copy(out=tl["xg5"][:].bitcast(F32)[:, 2 * b : 2 * b + 2, :, :], in_=tl["pt5_%d" % b][:].rearrange("p t u r -> p t r u"))
-        tl["acc"] = psum.tile([P, 512], F32, name="acc7", tag="b7")
-        nc.tensor.matmul_mx(out=tl["acc"][:], lhsT=x_codes[:, 4, 128:256].bitcast(FP8X4), lhsT_scale=x_scales[:, 4, 128:256], rhs=w_codes[:, 512:1024].bitcast(FP8X4), rhs_scale=w_scales[:, 512:1024], start=True, stop=True)
-        nc.vector.tensor_tensor(out=tl["o4"][:, 1, 512:1024], in0=tl["acc"][:], in1=bias_f[:, 512:1024], op=ALU.add)
-        tl["acc"] = psum.tile([P, 512], F32, name="acc4", tag="b4")
-        nc.tensor.matmul_mx(out=tl["acc"][:], lhsT=x_codes[:, 4, 256:384].bitcast(FP8X4), lhsT_scale=x_scales[:, 4, 256:384], rhs=w_codes[:, 0:512].bitcast(FP8X4), rhs_scale=w_scales[:, 0:512], start=True, stop=True)
-        nc.scalar.copy(out=tl["o4"][:, 2, 0:512], in_=tl["acc"][:])
-        nc.gpsimd.tensor_tensor(out=tl["o4"][:, 2, 0:512], in0=tl["o4"][:, 2, 0:512], in1=bias_f[:, 0:512], op=ALU.add)
-        tl["acc"] = psum.tile([P, 512], F32, name="acc5", tag="b5")
-        nc.tensor.matmul_mx(out=tl["acc"][:], lhsT=x_codes[:, 4, 256:384].bitcast(FP8X4), lhsT_scale=x_scales[:, 4, 256:384], rhs=w_codes[:, 512:1024].bitcast(FP8X4), rhs_scale=w_scales[:, 512:1024], start=True, stop=True)
-        nc.vector.tensor_tensor(out=tl["o4"][:, 2, 512:1024], in0=tl["acc"][:], in1=bias_f[:, 512:1024], op=ALU.add)
-        nc.vector.quantize_mx(out=x_codes[:, 5, :].bitcast(FP8X4), scales=x_scales[:, 5, :], in_=tl["xg5"][:].rearrange("p t r v -> p (t r v)"))
-        tl["acc"] = psum.tile([P, 512], F32, name="acc6", tag="b6")
-        nc.tensor.matmul_mx(out=tl["acc"][:], lhsT=x_codes[:, 4, 384:512].bitcast(FP8X4), lhsT_scale=x_scales[:, 4, 384:512], rhs=w_codes[:, 0:512].bitcast(FP8X4), rhs_scale=w_scales[:, 0:512], start=True, stop=True)
-        nc.vector.tensor_tensor(out=tl["o4"][:, 3, 0:512], in0=tl["acc"][:], in1=bias_f[:, 0:512], op=ALU.add)
-        tl["acc"] = psum.tile([P, 512], F32, name="acc7", tag="b7")
-        nc.tensor.matmul_mx(out=tl["acc"][:], lhsT=x_codes[:, 4, 384:512].bitcast(FP8X4), lhsT_scale=x_scales[:, 4, 384:512], rhs=w_codes[:, 512:1024].bitcast(FP8X4), rhs_scale=w_scales[:, 512:1024], start=True, stop=True)
-        nc.vector.tensor_tensor(out=tl["o4"][:, 3, 512:1024], in0=tl["acc"][:], in1=bias_f[:, 512:1024], op=ALU.add)
-        nc.sync.dma_start(out=of[2048 : 2560, :].rearrange("(p t) n -> p t n", t=4)[:, 0:4, 0:1024], in_=tl["o4"][:, 0:4, 0:1024])
-        for b in range(2):
-            tl["pt6_%d" % b] = psum.tile([P, 2, 2, P], F32, name="pt6_%d" % b, tag="b%d" % (2 + b))
-            for tt in range(2):
-                for u in range(2):
-                    nc.tensor.transpose(out=tl["pt6_%d" % b][:, tt, u, :], in_=x_sb[:, 6, 2 * b + tt, :].bitcast(F32)[:, u : 2 * P : 2], identity=ident[:])
-        tl["o5"] = opool.tile([P, 4, NOUT], F32, name="o_sb")
-        tl["acc"] = psum.tile([P, 512], F32, name="acc4", tag="b4")
-        nc.tensor.matmul_mx(out=tl["acc"][:], lhsT=x_codes[:, 5, 0:128].bitcast(FP8X4), lhsT_scale=x_scales[:, 5, 0:128], rhs=w_codes[:, 0:512].bitcast(FP8X4), rhs_scale=w_scales[:, 0:512], start=True, stop=True)
-        nc.scalar.copy(out=tl["o5"][:, 0, 0:512], in_=tl["acc"][:])
-        nc.gpsimd.tensor_tensor(out=tl["o5"][:, 0, 0:512], in0=tl["o5"][:, 0, 0:512], in1=bias_f[:, 0:512], op=ALU.add)
-        tl["acc"] = psum.tile([P, 512], F32, name="acc5", tag="b5")
-        nc.tensor.matmul_mx(out=tl["acc"][:], lhsT=x_codes[:, 5, 0:128].bitcast(FP8X4), lhsT_scale=x_scales[:, 5, 0:128], rhs=w_codes[:, 512:1024].bitcast(FP8X4), rhs_scale=w_scales[:, 512:1024], start=True, stop=True)
-        nc.vector.tensor_tensor(out=tl["o5"][:, 0, 512:1024], in0=tl["acc"][:], in1=bias_f[:, 512:1024], op=ALU.add)
-        tl["acc"] = psum.tile([P, 512], F32, name="acc6", tag="b6")
-        nc.tensor.matmul_mx(out=tl["acc"][:], lhsT=x_codes[:, 5, 128:256].bitcast(FP8X4), lhsT_scale=x_scales[:, 5, 128:256], rhs=w_codes[:, 0:512].bitcast(FP8X4), rhs_scale=w_scales[:, 0:512], start=True, stop=True)
-        nc.scalar.copy(out=tl["o5"][:, 1, 0:512], in_=tl["acc"][:])
-        nc.gpsimd.tensor_tensor(out=tl["o5"][:, 1, 0:512], in0=tl["o5"][:, 1, 0:512], in1=bias_f[:, 0:512], op=ALU.add)
-        tl["xg6"] = xgpool.tile([P, 4, P, 4], BF16, name="xg", align_bytes=64)
-        for b in range(2):
-            nc.scalar.copy(out=tl["xg6"][:].bitcast(F32)[:, 2 * b : 2 * b + 2, :, :], in_=tl["pt6_%d" % b][:].rearrange("p t u r -> p t r u"))
-        tl["acc"] = psum.tile([P, 512], F32, name="acc7", tag="b7")
-        nc.tensor.matmul_mx(out=tl["acc"][:], lhsT=x_codes[:, 5, 128:256].bitcast(FP8X4), lhsT_scale=x_scales[:, 5, 128:256], rhs=w_codes[:, 512:1024].bitcast(FP8X4), rhs_scale=w_scales[:, 512:1024], start=True, stop=True)
-        nc.vector.tensor_tensor(out=tl["o5"][:, 1, 512:1024], in0=tl["acc"][:], in1=bias_f[:, 512:1024], op=ALU.add)
-        tl["acc"] = psum.tile([P, 512], F32, name="acc4", tag="b4")
-        nc.tensor.matmul_mx(out=tl["acc"][:], lhsT=x_codes[:, 5, 256:384].bitcast(FP8X4), lhsT_scale=x_scales[:, 5, 256:384], rhs=w_codes[:, 0:512].bitcast(FP8X4), rhs_scale=w_scales[:, 0:512], start=True, stop=True)
-        nc.scalar.copy(out=tl["o5"][:, 2, 0:512], in_=tl["acc"][:])
-        nc.gpsimd.tensor_tensor(out=tl["o5"][:, 2, 0:512], in0=tl["o5"][:, 2, 0:512], in1=bias_f[:, 0:512], op=ALU.add)
-        tl["acc"] = psum.tile([P, 512], F32, name="acc5", tag="b5")
-        nc.tensor.matmul_mx(out=tl["acc"][:], lhsT=x_codes[:, 5, 256:384].bitcast(FP8X4), lhsT_scale=x_scales[:, 5, 256:384], rhs=w_codes[:, 512:1024].bitcast(FP8X4), rhs_scale=w_scales[:, 512:1024], start=True, stop=True)
-        nc.vector.tensor_tensor(out=tl["o5"][:, 2, 512:1024], in0=tl["acc"][:], in1=bias_f[:, 512:1024], op=ALU.add)
-        nc.vector.quantize_mx(out=x_codes[:, 6, :].bitcast(FP8X4), scales=x_scales[:, 6, :], in_=tl["xg6"][:].rearrange("p t r v -> p (t r v)"))
-        tl["acc"] = psum.tile([P, 512], F32, name="acc6", tag="b6")
-        nc.tensor.matmul_mx(out=tl["acc"][:], lhsT=x_codes[:, 5, 384:512].bitcast(FP8X4), lhsT_scale=x_scales[:, 5, 384:512], rhs=w_codes[:, 0:512].bitcast(FP8X4), rhs_scale=w_scales[:, 0:512], start=True, stop=True)
-        nc.vector.tensor_tensor(out=tl["o5"][:, 3, 0:512], in0=tl["acc"][:], in1=bias_f[:, 0:512], op=ALU.add)
-        tl["acc"] = psum.tile([P, 512], F32, name="acc7", tag="b7")
-        nc.tensor.matmul_mx(out=tl["acc"][:], lhsT=x_codes[:, 5, 384:512].bitcast(FP8X4), lhsT_scale=x_scales[:, 5, 384:512], rhs=w_codes[:, 512:1024].bitcast(FP8X4), rhs_scale=w_scales[:, 512:1024], start=True, stop=True)
-        nc.vector.tensor_tensor(out=tl["o5"][:, 3, 512:1024], in0=tl["acc"][:], in1=bias_f[:, 512:1024], op=ALU.add)
-        nc.sync.dma_start(out=of[2560 : 3072, :].rearrange("(p t) n -> p t n", t=4)[:, 0:4, 0:1024], in_=tl["o5"][:, 0:4, 0:1024])
-        for b in range(2):
-            tl["pt7_%d" % b] = psum.tile([P, 2, 2, P], F32, name="pt7_%d" % b, tag="b%d" % (0 + b))
-            for tt in range(2):
-                for u in range(2):
-                    nc.tensor.transpose(out=tl["pt7_%d" % b][:, tt, u, :], in_=x_sb[:, 7, 2 * b + tt, :].bitcast(F32)[:, u : 2 * P : 2], identity=ident[:])
-        tl["o6"] = opool.tile([P, 4, NOUT], F32, name="o_sb")
-        tl["acc"] = psum.tile([P, 512], F32, name="acc4", tag="b4")
-        nc.tensor.matmul_mx(out=tl["acc"][:], lhsT=x_codes[:, 6, 0:128].bitcast(FP8X4), lhsT_scale=x_scales[:, 6, 0:128], rhs=w_codes[:, 0:512].bitcast(FP8X4), rhs_scale=w_scales[:, 0:512], start=True, stop=True)
-        nc.scalar.copy(out=tl["o6"][:, 0, 0:512], in_=tl["acc"][:])
-        nc.gpsimd.tensor_tensor(out=tl["o6"][:, 0, 0:512], in0=tl["o6"][:, 0, 0:512], in1=bias_f[:, 0:512], op=ALU.add)
-        tl["acc"] = psum.tile([P, 512], F32, name="acc5", tag="b5")
-        nc.tensor.matmul_mx(out=tl["acc"][:], lhsT=x_codes[:, 6, 0:128].bitcast(FP8X4), lhsT_scale=x_scales[:, 6, 0:128], rhs=w_codes[:, 512:1024].bitcast(FP8X4), rhs_scale=w_scales[:, 512:1024], start=True, stop=True)
-        nc.vector.tensor_tensor(out=tl["o6"][:, 0, 512:1024], in0=tl["acc"][:], in1=bias_f[:, 512:1024], op=ALU.add)
-        tl["acc"] = psum.tile([P, 512], F32, name="acc6", tag="b6")
-        nc.tensor.matmul_mx(out=tl["acc"][:], lhsT=x_codes[:, 6, 128:256].bitcast(FP8X4), lhsT_scale=x_scales[:, 6, 128:256], rhs=w_codes[:, 0:512].bitcast(FP8X4), rhs_scale=w_scales[:, 0:512], start=True, stop=True)
-        nc.scalar.copy(out=tl["o6"][:, 1, 0:512], in_=tl["acc"][:])
-        nc.gpsimd.tensor_tensor(out=tl["o6"][:, 1, 0:512], in0=tl["o6"][:, 1, 0:512], in1=bias_f[:, 0:512], op=ALU.add)
-        tl["xg7"] = xgpool.tile([P, 4, P, 4], BF16, name="xg", align_bytes=64)
-        for b in range(2):
-            nc.scalar.copy(out=tl["xg7"][:].bitcast(F32)[:, 2 * b : 2 * b + 2, :, :], in_=tl["pt7_%d" % b][:].rearrange("p t u r -> p t r u"))
-        tl["acc"] = psum.tile([P, 512], F32, name="acc7", tag="b7")
-        nc.tensor.matmul_mx(out=tl["acc"][:], lhsT=x_codes[:, 6, 128:256].bitcast(FP8X4), lhsT_scale=x_scales[:, 6, 128:256], rhs=w_codes[:, 512:1024].bitcast(FP8X4), rhs_scale=w_scales[:, 512:1024], start=True, stop=True)
-        nc.vector.tensor_tensor(out=tl["o6"][:, 1, 512:1024], in0=tl["acc"][:], in1=bias_f[:, 512:1024], op=ALU.add)
-        tl["acc"] = psum.tile([P, 512], F32, name="acc4", tag="b4")
-        nc.tensor.matmul_mx(out=tl["acc"][:], lhsT=x_codes[:, 6, 256:384].bitcast(FP8X4), lhsT_scale=x_scales[:, 6, 256:384], rhs=w_codes[:, 0:512].bitcast(FP8X4), rhs_scale=w_scales[:, 0:512], start=True, stop=True)
-        nc.scalar.copy(out=tl["o6"][:, 2, 0:512], in_=tl["acc"][:])
-        nc.gpsimd.tensor_tensor(out=tl["o6"][:, 2, 0:512], in0=tl["o6"][:, 2, 0:512], in1=bias_f[:, 0:512], op=ALU.add)
-        tl["acc"] = psum.tile([P, 512], F32, name="acc5", tag="b5")
-        nc.tensor.matmul_mx(out=tl["acc"][:], lhsT=x_codes[:, 6, 256:384].bitcast(FP8X4), lhsT_scale=x_scales[:, 6, 256:384], rhs=w_codes[:, 512:1024].bitcast(FP8X4), rhs_scale=w_scales[:, 512:1024], start=True, stop=True)
-        nc.vector.tensor_tensor(out=tl["o6"][:, 2, 512:1024], in0=tl["acc"][:], in1=bias_f[:, 512:1024], op=ALU.add)
-        nc.vector.quantize_mx(out=x_codes[:, 7, :].bitcast(FP8X4), scales=x_scales[:, 7, :], in_=tl["xg7"][:].rearrange("p t r v -> p (t r v)"))
-        tl["acc"] = psum.tile([P, 512], F32, name="acc6", tag="b6")
-        nc.tensor.matmul_mx(out=tl["acc"][:], lhsT=x_codes[:, 6, 384:512].bitcast(FP8X4), lhsT_scale=x_scales[:, 6, 384:512], rhs=w_codes[:, 0:512].bitcast(FP8X4), rhs_scale=w_scales[:, 0:512], start=True, stop=True)
-        nc.vector.tensor_tensor(out=tl["o6"][:, 3, 0:512], in0=tl["acc"][:], in1=bias_f[:, 0:512], op=ALU.add)
-        tl["acc"] = psum.tile([P, 512], F32, name="acc7", tag="b7")
-        nc.tensor.matmul_mx(out=tl["acc"][:], lhsT=x_codes[:, 6, 384:512].bitcast(FP8X4), lhsT_scale=x_scales[:, 6, 384:512], rhs=w_codes[:, 512:1024].bitcast(FP8X4), rhs_scale=w_scales[:, 512:1024], start=True, stop=True)
-        nc.vector.tensor_tensor(out=tl["o6"][:, 3, 512:1024], in0=tl["acc"][:], in1=bias_f[:, 512:1024], op=ALU.add)
-        nc.sync.dma_start(out=of[3072 : 3584, :].rearrange("(p t) n -> p t n", t=4)[:, 0:4, 0:1024], in_=tl["o6"][:, 0:4, 0:1024])
-        tl["o7"] = opool.tile([P, 4, NOUT], F32, name="o_sb")
-        tl["acc"] = psum.tile([P, 512], F32, name="acc4", tag="b4")
-        nc.tensor.matmul_mx(out=tl["acc"][:], lhsT=x_codes[:, 7, 0:128].bitcast(FP8X4), lhsT_scale=x_scales[:, 7, 0:128], rhs=w_codes[:, 0:512].bitcast(FP8X4), rhs_scale=w_scales[:, 0:512], start=True, stop=True)
-        nc.scalar.copy(out=tl["o7"][:, 0, 0:512], in_=tl["acc"][:])
-        nc.gpsimd.tensor_tensor(out=tl["o7"][:, 0, 0:512], in0=tl["o7"][:, 0, 0:512], in1=bias_f[:, 0:512], op=ALU.add)
-        tl["acc"] = psum.tile([P, 512], F32, name="acc5", tag="b5")
-        nc.tensor.matmul_mx(out=tl["acc"][:], lhsT=x_codes[:, 7, 0:128].bitcast(FP8X4), lhsT_scale=x_scales[:, 7, 0:128], rhs=w_codes[:, 512:1024].bitcast(FP8X4), rhs_scale=w_scales[:, 512:1024], start=True, stop=True)
-        nc.vector.tensor_tensor(out=tl["o7"][:, 0, 512:1024], in0=tl["acc"][:], in1=bias_f[:, 512:1024], op=ALU.add)
-        nc.sync.dma_start(out=of[3584 : 4096, :].rearrange("(p t) n -> p t n", t=4)[:, 0, 0:1024], in_=tl["o7"][:, 0, 0:1024])
-        tl["acc"] = psum.tile([P, 512], F32, name="acc6", tag="b6")
-        nc.tensor.matmul_mx(out=tl["acc"][:], lhsT=x_codes[:, 7, 128:256].bitcast(FP8X4), lhsT_scale=x_scales[:, 7, 128:256], rhs=w_codes[:, 0:512].bitcast(FP8X4), rhs_scale=w_scales[:, 0:512], start=True, stop=True)
-        nc.scalar.copy(out=tl["o7"][:, 1, 0:512], in_=tl["acc"][:])
-        nc.gpsimd.tensor_tensor(out=tl["o7"][:, 1, 0:512], in0=tl["o7"][:, 1, 0:512], in1=bias_f[:, 0:512], op=ALU.add)
-        tl["acc"] = psum.tile([P, 512], F32, name="acc7", tag="b7")
-        nc.tensor.matmul_mx(out=tl["acc"][:], lhsT=x_codes[:, 7, 128:256].bitcast(FP8X4), lhsT_scale=x_scales[:, 7, 128:256], rhs=w_codes[:, 512:1024].bitcast(FP8X4), rhs_scale=w_scales[:, 512:1024], start=True, stop=True)
-        nc.vector.tensor_tensor(out=tl["o7"][:, 1, 512:1024], in0=tl["acc"][:], in1=bias_f[:, 512:1024], op=ALU.add)
-        nc.sync.dma_start(out=of[3584 : 4096, :].rearrange("(p t) n -> p t n", t=4)[:, 1, 0:1024], in_=tl["o7"][:, 1, 0:1024])
-        tl["acc"] = psum.tile([P, 512], F32, name="acc4", tag="b4")
-        nc.tensor.matmul_mx(out=tl["acc"][:], lhsT=x_codes[:, 7, 256:384].bitcast(FP8X4), lhsT_scale=x_scales[:, 7, 256:384], rhs=w_codes[:, 0:512].bitcast(FP8X4), rhs_scale=w_scales[:, 0:512], start=True, stop=True)
-        nc.scalar.copy(out=tl["o7"][:, 2, 0:512], in_=tl["acc"][:])
-        nc.gpsimd.tensor_tensor(out=tl["o7"][:, 2, 0:512], in0=tl["o7"][:, 2, 0:512], in1=bias_f[:, 0:512], op=ALU.add)
-        tl["acc"] = psum.tile([P, 512], F32, name="acc5", tag="b5")
-        nc.tensor.matmul_mx(out=tl["acc"][:], lhsT=x_codes[:, 7, 256:384].bitcast(FP8X4), lhsT_scale=x_scales[:, 7, 256:384], rhs=w_codes[:, 512:1024].bitcast(FP8X4), rhs_scale=w_scales[:, 512:1024], start=True, stop=True)
-        nc.vector.tensor_tensor(out=tl["o7"][:, 2, 512:1024], in0=tl["acc"][:], in1=bias_f[:, 512:1024], op=ALU.add)
-        nc.sync.dma_start(out=of[3584 : 4096, :].rearrange("(p t) n -> p t n", t=4)[:, 2, 0:1024], in_=tl["o7"][:, 2, 0:1024])
-        tl["acc"] = psum.tile([P, 512], F32, name="acc6", tag="b6")
-        nc.tensor.matmul_mx(out=tl["acc"][:], lhsT=x_codes[:, 7, 384:512].bitcast(FP8X4), lhsT_scale=x_scales[:, 7, 384:512], rhs=w_codes[:, 0:512].bitcast(FP8X4), rhs_scale=w_scales[:, 0:512], start=True, stop=True)
-        nc.vector.tensor_tensor(out=tl["o7"][:, 3, 0:512], in0=tl["acc"][:], in1=bias_f[:, 0:512], op=ALU.add)
-        tl["acc"] = psum.tile([P, 512], F32, name="acc7", tag="b7")
-        nc.tensor.matmul_mx(out=tl["acc"][:], lhsT=x_codes[:, 7, 384:512].bitcast(FP8X4), lhsT_scale=x_scales[:, 7, 384:512], rhs=w_codes[:, 512:1024].bitcast(FP8X4), rhs_scale=w_scales[:, 512:1024], start=True, stop=True)
-        nc.vector.tensor_tensor(out=tl["o7"][:, 3, 512:1024], in0=tl["acc"][:], in1=bias_f[:, 512:1024], op=ALU.add)
-        nc.sync.dma_start(out=of[3584 : 4096, :].rearrange("(p t) n -> p t n", t=4)[:, 3, 0:1024], in_=tl["o7"][:, 3, 0:1024])
+            nc.tensor.matmul(out=wacc[b][:], lhsT=ident_bf[:], rhs=aa[:, cols(4 + b, 512)], start=True, stop=False)
+        x_quant(0, xg0)
+        outliers(3)
+        nc.vector.tensor_copy(out=st2[:, 1:2], in_=ck[:])
+        nc.vector.scalar_tensor_tensor(out=junk_d[:], in0=gram[:], scalar=1.0, in1=ident[:], op0=ALU.mult, op1=ALU.mult, accum_out=st2[:, 0:1])
+        l2b = psum.tile([P, 2], F32, name="l2b", tag="b7")
+        nc.tensor.matmul(out=l2b[:], lhsT=ones_f[:], rhs=st2[:], start=True, stop=True)
+        for b in range(2, 4):
+            nc.tensor.matmul(out=wacc[b][:], lhsT=ident_bf[:], rhs=aa[:, cols(4 + b, 512)], start=True, stop=False)
+        outlier_mask(1, True)
+        outliers(0)
+        nc.vector.reciprocal(out=rc[:], in_=l2b[:, 1:2])
+        nc.vector.tensor_scalar(out=c_ident[:], in0=ident_bf[:], scalar1=l2b[:, 0:1], scalar2=rc[:], op0=ALU.mult, op1=ALU.mult)
+        for b in range(4):
+            nc.tensor.matmul(out=wacc[b][:], lhsT=c_ident[:], rhs=bm[:, cols(4 + b, 512)], start=False, stop=True)
+        for b in range(4):
+            nc.scalar.copy(out=wsim[:, cols(4 + b, 512)], in_=wacc[b][:])
+        nc.vector.tensor_scalar(out=cb[:], in0=bm[:, 0:2048], scalar1=l2b[:, 0:1], scalar2=rc[:], op0=ALU.mult, op1=ALU.mult)
+        outliers(1)
+        nc.vector.tensor_tensor(out=wsim[:, 0:1024], in0=cb[:, 0:1024], in1=aa[:, 0:1024], op=ALU.add)
+        nc.vector.tensor_tensor(out=wsim[:, 1024:2048], in0=cb[:, 1024:2048], in1=aa[:, 1024:2048], op=ALU.add)
+        for h in range(2):
+            nc.vector.quantize_mx(out=w_codes[:, cols(h, 512)].bitcast(FP8X4), scales=w_scales[:, cols(h, 512)], in_=wsim[:, cols(h, 2048)])
+        xg1 = x_copies(pt1)
+
+        ndma = {0: 1, 1: 2, 2: 2, 7: 1}
+        for g in range(GROUPS):
+            pts = transposes(g + 1, 2 * (g % 2)) if 1 <= g < GROUPS - 1 else None
+            xg = xg1 if g == 0 else None
+            o = opool.tile([P, 4, NOUT], F32, name="o_sb")
+            dst = of[512 * g : 512 * g + 512, :].rearrange("(p t) n -> p t n", t=4)
+            n = ndma.get(g, 4)
+            for t in range(4):
+                for h in range(2):
+                    hs = cols(h, 512)
+                    acc = psum.tile([P, 512], F32, name="acc", tag="b%d" % (4 + (2 * t + h + 2) % 4))
+                    nc.tensor.matmul_mx(
+                        out=acc[:],
+                        lhsT=x_codes[:, g, cols(t, P)].bitcast(FP8X4), lhsT_scale=x_scales[:, g, cols(t, P)],
+                        rhs=w_codes[:, hs].bitcast(FP8X4), rhs_scale=w_scales[:, hs],
+                        start=True, stop=True)
+                    if h == 0 and t < 3 and (g, t) != (0, 0):
+                        nc.scalar.copy(out=o[:, t, hs], in_=acc[:])
+                        nc.gpsimd.tensor_tensor(out=o[:, t, hs], in0=o[:, t, hs], in1=bias_bc[:, hs], op=ALU.add)
+                        if t == 1 and pts is not None:
+                            xg = x_copies(pts)
+                    else:
+                        nc.vector.tensor_tensor(out=o[:, t, hs], in0=acc[:], in1=bias_bc[:, hs], op=ALU.add)
+                if xg is not None and t == (1 if g == 0 else 2):
+                    x_quant(g + 1, xg)
+                if (t + 1) % n == 0:
+                    nc.sync.dma_start(out=dst[:, t + 1 - n : t + 1, :], in_=o[:, t + 1 - n : t + 1, :])

@@ -230,30 +230,40 @@ def tile_binaryxnorexceptoutlierslinear_t_kernel(tc, x, weight, bias, out):
             nc.vector.quantize_mx(out=w_codes[:, cols(h, 512)].bitcast(FP8X4), scales=w_scales[:, cols(h, 512)], in_=wsim[:, cols(h, 2048)])
         xg1 = x_copies(pt1)
 
+        def product(g, t, h):
+            hs = cols(h, 512)
+            acc = psum.tile([P, 512], F32, name="acc", tag="b%d" % (2 + (4 + 8 * g + 2 * t + h) % 6))
+            nc.tensor.matmul_mx(
+                out=acc[:],
+                lhsT=x_codes[:, g, cols(t, P)].bitcast(FP8X4), lhsT_scale=x_scales[:, g, cols(t, P)],
+                rhs=w_codes[:, hs].bitcast(FP8X4), rhs_scale=w_scales[:, hs],
+                start=True, stop=True)
+            return acc
+
+        def finish(o, t, h, acc, by_scalar):
+            hs = cols(h, 512)
+            if by_scalar:
+                nc.scalar.copy(out=o[:, t, hs], in_=acc[:])
+                nc.gpsimd.tensor_tensor(out=o[:, t, hs], in0=o[:, t, hs], in1=bias_bc[:, hs], op=ALU.add)
+            else:
+                nc.vector.tensor_tensor(out=o[:, t, hs], in0=acc[:], in1=bias_bc[:, hs], op=ALU.add)
+
         ndma = {0: 1, 1: 2, 2: 2, 7: 1}
+        xg = xg1
         for g in range(GROUPS):
-            pts = transposes(g + 1, 2 * (g % 2)) if 1 <= g < GROUPS - 1 else None
-            xg = xg1 if g == 0 else None
             o = opool.tile([P, 4, NOUT], F32, name="o_sb")
             dst = of[512 * g : 512 * g + 512, :].rearrange("(p t) n -> p t n", t=4)
             n = ndma.get(g, 4)
+            pts = transposes(g + 2, 0) if 0 < g < GROUPS - 2 else None
+            if 0 < g < GROUPS - 1:
+                x_quant(g + 1, xg)
             for t in range(4):
                 for h in range(2):
-                    hs = cols(h, 512)
-                    acc = psum.tile([P, 512], F32, name="acc", tag="b%d" % (4 + (2 * t + h + 2) % 4))
-                    nc.tensor.matmul_mx(
-                        out=acc[:],
-                        lhsT=x_codes[:, g, cols(t, P)].bitcast(FP8X4), lhsT_scale=x_scales[:, g, cols(t, P)],
-                        rhs=w_codes[:, hs].bitcast(FP8X4), rhs_scale=w_scales[:, hs],
-                        start=True, stop=True)
-                    if h == 0 and t < 3 and (g, t) != (0, 0):
-                        nc.scalar.copy(out=o[:, t, hs], in_=acc[:])
-                        nc.gpsimd.tensor_tensor(out=o[:, t, hs], in0=o[:, t, hs], in1=bias_bc[:, hs], op=ALU.add)
-                        if t == 1 and pts is not None:
-                            xg = x_copies(pts)
-                    else:
-                        nc.vector.tensor_tensor(out=o[:, t, hs], in0=acc[:], in1=bias_bc[:, hs], op=ALU.add)
-                if xg is not None and t == (1 if g == 0 else 2):
-                    x_quant(g + 1, xg)
+                    finish(o, t, h, product(g, t, h), h == 0 and t in ((1, 2) if g == 0 else (0, 1)))
+                if t == 1 and g == 0:
+                    x_quant(1, xg)
+                    pts = transposes(2, 0)
+                if t == 2 and pts is not None:
+                    xg = x_copies(pts)
                 if (t + 1) % n == 0:
                     nc.sync.dma_start(out=dst[:, t + 1 - n : t + 1, :], in_=o[:, t + 1 - n : t + 1, :])

@@ -108,9 +108,10 @@ def tile_binaryxnorexceptoutlierslinear_t_kernel(tc, x, weight, bias, out):
                     nc.tensor.transpose(out=pw[c][:, jj, u, :], in_=w_sb[:, 2 * c + jj, :].bitcast(F32)[:, u : 2 * P : 2], identity=ident[:])
 
         w_transposes(0)
+        w_transposes(1)
         cs = psum.tile([P, 8], F32, name="cs", tag="b5")
         nc.tensor.matmul(out=cs[:, 0:7], lhsT=ones_f[:], rhs=st[:, 0:7], start=True, stop=True)
-        for c in range(1, 4):
+        for c in range(2, 4):
             w_transposes(c)
 
         def evac(c, copy):
@@ -119,11 +120,11 @@ def tile_binaryxnorexceptoutlierslinear_t_kernel(tc, x, weight, bias, out):
         def sign(c):
             nc.vector.tensor_scalar(out=ws[:, cols(c)], in0=wTf[:, cols(c)], scalar1=-TINY, scalar2=TINY, op0=ALU.max, op1=ALU.min)
 
-        def square(c):
-            nc.scalar.activation(out=q[:, cols(c)], in_=wTf[:, cols(c)], func=ACT.Square, bias=nbt[:], scale=SC)
+        def square(c, n=1024):
+            nc.scalar.activation(out=q[:, cols(c, n)], in_=wTf[:, cols(c, n)], func=ACT.Square, bias=nbt[:], scale=SC)
 
-        def mask(c):
-            nc.vector.tensor_scalar(out=kk[:, cols(c)], in0=q[:, cols(c)], scalar1=thr[:], scalar2=HUGE, op0=ALU.is_le, op1=ALU.mult)
+        def mask(c, n=1024):
+            nc.vector.tensor_scalar(out=kk[:, cols(c, n)], in0=q[:, cols(c, n)], scalar1=thr[:], scalar2=HUGE, op0=ALU.is_le, op1=ALU.mult)
 
         def masked_sign(c):
             nc.vector.tensor_tensor(out=bm[:, cols(c)], in0=ws[:, cols(c)], in1=kk[:, cols(c)], op=ALU.mult)
@@ -166,16 +167,18 @@ def tile_binaryxnorexceptoutlierslinear_t_kernel(tc, x, weight, bias, out):
 
         vcopy, scopy = nc.vector.tensor_copy, nc.scalar.copy
         evac(0, vcopy)
+        evac(1, scopy)
         nc.vector.tensor_scalar(out=nbt[:], in0=cs[:, 0:1], scalar1=-SC * half / NW, scalar2=nbs[:], op0=ALU.mult, op1=ALU.add)
         nc.vector.reduce_sum(out=s4[:], in_=cs[:, 2:6], axis=mybir.AxisListType.X)
         nc.vector.tensor_scalar(out=sm2[:], in0=nbt[:], scalar1=nbt[:], scalar2=-NW / (SC * SC), op0=ALU.mult, op1=ALU.mult)
         nc.vector.tensor_scalar(out=ssq[:], in0=cs[:, 6:7], scalar1=float(half), scalar2=s4[:], op0=ALU.mult, op1=ALU.add)
         sign(0)
         nc.vector.tensor_scalar(out=thr[:], in0=ssq[:], scalar1=sm2[:], scalar2=None, op0=ALU.add)
-        evac(1, vcopy)
-        square(0)
-        mask(0)
+        square(0, 512)
+        square(1, 512)
         sign(1)
+        mask(0, 512)
+        mask(1, 512)
         masked_sign(0)
         keep_sums(0)
         pt0 = transposes(0, 0)
@@ -220,6 +223,7 @@ def tile_binaryxnorexceptoutlierslinear_t_kernel(tc, x, weight, bias, out):
         nc.vector.tensor_scalar(out=c_ident[:], in0=ident_bf[:], scalar1=l2b[:, 0:1], scalar2=rc[:], op0=ALU.mult, op1=ALU.mult)
         for b in range(4):
             nc.tensor.matmul(out=wacc[b][:], lhsT=c_ident[:], rhs=bm[:, cols(4 + b, 512)], start=False, stop=True)
+        xg1 = x_copies(pt1)
         for b in range(4):
             nc.scalar.copy(out=wsim[:, cols(4 + b, 512)], in_=wacc[b][:])
         nc.vector.tensor_scalar(out=cb[:], in0=bm[:, 0:2048], scalar1=l2b[:, 0:1], scalar2=rc[:], op0=ALU.mult, op1=ALU.mult)
@@ -228,11 +232,11 @@ def tile_binaryxnorexceptoutlierslinear_t_kernel(tc, x, weight, bias, out):
         nc.vector.tensor_tensor(out=wsim[:, 1024:2048], in0=cb[:, 1024:2048], in1=aa[:, 1024:2048], op=ALU.add)
         for h in range(2):
             nc.vector.quantize_mx(out=w_codes[:, cols(h, 512)].bitcast(FP8X4), scales=w_scales[:, cols(h, 512)], in_=wsim[:, cols(h, 2048)])
-        xg1 = x_copies(pt1)
 
-        def product(g, t, h):
+        def product(g, i, t, h):
             hs = cols(h, 512)
-            acc = psum.tile([P, 512], F32, name="acc", tag="b%d" % (2 + (4 + 8 * g + 2 * t + h) % 6))
+            bank = (6, 7, 2, 3, 0, 1, 4, 5)[i] if g == 0 else 2 + (8 * (g - 1) + i) % 6
+            acc = psum.tile([P, 512], F32, name="acc", tag="b%d" % bank)
             nc.tensor.matmul_mx(
                 out=acc[:],
                 lhsT=x_codes[:, g, cols(t, P)].bitcast(FP8X4), lhsT_scale=x_scales[:, g, cols(t, P)],
@@ -248,22 +252,30 @@ def tile_binaryxnorexceptoutlierslinear_t_kernel(tc, x, weight, bias, out):
             else:
                 nc.vector.tensor_tensor(out=o[:, t, hs], in0=acc[:], in1=bias_bc[:, hs], op=ALU.add)
 
-        ndma = {0: 1, 1: 2, 2: 2, 7: 1}
-        xg = xg1
+        ramp = (((2, 0), True), ((0, 0), False), ((3, 0), True), ((0, 1), False), ((1, 0), False), ((3, 1), True), ((1, 1), False), ((2, 1), False))
+        steady = (((2, 0), True), ((0, 0), False), ((0, 1), False), ((3, 0), True), ((1, 0), False), ((1, 1), False), ((2, 1), False), ((3, 1), False))
+        ndma = {0: 1, 1: 1, 2: 2, 7: 1}
+        xg = None
         for g in range(GROUPS):
             o = opool.tile([P, 4, NOUT], F32, name="o_sb")
             dst = of[512 * g : 512 * g + 512, :].rearrange("(p t) n -> p t n", t=4)
             n = ndma.get(g, 4)
-            pts = transposes(g + 2, 0) if 0 < g < GROUPS - 2 else None
+            pts = None
             if 0 < g < GROUPS - 1:
                 x_quant(g + 1, xg)
-            for t in range(4):
-                for h in range(2):
-                    finish(o, t, h, product(g, t, h), h == 0 and t in ((1, 2) if g == 0 else (0, 1)))
-                if t == 1 and g == 0:
-                    x_quant(1, xg)
-                    pts = transposes(2, 0)
-                if t == 2 and pts is not None:
+            done = []
+            stored = 0
+            for i, ((t, h), by_scalar) in enumerate(ramp if g < 2 else steady):
+                finish(o, t, h, product(g, i, t, h), by_scalar)
+                done.append(t)
+                if i == 3 and 0 < g < GROUPS - 2:
+                    pts = transposes(g + 2, 0)
+                if i == 6 and pts is not None:
                     xg = x_copies(pts)
-                if (t + 1) % n == 0:
-                    nc.sync.dma_start(out=dst[:, t + 1 - n : t + 1, :], in_=o[:, t + 1 - n : t + 1, :])
+                while stored < 4 and all(done.count(r) == 2 for r in range(stored, stored + n)):
+                    nc.sync.dma_start(out=dst[:, stored : stored + n, :], in_=o[:, stored : stored + n, :])
+                    stored += n
+                if g == 0 and (t, h) == (1, 1):
+                    x_quant(1, xg1)
+            if g == 0:
+                xg = x_copies(transposes(2, 0))

@@ -22,6 +22,7 @@ GROUPS = 8
 SC = math.sqrt((NW - 1) / (1.6 * 1.6))
 TINY = 2.0 ** -126
 HUGE = 2.0 ** 126
+DIRECT = 1536
 
 
 def tile_binaryxnorexceptoutlierslinear_t_kernel(tc, x, weight, bias, out):
@@ -48,6 +49,9 @@ def tile_binaryxnorexceptoutlierslinear_t_kernel(tc, x, weight, bias, out):
         x_scales = keep.tile([P, GROUPS, 512], U8, name="x_scales", align_bytes=64)
         w_codes = keep.tile([P, NOUT], U32, name="w_codes", align_bytes=64)
         w_scales = keep.tile([P, NOUT], U8, name="w_scales", align_bytes=64)
+        zero = keep.tile([P, 1024], BF16, name="zero", align_bytes=64)
+        z_codes = keep.tile([P, 256], U32, name="z_codes", align_bytes=64)
+        z_scales = keep.tile([P, 256], U8, name="z_scales", align_bytes=64)
         wT = keep.tile([P, NOUT, 4], BF16, name="wT")
         wT32 = wT[:].bitcast(F32)
         wTf = wT[:].rearrange("p n v -> p (n v)")
@@ -75,14 +79,24 @@ def tile_binaryxnorexceptoutlierslinear_t_kernel(tc, x, weight, bias, out):
         def cols(c, n=1024):
             return slice(n * c, n * c + n)
 
+        nc.vector.memset(zero[:], 0.0)
         nc.vector.memset(ones_bf[:], 1.0)
         nc.vector.memset(ones_f[:], 1.0)
         nc.vector.memset(tinycol[:], TINY)
         masks.make_identity(nc, ident[:])
         masks.make_identity(nc, ident_bf[:])
 
+        nc.vector.quantize_mx(out=z_codes[:].bitcast(FP8X4), scales=z_scales[:], in_=zero[:])
+
+        def zero_products(n, bank):
+            z = psum.tile([P, 256], F32, name="z", tag="b%d" % bank)
+            for i in range(n):
+                nc.tensor.matmul_mx(out=z[:], lhsT=z_codes[:, 0:P].bitcast(FP8X4), lhsT_scale=z_scales[:, 0:P], rhs=z_codes[:].bitcast(FP8X4), rhs_scale=z_scales[:], start=True, stop=True)
+
+        zero_products(6, 7)
+
         for c in range(4):
-            nc.sync.dma_start(out=w_sb[:, 2 * c : 2 * c + 2, :], in_=weight[256 * c : 256 * c + 256, :].rearrange("(j p) k -> p j k", p=P))
+            nc.sync.dma_start(out=w_sb[:, 2 * c : 2 * c + 2, :], in_=weight[256 * c : 256 * c + 256, :].rearrange("(p j) k -> p j k", j=2))
         for g in range(GROUPS):
             nc.sync.dma_start(out=x_sb[:, g, :, :], in_=xf[512 * g : 512 * g + 512, :].rearrange("(p t) k -> p t k", t=4))
             if g == 1:
@@ -113,9 +127,10 @@ def tile_binaryxnorexceptoutlierslinear_t_kernel(tc, x, weight, bias, out):
         nc.tensor.matmul(out=cs[:, 0:7], lhsT=ones_f[:], rhs=st[:, 0:7], start=True, stop=True)
         for c in range(2, 4):
             w_transposes(c)
+        zero_products(8, 7)
 
         def evac(c, copy):
-            copy(out=wT32[:, 256 * c : 256 * c + 256, :].rearrange("p (j r) u -> p j r u", j=2), in_=pw[c][:].rearrange("p j u r -> p j r u"))
+            copy(out=wT32[:, 256 * c : 256 * c + 256, :].rearrange("p (r j) u -> p r j u", j=2), in_=pw[c][:].rearrange("p j u r -> p r j u"))
 
         def sign(c):
             nc.vector.tensor_scalar(out=ws[:, cols(c)], in0=wTf[:, cols(c)], scalar1=-TINY, scalar2=TINY, op0=ALU.max, op1=ALU.min)
@@ -129,14 +144,14 @@ def tile_binaryxnorexceptoutlierslinear_t_kernel(tc, x, weight, bias, out):
         def masked_sign(c):
             nc.vector.tensor_tensor(out=bm[:, cols(c)], in0=ws[:, cols(c)], in1=kk[:, cols(c)], op=ALU.mult)
 
-        def outlier_mask(c, by_scalar):
-            if by_scalar:
-                nc.scalar.activation(out=oo[:, cols(c)], in_=kk[:, cols(c)], func=ACT.Identity, scale=-TINY, bias=1.0)
-            else:
-                nc.vector.tensor_scalar(out=oo[:, cols(c)], in0=kk[:, cols(c)], scalar1=-TINY, scalar2=1.0, op0=ALU.mult, op1=ALU.add)
+        def outlier_mask_v(s):
+            nc.vector.tensor_scalar(out=oo[:, s], in0=kk[:, s], scalar1=-TINY, scalar2=1.0, op0=ALU.mult, op1=ALU.add)
 
-        def outliers(c):
-            nc.vector.tensor_tensor(out=aa[:, cols(c)], in0=wTf[:, cols(c)], in1=oo[:, cols(c)], op=ALU.mult)
+        def outlier_mask_s(s):
+            nc.scalar.activation(out=oo[:, s], in_=kk[:, s], func=ACT.Identity, scale=-TINY, bias=1.0)
+
+        def outliers(s):
+            nc.vector.tensor_tensor(out=aa[:, s], in0=wTf[:, s], in1=oo[:, s], op=ALU.mult)
 
         gram = psum.tile([P, P], F32, name="gram", tag="b6")
         ck = psum.tile([P, 1], F32, name="ck", tag="b7")
@@ -176,62 +191,71 @@ def tile_binaryxnorexceptoutlierslinear_t_kernel(tc, x, weight, bias, out):
         nc.vector.tensor_scalar(out=thr[:], in0=ssq[:], scalar1=sm2[:], scalar2=None, op0=ALU.add)
         square(0, 512)
         square(1, 512)
-        sign(1)
         mask(0, 512)
         mask(1, 512)
+        sign(1)
+        square(1)
+        evac(2, scopy)
         masked_sign(0)
         keep_sums(0)
         pt0 = transposes(0, 0)
-        square(1)
-        evac(2, scopy)
         mask(1)
-        sign(2)
-        masked_sign(1)
-        keep_sums(1)
-        pt1 = transposes(1, 4)
         square(2)
         evac(3, scopy)
+        sign(2)
+        masked_sign(1)
+        zero_products(2, 2)
+        keep_sums(1)
+        pt1 = transposes(1, 4)
         mask(2)
+        square(3)
         sign(3)
         masked_sign(2)
+        zero_products(2, 2)
         keep_sums(2)
-        square(3)
         xg0 = x_copies(pt0)
-        outlier_mask(2, False)
+        outlier_mask_v(cols(2))
         mask(3)
-        outliers(2)
+        outliers(cols(2))
         masked_sign(3)
+        zero_products(2, 2)
         keep_sums(3)
-        outlier_mask(3, False)
-        outlier_mask(0, True)
-        wacc = []
-        for b in range(4):
-            wacc.append(psum.tile([P, 512], F32, name="wacc", tag="b%d" % ((2, 3, 0, 1)[b])))
-        for b in range(2):
-            nc.tensor.matmul(out=wacc[b][:], lhsT=ident_bf[:], rhs=aa[:, cols(4 + b, 512)], start=True, stop=False)
+        outlier_mask_s(cols(1))
+        outlier_mask_s(cols(0))
+        xg1 = x_copies(pt1)
+        outlier_mask_v(cols(3))
+
+        wacc = {}
+
+        def add_outliers(b, bank):
+            wacc[b] = psum.tile([P, 512], F32, name="wacc", tag="b%d" % bank)
+            nc.tensor.matmul(out=wacc[b][:], lhsT=ident_bf[:], rhs=aa[:, cols(b, 512)], start=True, stop=False)
+
         x_quant(0, xg0)
-        outliers(3)
+        outliers(cols(3))
+        add_outliers(4, 2)
+        add_outliers(5, 3)
         nc.vector.tensor_copy(out=st2[:, 1:2], in_=ck[:])
         nc.vector.scalar_tensor_tensor(out=junk_d[:], in0=gram[:], scalar=1.0, in1=ident[:], op0=ALU.mult, op1=ALU.mult, accum_out=st2[:, 0:1])
         l2b = psum.tile([P, 2], F32, name="l2b", tag="b7")
         nc.tensor.matmul(out=l2b[:], lhsT=ones_f[:], rhs=st2[:], start=True, stop=True)
-        for b in range(2, 4):
-            nc.tensor.matmul(out=wacc[b][:], lhsT=ident_bf[:], rhs=aa[:, cols(4 + b, 512)], start=True, stop=False)
-        outlier_mask(1, True)
-        outliers(0)
+        add_outliers(6, 0)
+        add_outliers(7, 1)
+        outliers(cols(3, 512))
+        add_outliers(3, 6)
         nc.vector.reciprocal(out=rc[:], in_=l2b[:, 1:2])
+        outliers(cols(2, 512))
         nc.vector.tensor_scalar(out=c_ident[:], in0=ident_bf[:], scalar1=l2b[:, 0:1], scalar2=rc[:], op0=ALU.mult, op1=ALU.mult)
-        for b in range(4):
-            nc.tensor.matmul(out=wacc[b][:], lhsT=c_ident[:], rhs=bm[:, cols(4 + b, 512)], start=False, stop=True)
-        xg1 = x_copies(pt1)
-        for b in range(4):
-            nc.scalar.copy(out=wsim[:, cols(4 + b, 512)], in_=wacc[b][:])
-        nc.vector.tensor_scalar(out=cb[:], in0=bm[:, 0:2048], scalar1=l2b[:, 0:1], scalar2=rc[:], op0=ALU.mult, op1=ALU.mult)
-        outliers(1)
-        nc.vector.tensor_tensor(out=wsim[:, 0:1024], in0=cb[:, 0:1024], in1=aa[:, 0:1024], op=ALU.add)
-        nc.vector.tensor_tensor(out=wsim[:, 1024:2048], in0=cb[:, 1024:2048], in1=aa[:, 1024:2048], op=ALU.add)
-        for h in range(2):
-            nc.vector.quantize_mx(out=w_codes[:, cols(h, 512)].bitcast(FP8X4), scales=w_scales[:, cols(h, 512)], in_=wsim[:, cols(h, 2048)])
+        for b in range(3, 8):
+            nc.tensor.matmul(out=wacc[b][:], lhsT=c_ident[:], rhs=bm[:, cols(b, 512)], start=False, stop=True)
+        for b in range(3, 8):
+            nc.scalar.copy(out=wsim[:, cols(b, 512)], in_=wacc[b][:])
+        nc.vector.tensor_scalar(out=cb[:, 0:DIRECT], in0=bm[:, 0:DIRECT], scalar1=l2b[:, 0:1], scalar2=rc[:], op0=ALU.mult, op1=ALU.mult)
+        outliers(cols(0))
+        for s in (slice(1024, DIRECT), slice(0, 1024)):
+            nc.vector.tensor_tensor(out=wsim[:, s], in0=cb[:, s], in1=aa[:, s], op=ALU.add)
+        for n0 in (256, 0, 512, 768):
+            nc.vector.quantize_mx(out=w_codes[:, n0 : n0 + 256].bitcast(FP8X4), scales=w_scales[:, n0 : n0 + 256], in_=wsim[:, 4 * n0 : 4 * n0 + 1024])
 
         def product(g, i, t, h):
             hs = cols(h, 512)

@@ -22,7 +22,7 @@ GROUPS = 8
 SC = math.sqrt((NW - 1) / (1.6 * 1.6))
 TINY = 2.0 ** -126
 HUGE = 2.0 ** 126
-DIRECT = 1536
+DIRECT = 1024
 
 
 def tile_binaryxnorexceptoutlierslinear_t_kernel(tc, x, weight, bias, out):
@@ -79,7 +79,7 @@ def tile_binaryxnorexceptoutlierslinear_t_kernel(tc, x, weight, bias, out):
         def cols(c, n=1024):
             return slice(n * c, n * c + n)
 
-        nc.vector.memset(zero[:], 0.0)
+        nc.vector.memset(zero[:].bitcast(U32), 0)
         nc.vector.memset(ones_bf[:], 1.0)
         nc.vector.memset(ones_f[:], 1.0)
         nc.vector.memset(tinycol[:], TINY)
@@ -93,7 +93,7 @@ def tile_binaryxnorexceptoutlierslinear_t_kernel(tc, x, weight, bias, out):
             for i in range(n):
                 nc.tensor.matmul_mx(out=z[:], lhsT=z_codes[:, 0:P].bitcast(FP8X4), lhsT_scale=z_scales[:, 0:P], rhs=z_codes[:].bitcast(FP8X4), rhs_scale=z_scales[:], start=True, stop=True)
 
-        zero_products(6, 7)
+        zero_products(5, 7)
 
         for c in range(4):
             nc.sync.dma_start(out=w_sb[:, 2 * c : 2 * c + 2, :], in_=weight[256 * c : 256 * c + 256, :].rearrange("(p j) k -> p j k", j=2))
@@ -228,7 +228,7 @@ def tile_binaryxnorexceptoutlierslinear_t_kernel(tc, x, weight, bias, out):
         wacc = {}
 
         def add_outliers(b, bank):
-            wacc[b] = psum.tile([P, 512], F32, name="wacc", tag="b%d" % bank)
+            wacc[b] = psum.tile([P, 512], BF16, name="wacc", tag="b%d" % bank)
             nc.tensor.matmul(out=wacc[b][:], lhsT=ident_bf[:], rhs=aa[:, cols(b, 512)], start=True, stop=False)
 
         x_quant(0, xg0)
@@ -241,19 +241,19 @@ def tile_binaryxnorexceptoutlierslinear_t_kernel(tc, x, weight, bias, out):
         nc.tensor.matmul(out=l2b[:], lhsT=ones_f[:], rhs=st2[:], start=True, stop=True)
         add_outliers(6, 0)
         add_outliers(7, 1)
-        outliers(cols(3, 512))
+        outliers(cols(1))
         add_outliers(3, 6)
+        add_outliers(2, 4)
         nc.vector.reciprocal(out=rc[:], in_=l2b[:, 1:2])
-        outliers(cols(2, 512))
+        outliers(cols(0, 512))
         nc.vector.tensor_scalar(out=c_ident[:], in0=ident_bf[:], scalar1=l2b[:, 0:1], scalar2=rc[:], op0=ALU.mult, op1=ALU.mult)
-        for b in range(3, 8):
+        for b in range(2, 8):
             nc.tensor.matmul(out=wacc[b][:], lhsT=c_ident[:], rhs=bm[:, cols(b, 512)], start=False, stop=True)
-        for b in range(3, 8):
+        for b in range(2, 8):
             nc.scalar.copy(out=wsim[:, cols(b, 512)], in_=wacc[b][:])
         nc.vector.tensor_scalar(out=cb[:, 0:DIRECT], in0=bm[:, 0:DIRECT], scalar1=l2b[:, 0:1], scalar2=rc[:], op0=ALU.mult, op1=ALU.mult)
-        outliers(cols(0))
-        for s in (slice(1024, DIRECT), slice(0, 1024)):
-            nc.vector.tensor_tensor(out=wsim[:, s], in0=cb[:, s], in1=aa[:, s], op=ALU.add)
+        outliers(cols(1, 512))
+        nc.vector.tensor_tensor(out=wsim[:, 0:DIRECT], in0=cb[:, 0:DIRECT], in1=aa[:, 0:DIRECT], op=ALU.add)
         for n0 in (256, 0, 512, 768):
             nc.vector.quantize_mx(out=w_codes[:, n0 : n0 + 256].bitcast(FP8X4), scales=w_scales[:, n0 : n0 + 256], in_=wsim[:, 4 * n0 : 4 * n0 + 1024])
 
@@ -278,20 +278,22 @@ def tile_binaryxnorexceptoutlierslinear_t_kernel(tc, x, weight, bias, out):
 
         ramp = (((2, 0), True), ((0, 0), False), ((3, 0), True), ((0, 1), False), ((1, 0), False), ((3, 1), True), ((1, 1), False), ((2, 1), False))
         steady = (((2, 0), True), ((0, 0), False), ((0, 1), False), ((3, 0), True), ((1, 0), False), ((1, 1), False), ((2, 1), False), ((3, 1), False))
-        ndma = {0: 1, 1: 1, 2: 2, 7: 1}
+        ndma = {0: 1, 1: 1, 7: 1}
         xg = None
         for g in range(GROUPS):
             o = opool.tile([P, 4, NOUT], F32, name="o_sb")
             dst = of[512 * g : 512 * g + 512, :].rearrange("(p t) n -> p t n", t=4)
-            n = ndma.get(g, 4)
+            n = ndma.get(g, 2)
             pts = None
-            if 0 < g < GROUPS - 1:
+            if 1 < g < GROUPS - 1:
                 x_quant(g + 1, xg)
             done = []
             stored = 0
-            for i, ((t, h), by_scalar) in enumerate(ramp if g < 2 else steady):
+            for i, ((t, h), by_scalar) in enumerate(steady if g in (2, 4, 6) else ramp):
                 finish(o, t, h, product(g, i, t, h), by_scalar)
                 done.append(t)
+                if i == 4 and g == 1:
+                    x_quant(2, xg)
                 if i == 3 and 0 < g < GROUPS - 2:
                     pts = transposes(g + 2, 0)
                 if i == 6 and pts is not None:

@@ -20,9 +20,9 @@ NW = NOUT * K
 FLOPS = 2 * TOK * NOUT * K
 GROUPS = 8
 SC = math.sqrt((NW - 1) / (1.6 * 1.6))
-TINY = 2.0 ** -126
-HUGE = 2.0 ** 126
 DIRECT = 1024
+BIG = 2.0 ** 63
+SMALL = 2.0 ** -63
 
 
 def tile_binaryxnorexceptoutlierslinear_t_kernel(tc, x, weight, bias, out):
@@ -38,9 +38,10 @@ def tile_binaryxnorexceptoutlierslinear_t_kernel(tc, x, weight, bias, out):
 
         ones_bf = keep.tile([P, P], BF16, name="ones_bf")
         ones_f = keep.tile([P, P], F32, name="ones_f")
-        tinycol = keep.tile([P, 2], BF16, name="tinycol")
+        smallcol = keep.tile([P, 2], BF16, name="smallcol")
         ident = keep.tile([P, P], F32, name="ident")
         ident_bf = keep.tile([P, P], BF16, name="ident_bf")
+        minus_ident = keep.tile([P, P], BF16, name="minus_ident")
         c_ident = keep.tile([P, P], BF16, name="c_ident")
         w_sb = keep.tile([P, 8, K], BF16, name="w_sb")
         x_sb = keep.tile([P, GROUPS, 4, K], BF16, name="x_sb")
@@ -55,22 +56,22 @@ def tile_binaryxnorexceptoutlierslinear_t_kernel(tc, x, weight, bias, out):
         wT = keep.tile([P, NOUT, 4], BF16, name="wT")
         wT32 = wT[:].bitcast(F32)
         wTf = wT[:].rearrange("p n v -> p (n v)")
-        ws = keep.tile([P, 4 * NOUT], BF16, name="ws")
         q = keep.tile([P, 4 * NOUT], F32, name="q")
         kk = keep.tile([P, 4 * NOUT], BF16, name="kk")
+        kw = keep.tile([P, 4 * NOUT], BF16, name="kw")
         bm = keep.tile([P, 4 * NOUT], BF16, name="bm")
-        oo = keep.tile([P, 4 * NOUT], BF16, name="oo")
-        aa = keep.tile([P, 4 * NOUT], BF16, name="aa")
-        cb = keep.tile([P, 2 * NOUT], BF16, name="cb")
+        oo = keep.tile([P, DIRECT], BF16, name="oo")
+        aa = keep.tile([P, DIRECT], BF16, name="aa")
+        cb = keep.tile([P, DIRECT], BF16, name="cb")
         wsim = keep.tile([P, 4 * NOUT], BF16, name="wsim", align_bytes=64)
-        junk_s = keep.tile([P, 512], BF16, name="junk_s")
+        junk_s = keep.tile([P, 1024], BF16, name="junk_s")
         junk_d = keep.tile([P, P], F32, name="junk_d")
-        bn = keep.tile([P, 4, 6], F32, name="bn")
-        st = keep.tile([P, 8], F32, name="st")
-        nbs = keep.tile([P, 1], F32, name="nbs")
-        s4 = keep.tile([P, 1], F32, name="s4")
-        ssq = keep.tile([P, 1], F32, name="ssq")
+        st = keep.tile([P, 14, 3], F32, name="st")
+        stf = st[:].rearrange("p r s -> p (r s)")
+        junk_t = keep.tile([P, 14], F32, name="junk_t")
+        junk_m = keep.tile([P, 9], F32, name="junk_m")
         st2 = keep.tile([P, 2], F32, name="st2")
+        abs0 = keep.tile([P, 1], F32, name="abs0")
         nbt = keep.tile([P, 1], F32, name="nbt")
         sm2 = keep.tile([P, 1], F32, name="sm2")
         thr = keep.tile([P, 1], F32, name="thr")
@@ -79,21 +80,23 @@ def tile_binaryxnorexceptoutlierslinear_t_kernel(tc, x, weight, bias, out):
         def cols(c, n=1024):
             return slice(n * c, n * c + n)
 
+        nc.vector.memset(smallcol[:], SMALL)
+        nc.scalar.activation(out=junk_s[:, 0:2], in_=smallcol[:], func=ACT.Square)
         nc.vector.memset(zero[:].bitcast(U32), 0)
         nc.vector.memset(ones_bf[:], 1.0)
         nc.vector.memset(ones_f[:], 1.0)
-        nc.vector.memset(tinycol[:], TINY)
+        nc.vector.memset(st[:], 0.0)
         masks.make_identity(nc, ident[:])
         masks.make_identity(nc, ident_bf[:])
 
         nc.vector.quantize_mx(out=z_codes[:].bitcast(FP8X4), scales=z_scales[:], in_=zero[:])
 
-        def zero_products(n, bank):
-            z = psum.tile([P, 256], F32, name="z", tag="b%d" % bank)
+        def zero_products(n):
+            z = psum.tile([P, 256], F32, name="z", tag="b7")
             for i in range(n):
                 nc.tensor.matmul_mx(out=z[:], lhsT=z_codes[:, 0:P].bitcast(FP8X4), lhsT_scale=z_scales[:, 0:P], rhs=z_codes[:].bitcast(FP8X4), rhs_scale=z_scales[:], start=True, stop=True)
 
-        zero_products(5, 7)
+        zero_products(5)
 
         for c in range(4):
             nc.sync.dma_start(out=w_sb[:, 2 * c : 2 * c + 2, :], in_=weight[256 * c : 256 * c + 256, :].rearrange("(p j) k -> p j k", j=2))
@@ -102,16 +105,7 @@ def tile_binaryxnorexceptoutlierslinear_t_kernel(tc, x, weight, bias, out):
             if g == 1:
                 nc.sync.dma_start(out=bias_bc[:], in_=bias.partition_broadcast(P))
 
-        half = NW // (2 * P)
-        sw = psum.tile([P, 256], F32, name="sw", tag="b4")
-        for c in range(4):
-            for b in range(2):
-                nc.tensor.matmul(out=sw[:], lhsT=ones_bf[:], rhs=w_sb[:, 2 * c, cols(b, 256)], start=(c == 0 and b == 0), stop=(c == 3 and b == 1))
-            nc.scalar.activation(out=junk_s[:], in_=w_sb[:, 2 * c, :], func=ACT.Square, accum_out=st[:, 2 + c : 3 + c])
-            nc.vector.bn_stats(out=bn[:, c, :], in_=w_sb[:, 2 * c + 1, :])
-        nc.scalar.activation(out=junk_s[:, 0:256], in_=sw[:], func=ACT.Identity, scale=-SC / NW, accum_out=nbs[:])
-        nc.vector.bn_aggr(out=st[:, 0:2], in_=bn[:].rearrange("p c s -> p (c s)"))
-        nc.vector.scalar_tensor_tensor(out=st[:, 6:7], in0=st[:, 0:1], scalar=st[:, 0:1], in1=st[:, 1:2], op0=ALU.mult, op1=ALU.add)
+        colsum = psum.tile([P, 1], F32, name="colsum", tag="b4")
         pw = []
         for c in range(4):
             pw.append(psum.tile([P, 2, 2, P], F32, name="pw", tag="b%d" % c))
@@ -121,45 +115,48 @@ def tile_binaryxnorexceptoutlierslinear_t_kernel(tc, x, weight, bias, out):
                 for u in range(2):
                     nc.tensor.transpose(out=pw[c][:, jj, u, :], in_=w_sb[:, 2 * c + jj, :].bitcast(F32)[:, u : 2 * P : 2], identity=ident[:])
 
-        w_transposes(0)
-        w_transposes(1)
-        cs = psum.tile([P, 8], F32, name="cs", tag="b5")
-        nc.tensor.matmul(out=cs[:, 0:7], lhsT=ones_f[:], rhs=st[:, 0:7], start=True, stop=True)
-        for c in range(2, 4):
-            w_transposes(c)
-        zero_products(8, 7)
+        for c in range(4):
+            for b in range(4):
+                nc.tensor.matmul(out=colsum[:], lhsT=w_sb[:, 2 * c, cols(b, P)], rhs=ones_bf[:, 0:1], start=(c == 0 and b == 0), stop=(c == 3 and b == 3))
+            nc.scalar.activation(out=junk_s[:, 0:512], in_=w_sb[:, 2 * c, :], func=ACT.Square, accum_out=st[:, 10 + c, 2:3])
+            nc.vector.bn_stats(out=stf[:, 6 * c : 6 * c + 6], in_=w_sb[:, 2 * c + 1, :])
+            if c < 2:
+                w_transposes(c)
+        nc.scalar.activation(out=st[:, 8, 1:2], in_=colsum[:], func=ACT.Identity, scale=1.0 / 256)
+        nc.scalar.activation(out=junk_s[:, 0:8], in_=st[:, 0:8, 1], func=ACT.Square, scale=16.0, accum_out=st[:, 9, 2:3])
+        w_transposes(2)
+        cs = psum.tile([P, 42], F32, name="cs", tag="b5")
+        nc.tensor.matmul(out=cs[:, 0:27], lhsT=ones_f[:], rhs=stf[:, 0:27], start=True, stop=True)
+        nc.tensor.matmul(out=cs[:, 27:42], lhsT=ones_f[:], rhs=stf[:, 27:42], start=True, stop=True)
+        w_transposes(3)
 
         def evac(c, copy):
             copy(out=wT32[:, 256 * c : 256 * c + 256, :].rearrange("p (r j) u -> p r j u", j=2), in_=pw[c][:].rearrange("p j u r -> p r j u"))
-
-        def sign(c):
-            nc.vector.tensor_scalar(out=ws[:, cols(c)], in0=wTf[:, cols(c)], scalar1=-TINY, scalar2=TINY, op0=ALU.max, op1=ALU.min)
 
         def square(c, n=1024):
             nc.scalar.activation(out=q[:, cols(c, n)], in_=wTf[:, cols(c, n)], func=ACT.Square, bias=nbt[:], scale=SC)
 
         def mask(c, n=1024):
-            nc.vector.tensor_scalar(out=kk[:, cols(c, n)], in0=q[:, cols(c, n)], scalar1=thr[:], scalar2=HUGE, op0=ALU.is_le, op1=ALU.mult)
+            nc.vector.tensor_scalar(out=kk[:, cols(c, n)], in0=q[:, cols(c, n)], scalar1=thr[:], scalar2=BIG, op0=ALU.is_le, op1=ALU.mult)
 
-        def masked_sign(c):
-            nc.vector.tensor_tensor(out=bm[:, cols(c)], in0=ws[:, cols(c)], in1=kk[:, cols(c)], op=ALU.mult)
+        def kept(c, n=1024):
+            nc.vector.tensor_tensor(out=kw[:, cols(c, n)], in0=wTf[:, cols(c, n)], in1=kk[:, cols(c, n)], op=ALU.mult)
 
-        def outlier_mask_v(s):
-            nc.vector.tensor_scalar(out=oo[:, s], in0=kk[:, s], scalar1=-TINY, scalar2=1.0, op0=ALU.mult, op1=ALU.add)
-
-        def outlier_mask_s(s):
-            nc.scalar.activation(out=oo[:, s], in_=kk[:, s], func=ACT.Identity, scale=-TINY, bias=1.0)
+        def kept_sign(c, n=1024):
+            nc.vector.tensor_scalar(out=bm[:, cols(c, n)], in0=kw[:, cols(c, n)], scalar1=-SMALL, scalar2=SMALL, op0=ALU.max, op1=ALU.min)
 
         def outliers(s):
             nc.vector.tensor_tensor(out=aa[:, s], in0=wTf[:, s], in1=oo[:, s], op=ALU.mult)
 
         gram = psum.tile([P, P], F32, name="gram", tag="b6")
-        ck = psum.tile([P, 1], F32, name="ck", tag="b7")
 
-        def keep_sums(c):
+        def counts(c):
             for b in range(8 * c, 8 * c + 8):
-                nc.tensor.matmul(out=gram[:], lhsT=wTf[:, cols(b, P)], rhs=bm[:, cols(b, P)], start=(b == 0), stop=(b == 31))
-                nc.tensor.matmul(out=ck[:], lhsT=kk[:, cols(b, P)], rhs=tinycol[:, 0:1], start=(b == 0), stop=(b == 31))
+                nc.tensor.matmul(out=ck[:], lhsT=kk[:, cols(b, P)], rhs=smallcol[:, 0:1], start=(b == 0), stop=(b == 31))
+
+        def kept_trace(c):
+            for b in range(8 * c, 8 * c + 8):
+                nc.tensor.matmul(out=gram[:], lhsT=wTf[:, cols(b, P)], rhs=bm[:, cols(b, P)], start=(b == 8), stop=(b == 31))
 
         def transposes(g, bank):
             pts = []
@@ -180,86 +177,109 @@ def tile_binaryxnorexceptoutlierslinear_t_kernel(tc, x, weight, bias, out):
         def x_quant(g, xg):
             nc.vector.quantize_mx(out=x_codes[:, g, :].bitcast(FP8X4), scales=x_scales[:, g, :], in_=xg[:].rearrange("p t r v -> p (t r v)"))
 
-        vcopy, scopy = nc.vector.tensor_copy, nc.scalar.copy
-        evac(0, vcopy)
-        evac(1, scopy)
-        nc.vector.tensor_scalar(out=nbt[:], in0=cs[:, 0:1], scalar1=-SC * half / NW, scalar2=nbs[:], op0=ALU.mult, op1=ALU.add)
-        nc.vector.reduce_sum(out=s4[:], in_=cs[:, 2:6], axis=mybir.AxisListType.X)
-        nc.vector.tensor_scalar(out=sm2[:], in0=nbt[:], scalar1=nbt[:], scalar2=-NW / (SC * SC), op0=ALU.mult, op1=ALU.mult)
-        nc.vector.tensor_scalar(out=ssq[:], in0=cs[:, 6:7], scalar1=float(half), scalar2=s4[:], op0=ALU.mult, op1=ALU.add)
-        sign(0)
-        nc.vector.tensor_scalar(out=thr[:], in0=ssq[:], scalar1=sm2[:], scalar2=None, op0=ALU.add)
-        square(0, 512)
-        square(1, 512)
-        mask(0, 512)
-        mask(1, 512)
-        sign(1)
-        square(1)
-        evac(2, scopy)
-        masked_sign(0)
-        keep_sums(0)
-        pt0 = transposes(0, 0)
-        mask(1)
-        square(2)
-        evac(3, scopy)
-        sign(2)
-        masked_sign(1)
-        zero_products(2, 2)
-        keep_sums(1)
-        pt1 = transposes(1, 4)
-        mask(2)
-        square(3)
-        sign(3)
-        masked_sign(2)
-        zero_products(2, 2)
-        keep_sums(2)
-        xg0 = x_copies(pt0)
-        outlier_mask_v(cols(2))
-        mask(3)
-        outliers(cols(2))
-        masked_sign(3)
-        zero_products(2, 2)
-        keep_sums(3)
-        outlier_mask_s(cols(1))
-        outlier_mask_s(cols(0))
-        xg1 = x_copies(pt1)
-        outlier_mask_v(cols(3))
-
         wacc = {}
 
-        def add_outliers(b, bank):
+        def all_pass(b, bank):
             wacc[b] = psum.tile([P, 512], BF16, name="wacc", tag="b%d" % bank)
-            nc.tensor.matmul(out=wacc[b][:], lhsT=ident_bf[:], rhs=aa[:, cols(b, 512)], start=True, stop=False)
+            nc.tensor.matmul(out=wacc[b][:], lhsT=ident_bf[:], rhs=wTf[:, cols(b, 512)], start=True, stop=False)
 
-        x_quant(0, xg0)
-        outliers(cols(3))
-        add_outliers(4, 2)
-        add_outliers(5, 3)
-        nc.vector.tensor_copy(out=st2[:, 1:2], in_=ck[:])
-        nc.vector.scalar_tensor_tensor(out=junk_d[:], in0=gram[:], scalar=1.0, in1=ident[:], op0=ALU.mult, op1=ALU.mult, accum_out=st2[:, 0:1])
-        l2b = psum.tile([P, 2], F32, name="l2b", tag="b7")
-        nc.tensor.matmul(out=l2b[:], lhsT=ones_f[:], rhs=st2[:], start=True, stop=True)
-        add_outliers(6, 0)
-        add_outliers(7, 1)
-        outliers(cols(1))
-        add_outliers(3, 6)
-        add_outliers(2, 4)
-        nc.vector.reciprocal(out=rc[:], in_=l2b[:, 1:2])
-        outliers(cols(0, 512))
-        nc.vector.tensor_scalar(out=c_ident[:], in0=ident_bf[:], scalar1=l2b[:, 0:1], scalar2=rc[:], op0=ALU.mult, op1=ALU.mult)
-        for b in range(2, 8):
+        def kept_pass(b):
+            nc.tensor.matmul(out=wacc[b][:], lhsT=minus_ident[:], rhs=kw[:, cols(b, 512)], start=False, stop=False)
+
+        def sign_pass(b):
             nc.tensor.matmul(out=wacc[b][:], lhsT=c_ident[:], rhs=bm[:, cols(b, 512)], start=False, stop=True)
+
+        vcopy, scopy = nc.vector.tensor_copy, nc.scalar.copy
+        evac(0, vcopy)
+        evac(1, vcopy)
+        evac(2, vcopy)
+        nc.scalar.activation(out=junk_m[:], in_=cs[:, 1:27:3], func=ACT.Identity, scale=-SC * 256 / NW, accum_out=nbt[:])
+        nc.vector.tensor_scalar(out=sm2[:], in0=nbt[:], scalar1=nbt[:], scalar2=-NW / (SC * SC), op0=ALU.mult, op1=ALU.mult)
+        nc.vector.tensor_scalar(out=minus_ident[:], in0=ident_bf[:], scalar1=-SMALL, scalar2=None, op0=ALU.mult)
+        nc.vector.tensor_scalar(out=junk_t[:], in0=cs[:, 2:42:3], scalar1=1.0, scalar2=sm2[:], op0=ALU.mult, op1=ALU.add, accum_out=thr[:])
+        square(0, 512)
+        square(1, 512)
+        zero_products(4)
+        pt0 = transposes(0, 0)
+        zero_products(2)
+        pt1 = transposes(1, 4)
+        mask(0, 512)
+        mask(1, 512)
+        kept(0, 512)
+        kept(1, 512)
+        square(1)
+        mask(1)
+        kept_sign(0)
+        ck = psum.tile([P, 1], F32, name="ck", tag="b7")
+        counts(0)
+        square(2)
+        evac(3, scopy)
+        all_pass(5, 2)
+        counts(1)
+        kept(1)
+        mask(2)
+        kept_sign(1)
+        kept_trace(1)
+        counts(2)
+        square(3)
+        all_pass(6, 3)
+        xg0 = x_copies(pt0)
+        kept(2)
+        mask(3)
+        kept_sign(2)
+        kept_trace(2)
+        counts(3)
+        all_pass(2, 0)
+        kept_pass(2)
+        kept_pass(5)
+        nc.scalar.activation(out=oo[:], in_=kk[:, 0:DIRECT], func=ACT.Identity, scale=-SMALL, bias=1.0)
+        nc.scalar.activation(out=junk_s[:], in_=kw[:, cols(0)], func=ACT.Abs, accum_out=abs0[:])
+        xg1 = x_copies(pt1)
+        kept(6, 512)
+        kept(7, 512)
+        kept_sign(6, 512)
+        nc.vector.tensor_copy(out=st2[:, 1:2], in_=ck[:])
+        kept_sign(7, 512)
+        l2b = psum.tile([P, 2], F32, name="l2b", tag="b7")
+        nc.tensor.matmul(out=l2b[:, 1:2], lhsT=ones_f[:], rhs=st2[:, 1:2], start=True, stop=True)
+        kept_trace(3)
+        kept_pass(6)
+        x_quant(0, xg0)
+        nc.vector.reciprocal(out=rc[:], in_=l2b[:, 1:2])
+        outliers(slice(0, 512))
+        nc.vector.scalar_tensor_tensor(out=junk_d[:], in0=gram[:], scalar=BIG * BIG, in1=ident[:], op0=ALU.mult, op1=ALU.mult, accum_out=st2[:, 0:1])
+        nc.tensor.matmul(out=l2b[:, 0:1], lhsT=ones_f[:], rhs=abs0[:], start=True, stop=False)
+        nc.tensor.matmul(out=l2b[:, 0:1], lhsT=ones_f[:], rhs=st2[:, 0:1], start=False, stop=True)
+        all_pass(3, 4)
+        kept_pass(3)
+        outliers(slice(512, 1024))
+        nc.vector.tensor_scalar(out=c_ident[:], in0=ident_bf[:], scalar1=l2b[:, 0:1], scalar2=rc[:], op0=ALU.mult, op1=ALU.mult)
+        sign_pass(2)
+        sign_pass(3)
+        all_pass(4, 5)
+        kept_pass(4)
+        for b in range(4, 7):
+            sign_pass(b)
+        all_pass(7, 6)
+        kept_pass(7)
+        sign_pass(7)
         for b in range(2, 8):
             nc.scalar.copy(out=wsim[:, cols(b, 512)], in_=wacc[b][:])
-        nc.vector.tensor_scalar(out=cb[:, 0:DIRECT], in0=bm[:, 0:DIRECT], scalar1=l2b[:, 0:1], scalar2=rc[:], op0=ALU.mult, op1=ALU.mult)
-        outliers(cols(1, 512))
-        nc.vector.tensor_tensor(out=wsim[:, 0:DIRECT], in0=cb[:, 0:DIRECT], in1=aa[:, 0:DIRECT], op=ALU.add)
-        for n0 in (256, 0, 512, 768):
-            nc.vector.quantize_mx(out=w_codes[:, n0 : n0 + 256].bitcast(FP8X4), scales=w_scales[:, n0 : n0 + 256], in_=wsim[:, 4 * n0 : 4 * n0 + 1024])
+        nc.vector.tensor_scalar(out=cb[:], in0=bm[:, 0:DIRECT], scalar1=l2b[:, 0:1], scalar2=rc[:], op0=ALU.mult, op1=ALU.mult)
+        for s in (slice(0, 512), slice(512, 1024)):
+            nc.vector.tensor_tensor(out=wsim[:, s], in0=cb[:, s], in1=aa[:, s], op=ALU.add)
+
+        def w_quant(n0, n=256):
+            nc.vector.quantize_mx(out=w_codes[:, n0 : n0 + n].bitcast(FP8X4), scales=w_scales[:, n0 : n0 + n], in_=wsim[:, 4 * n0 : 4 * (n0 + n)])
+
+        w_quant(0, 128)
+        w_quant(128, 128)
+        w_quant(256)
+        w_quant(512)
 
         def product(g, i, t, h):
             hs = cols(h, 512)
-            bank = (6, 7, 2, 3, 0, 1, 4, 5)[i] if g == 0 else 2 + (8 * (g - 1) + i) % 6
+            bank = (7, 4, 5, 2, 3, 6)[(8 * g + i) % 6]
             acc = psum.tile([P, 512], F32, name="acc", tag="b%d" % bank)
             nc.tensor.matmul_mx(
                 out=acc[:],
@@ -278,11 +298,37 @@ def tile_binaryxnorexceptoutlierslinear_t_kernel(tc, x, weight, bias, out):
 
         ramp = (((2, 0), True), ((0, 0), False), ((3, 0), True), ((0, 1), False), ((1, 0), False), ((3, 1), True), ((1, 1), False), ((2, 1), False))
         steady = (((2, 0), True), ((0, 0), False), ((0, 1), False), ((3, 0), True), ((1, 0), False), ((1, 1), False), ((2, 1), False), ((3, 1), False))
-        ndma = {0: 1, 1: 1, 7: 1}
-        xg = None
-        for g in range(GROUPS):
+        ndma = {1: 1, 7: 1}
+
+        def group_tiles(g):
             o = opool.tile([P, 4, NOUT], F32, name="o_sb")
-            dst = of[512 * g : 512 * g + 512, :].rearrange("(p t) n -> p t n", t=4)
+            return o, of[512 * g : 512 * g + 512, :].rearrange("(p t) n -> p t n", t=4)
+
+        o, dst = group_tiles(0)
+
+        def store_half(t, h):
+            nc.sync.dma_start(out=dst[:, t, cols(h, 512)], in_=o[:, t, cols(h, 512)])
+
+        late = None
+        for i, ((t, h), by_scalar) in enumerate((((0, 0), False), ((1, 0), True), ((2, 0), False), ((3, 0), False), ((0, 1), False), ((1, 1), True), ((2, 1), False), ((3, 1), True))):
+            finish(o, t, h, product(0, i, t, h), by_scalar)
+            if i == 0:
+                w_quant(768)
+            if i == 3:
+                pts = transposes(2, 0)
+            if i == 6:
+                xg = x_copies(pts)
+            if i == 4:
+                x_quant(1, xg1)
+            if by_scalar:
+                late = (t, h)
+            else:
+                store_half(t, h)
+            if i in (3, 6, 7):
+                store_half(*late)
+
+        for g in range(1, GROUPS):
+            o, dst = group_tiles(g)
             n = ndma.get(g, 2)
             pts = None
             if 1 < g < GROUPS - 1:
@@ -294,14 +340,10 @@ def tile_binaryxnorexceptoutlierslinear_t_kernel(tc, x, weight, bias, out):
                 done.append(t)
                 if i == 4 and g == 1:
                     x_quant(2, xg)
-                if i == 3 and 0 < g < GROUPS - 2:
+                if i == 3 and g < GROUPS - 2:
                     pts = transposes(g + 2, 0)
                 if i == 6 and pts is not None:
                     xg = x_copies(pts)
                 while stored < 4 and all(done.count(r) == 2 for r in range(stored, stored + n)):
                     nc.sync.dma_start(out=dst[:, stored : stored + n, :], in_=o[:, stored : stored + n, :])
                     stored += n
-                if g == 0 and (t, h) == (1, 1):
-                    x_quant(1, xg1)
-            if g == 0:
-                xg = x_copies(transposes(2, 0))

from contextlib import ExitStack
import math

import concourse.masks as masks
import concourse.mybir as mybir

F32 = mybir.dt.float32
BF16 = mybir.dt.bfloat16
U32 = mybir.dt.uint32
U8 = mybir.dt.uint8
FP8X4 = mybir.dt.float8_e4m3fn_x4
ALU = mybir.AluOpType
ACT = mybir.ActivationFunctionType

P = 128
TOK = 4096
K = 512
NOUT = 1024
NW = NOUT * K
FLOPS = 2 * TOK * NOUT * K
GROUPS = 8
SC = math.sqrt((NW - 1) / (1.6 * 1.6))
DIRECT = 1024
BIG = 2.0 ** 63
SMALL = 2.0 ** -63


def tile_binaryxnorexceptoutlierslinear_t_kernel(tc, x, weight, bias, out):
    nc = tc.nc
    xf = x.flatten_outer_dims()
    of = out.flatten_outer_dims()
    with ExitStack() as ctx:
        ctx.enter_context(tc.manual_schedule())
        keep = ctx.enter_context(tc.tile_pool(name="keep", bufs=1))
        xgpool = ctx.enter_context(tc.tile_pool(name="xgp", bufs=2))
        opool = ctx.enter_context(tc.tile_pool(name="op", bufs=3))
        psum = ctx.enter_context(tc.psum_pool(name="psum", bufs=1))

        ones_bf = keep.tile([P, P], BF16, name="ones_bf")
        ones_f = keep.tile([P, P], F32, name="ones_f")
        smallcol = keep.tile([P, 2], BF16, name="smallcol")
        ident = keep.tile([P, P], F32, name="ident")
        ident_bf = keep.tile([P, P], BF16, name="ident_bf")
        minus_ident = keep.tile([P, P], BF16, name="minus_ident")
        c_ident = keep.tile([P, P], BF16, name="c_ident")
        w_sb = keep.tile([P, 8, K], BF16, name="w_sb")
        x_sb = keep.tile([P, GROUPS, 4, K], BF16, name="x_sb")
        bias_bc = keep.tile([P, NOUT], BF16, name="bias_bc")
        x_codes = keep.tile([P, GROUPS, 512], U32, name="x_codes", align_bytes=64)
        x_scales = keep.tile([P, GROUPS, 512], U8, name="x_scales", align_bytes=64)
        w_codes = keep.tile([P, NOUT], U32, name="w_codes", align_bytes=64)
        w_scales = keep.tile([P, NOUT], U8, name="w_scales", align_bytes=64)
        zero = keep.tile([P, 1024], BF16, name="zero", align_bytes=64)
        z_codes = keep.tile([P, 256], U32, name="z_codes", align_bytes=64)
        z_scales = keep.tile([P, 256], U8, name="z_scales", align_bytes=64)
        wT = keep.tile([P, NOUT, 4], BF16, name="wT")
        wT32 = wT[:].bitcast(F32)
        wTf = wT[:].rearrange("p n v -> p (n v)")
        q = keep.tile([P, 4 * NOUT], F32, name="q")
        kk = keep.tile([P, 4 * NOUT], BF16, name="kk")
        kw = keep.tile([P, 4 * NOUT], BF16, name="kw")
        bm = keep.tile([P, 4 * NOUT], BF16, name="bm")
        oo = keep.tile([P, DIRECT], BF16, name="oo")
        aa = keep.tile([P, DIRECT], BF16, name="aa")
        cb = keep.tile([P, DIRECT], BF16, name="cb")
        wsim = keep.tile([P, 4 * NOUT], BF16, name="wsim", align_bytes=64)
        junk_s = keep.tile([P, 1024], BF16, name="junk_s")
        junk_d = keep.tile([P, P], F32, name="junk_d")
        st = keep.tile([P, 14, 3], F32, name="st")
        stf = st[:].rearrange("p r s -> p (r s)")
        junk_t = keep.tile([P, 14], F32, name="junk_t")
        junk_m = keep.tile([P, 9], F32, name="junk_m")
        st2 = keep.tile([P, 2], F32, name="st2")
        abs0 = keep.tile([P, 1], F32, name="abs0")
        nbt = keep.tile([P, 1], F32, name="nbt")
        sm2 = keep.tile([P, 1], F32, name="sm2")
        thr = keep.tile([P, 1], F32, name="thr")
        rc = keep.tile([P, 1], F32, name="rc")

        def cols(c, n=1024):
            return slice(n * c, n * c + n)

        nc.vector.memset(smallcol[:], SMALL)
        nc.scalar.activation(out=junk_s[:, 0:2], in_=smallcol[:], func=ACT.Square)
        nc.vector.memset(zero[:].bitcast(U32), 0)
        nc.vector.memset(ones_bf[:], 1.0)
        nc.vector.memset(ones_f[:], 1.0)
        nc.vector.memset(st[:], 0.0)
        masks.make_identity(nc, ident[:])
        masks.make_identity(nc, ident_bf[:])

        nc.vector.quantize_mx(out=z_codes[:].bitcast(FP8X4), scales=z_scales[:], in_=zero[:])

        def zero_products(n):
            z = psum.tile([P, 256], F32, name="z", tag="b7")
            for i in range(n):
                nc.tensor.matmul_mx(out=z[:], lhsT=z_codes[:, 0:P].bitcast(FP8X4), lhsT_scale=z_scales[:, 0:P], rhs=z_codes[:].bitcast(FP8X4), rhs_scale=z_scales[:], start=True, stop=True)

        zero_products(5)

        for c in range(4):
            nc.sync.dma_start(out=w_sb[:, 2 * c : 2 * c + 2, :], in_=weight[256 * c : 256 * c + 256, :].rearrange("(p j) k -> p j k", j=2))
        for g in range(GROUPS):
            nc.sync.dma_start(out=x_sb[:, g, :, :], in_=xf[512 * g : 512 * g + 512, :].rearrange("(p t) k -> p t k", t=4))
            if g == 1:
                nc.sync.dma_start(out=bias_bc[:], in_=bias.partition_broadcast(P))

        colsum = psum.tile([P, 1], F32, name="colsum", tag="b4")
        pw = []
        for c in range(4):
            pw.append(psum.tile([P, 2, 2, P], F32, name="pw", tag="b%d" % c))

        def w_transposes(c):
            for jj in range(2):
                for u in range(2):
                    nc.tensor.transpose(out=pw[c][:, jj, u, :], in_=w_sb[:, 2 * c + jj, :].bitcast(F32)[:, u : 2 * P : 2], identity=ident[:])

        for c in range(4):
            for b in range(4):
                nc.tensor.matmul(out=colsum[:], lhsT=w_sb[:, 2 * c, cols(b, P)], rhs=ones_bf[:, 0:1], start=(c == 0 and b == 0), stop=(c == 3 and b == 3))
            nc.scalar.activation(out=junk_s[:, 0:512], in_=w_sb[:, 2 * c, :], func=ACT.Square, accum_out=st[:, 10 + c, 2:3])
            nc.vector.bn_stats(out=stf[:, 6 * c : 6 * c + 6], in_=w_sb[:, 2 * c + 1, :])
            if c < 2:
                w_transposes(c)
        nc.scalar.activation(out=st[:, 8, 1:2], in_=colsum[:], func=ACT.Identity, scale=1.0 / 256)
        nc.scalar.activation(out=junk_s[:, 0:8], in_=st[:, 0:8, 1], func=ACT.Square, scale=16.0, accum_out=st[:, 9, 2:3])
        w_transposes(2)
        cs = psum.tile([P, 42], F32, name="cs", tag="b5")
        nc.tensor.matmul(out=cs[:, 0:27], lhsT=ones_f[:], rhs=stf[:, 0:27], start=True, stop=True)
        nc.tensor.matmul(out=cs[:, 27:42], lhsT=ones_f[:], rhs=stf[:, 27:42], start=True, stop=True)
        w_transposes(3)

        def evac(c, copy):
            copy(out=wT32[:, 256 * c : 256 * c + 256, :].rearrange("p (r j) u -> p r j u", j=2), in_=pw[c][:].rearrange("p j u r -> p r j u"))

        def square(c, n=1024):
            nc.scalar.activation(out=q[:, cols(c, n)], in_=wTf[:, cols(c, n)], func=ACT.Square, bias=nbt[:], scale=SC)

        def mask(c, n=1024):
            nc.vector.tensor_scalar(out=kk[:, cols(c, n)], in0=q[:, cols(c, n)], scalar1=thr[:], scalar2=BIG, op0=ALU.is_le, op1=ALU.mult)

        def kept(c, n=1024):
            nc.vector.tensor_tensor(out=kw[:, cols(c, n)], in0=wTf[:, cols(c, n)], in1=kk[:, cols(c, n)], op=ALU.mult)

        def kept_sign(c, n=1024):
            nc.vector.tensor_scalar(out=bm[:, cols(c, n)], in0=kw[:, cols(c, n)], scalar1=-SMALL, scalar2=SMALL, op0=ALU.max, op1=ALU.min)

        def outliers(s):
            nc.vector.tensor_tensor(out=aa[:, s], in0=wTf[:, s], in1=oo[:, s], op=ALU.mult)

        gram = psum.tile([P, P], F32, name="gram", tag="b6")

        def counts(c):
            for b in range(8 * c, 8 * c + 8):
                nc.tensor.matmul(out=ck[:], lhsT=kk[:, cols(b, P)], rhs=smallcol[:, 0:1], start=(b == 0), stop=(b == 31))

        def kept_trace(c):
            for b in range(8 * c, 8 * c + 8):
                nc.tensor.matmul(out=gram[:], lhsT=wTf[:, cols(b, P)], rhs=bm[:, cols(b, P)], start=(b == 8), stop=(b == 31))

        def transposes(g, bank):
            pts = []
            for b in range(2):
                pt = psum.tile([P, 2, 2, P], F32, name="pt", tag="b%d" % (bank + b))
                for tt in range(2):
                    for u in range(2):
                        nc.tensor.transpose(out=pt[:, tt, u, :], in_=x_sb[:, g, 2 * b + tt, :].bitcast(F32)[:, u : 2 * P : 2], identity=ident[:])
                pts.append(pt)
            return pts

        def x_copies(pts):
            xg = xgpool.tile([P, 4, P, 4], BF16, name="xg", align_bytes=64)
            for b in range(2):
                nc.scalar.copy(out=xg[:].bitcast(F32)[:, 2 * b : 2 * b + 2, :, :], in_=pts[b][:].rearrange("p t u r -> p t r u"))
            return xg

        def x_quant(g, xg):
            nc.vector.quantize_mx(out=x_codes[:, g, :].bitcast(FP8X4), scales=x_scales[:, g, :], in_=xg[:].rearrange("p t r v -> p (t r v)"))

        wacc = {}

        def all_pass(b, bank):
            wacc[b] = psum.tile([P, 512], BF16, name="wacc", tag="b%d" % bank)
            nc.tensor.matmul(out=wacc[b][:], lhsT=ident_bf[:], rhs=wTf[:, cols(b, 512)], start=True, stop=False)

        def kept_pass(b):
            nc.tensor.matmul(out=wacc[b][:], lhsT=minus_ident[:], rhs=kw[:, cols(b, 512)], start=False, stop=False)

        def sign_pass(b):
            nc.tensor.matmul(out=wacc[b][:], lhsT=c_ident[:], rhs=bm[:, cols(b, 512)], start=False, stop=True)

        vcopy, scopy = nc.vector.tensor_copy, nc.scalar.copy
        evac(0, vcopy)
        evac(1, vcopy)
        evac(2, vcopy)
        nc.scalar.activation(out=junk_m[:], in_=cs[:, 1:27:3], func=ACT.Identity, scale=-SC * 256 / NW, accum_out=nbt[:])
        nc.vector.tensor_scalar(out=sm2[:], in0=nbt[:], scalar1=nbt[:], scalar2=-NW / (SC * SC), op0=ALU.mult, op1=ALU.mult)
        nc.vector.tensor_scalar(out=minus_ident[:], in0=ident_bf[:], scalar1=-SMALL, scalar2=None, op0=ALU.mult)
        nc.vector.tensor_scalar(out=junk_t[:], in0=cs[:, 2:42:3], scalar1=1.0, scalar2=sm2[:], op0=ALU.mult, op1=ALU.add, accum_out=thr[:])
        square(0, 512)
        square(1, 512)
        zero_products(4)
        pt0 = transposes(0, 0)
        zero_products(2)
        pt1 = transposes(1, 4)
        mask(0, 512)
        mask(1, 512)
        kept(0, 512)
        kept(1, 512)
        square(1)
        mask(1)
        kept_sign(0)
        ck = psum.tile([P, 1], F32, name="ck", tag="b7")
        counts(0)
        square(2)
        evac(3, scopy)
        all_pass(5, 2)
        counts(1)
        kept(1)
        mask(2)
        kept_sign(1)
        kept_trace(1)
        counts(2)
        square(3)
        all_pass(6, 3)
        xg0 = x_copies(pt0)
        kept(2)
        mask(3)
        kept_sign(2)
        kept_trace(2)
        counts(3)
        all_pass(2, 0)
        kept_pass(2)
        kept_pass(5)
        nc.scalar.activation(out=oo[:], in_=kk[:, 0:DIRECT], func=ACT.Identity, scale=-SMALL, bias=1.0)
        nc.scalar.activation(out=junk_s[:], in_=kw[:, cols(0)], func=ACT.Abs, accum_out=abs0[:])
        xg1 = x_copies(pt1)
        kept(6, 512)
        kept(7, 512)
        kept_sign(6, 512)
        nc.vector.tensor_copy(out=st2[:, 1:2], in_=ck[:])
        kept_sign(7, 512)
        l2b = psum.tile([P, 2], F32, name="l2b", tag="b7")
        nc.tensor.matmul(out=l2b[:, 1:2], lhsT=ones_f[:], rhs=st2[:, 1:2], start=True, stop=True)
        kept_trace(3)
        kept_pass(6)
        x_quant(0, xg0)
        nc.vector.reciprocal(out=rc[:], in_=l2b[:, 1:2])
        outliers(slice(0, 512))
        nc.vector.scalar_tensor_tensor(out=junk_d[:], in0=gram[:], scalar=BIG * BIG, in1=ident[:], op0=ALU.mult, op1=ALU.mult, accum_out=st2[:, 0:1])
        nc.tensor.matmul(out=l2b[:, 0:1], lhsT=ones_f[:], rhs=abs0[:], start=True, stop=False)
        nc.tensor.matmul(out=l2b[:, 0:1], lhsT=ones_f[:], rhs=st2[:, 0:1], start=False, stop=True)
        all_pass(3, 4)
        kept_pass(3)
        outliers(slice(512, 1024))
        nc.vector.tensor_scalar(out=c_ident[:], in0=ident_bf[:], scalar1=l2b[:, 0:1], scalar2=rc[:], op0=ALU.mult, op1=ALU.mult)
        sign_pass(2)
        sign_pass(3)
        all_pass(4, 5)
        kept_pass(4)
        for b in range(4, 7):
            sign_pass(b)
        all_pass(7, 6)
        kept_pass(7)
        sign_pass(7)
        for b in range(2, 8):
            nc.scalar.copy(out=wsim[:, cols(b, 512)], in_=wacc[b][:])
        nc.vector.tensor_scalar(out=cb[:], in0=bm[:, 0:DIRECT], scalar1=l2b[:, 0:1], scalar2=rc[:], op0=ALU.mult, op1=ALU.mult)
        for s in (slice(0, 512), slice(512, 1024)):
            nc.vector.tensor_tensor(out=wsim[:, s], in0=cb[:, s], in1=aa[:, s], op=ALU.add)

        def w_quant(n0, n=256):
            nc.vector.quantize_mx(out=w_codes[:, n0 : n0 + n].bitcast(FP8X4), scales=w_scales[:, n0 : n0 + n], in_=wsim[:, 4 * n0 : 4 * (n0 + n)])

        w_quant(0, 128)
        w_quant(128, 128)
        w_quant(256)
        w_quant(512)

        def product(g, i, t, h):
            hs = cols(h, 512)
            bank = (7, 4, 5, 2, 3, 6)[(8 * g + i) % 6]
            acc = psum.tile([P, 512], F32, name="acc", tag="b%d" % bank)
            nc.tensor.matmul_mx(
                out=acc[:],
                lhsT=x_codes[:, g, cols(t, P)].bitcast(FP8X4), lhsT_scale=x_scales[:, g, cols(t, P)],
                rhs=w_codes[:, hs].bitcast(FP8X4), rhs_scale=w_scales[:, hs],
                start=True, stop=True)
            return acc

        def finish(o, t, h, acc, by_scalar):
            hs = cols(h, 512)
            if by_scalar:
                nc.scalar.copy(out=o[:, t, hs], in_=acc[:])
                nc.gpsimd.tensor_tensor(out=o[:, t, hs], in0=o[:, t, hs], in1=bias_bc[:, hs], op=ALU.add)
            else:
                nc.vector.tensor_tensor(out=o[:, t, hs], in0=acc[:], in1=bias_bc[:, hs], op=ALU.add)

        ramp = (((2, 0), True), ((0, 0), False), ((3, 0), True), ((0, 1), False), ((1, 0), False), ((3, 1), True), ((1, 1), False), ((2, 1), False))
        steady = (((2, 0), True), ((0, 0), False), ((0, 1), False), ((3, 0), True), ((1, 0), False), ((1, 1), False), ((2, 1), False), ((3, 1), False))
        ndma = {1: 1, 7: 1}

        def group_tiles(g):
            o = opool.tile([P, 4, NOUT], F32, name="o_sb")
            return o, of[512 * g : 512 * g + 512, :].rearrange("(p t) n -> p t n", t=4)

        o, dst = group_tiles(0)

        def store_half(t, h):
            nc.sync.dma_start(out=dst[:, t, cols(h, 512)], in_=o[:, t, cols(h, 512)])

        late = None
        for i, ((t, h), by_scalar) in enumerate((((0, 0), False), ((1, 0), True), ((2, 0), False), ((3, 0), False), ((0, 1), False), ((1, 1), True), ((2, 1), False), ((3, 1), True))):
            finish(o, t, h, product(0, i, t, h), by_scalar)
            if i == 0:
                w_quant(768)
            if i == 3:
                pts = transposes(2, 0)
            if i == 6:
                xg = x_copies(pts)
            if i == 4:
                x_quant(1, xg1)
            if by_scalar:
                late = (t, h)
            else:
                store_half(t, h)
            if i in (3, 6, 7):
                store_half(*late)

        for g in range(1, GROUPS):
            o, dst = group_tiles(g)
            n = ndma.get(g, 2)
            pts = None
            if 1 < g < GROUPS - 1:
                x_quant(g + 1, xg)
            done = []
            stored = 0
            for i, ((t, h), by_scalar) in enumerate(steady if g in (2, 4, 6) else ramp):
                finish(o, t, h, product(g, i, t, h), by_scalar)
                done.append(t)
                if i == 4 and g == 1:
                    x_quant(2, xg)
                if i == 3 and g < GROUPS - 2:
                    pts = transposes(g + 2, 0)
                if i == 6 and pts is not None:
                    xg = x_copies(pts)
                while stored < 4 and all(done.count(r) == 2 for r in range(stored, stored + n)):
                    nc.sync.dma_start(out=dst[:, stored : stored + n, :], in_=o[:, stored : stored + n, :])
                    stored += n
